import numpy as np
import ml_dtypes


def mxq(x, axis, fmt="e4m3"):
    dtype, down = {"e4m3": (ml_dtypes.float8_e4m3fn, 7), "e5m2": (ml_dtypes.float8_e5m2, 14)}[fmt]
    v = np.moveaxis(np.asarray(x, np.float32).astype(ml_dtypes.bfloat16).astype(np.float64), axis, -1)
    blocks = v.reshape(v.shape[:-1] + (-1, 32))
    amax = np.abs(blocks).max(-1, keepdims=True)
    byte = np.maximum(np.where(amax > 0, np.frexp(amax)[1] - 1 + 127, 0) - down, 1)
    scale = np.exp2(byte - 127.0)
    codes = (blocks / scale).astype(np.float32).astype(dtype).astype(np.float64)
    return np.moveaxis((codes * scale).reshape(v.shape), -1, axis)


WIDE = False


def mx_kscale(k):
    if not WIDE:
        return np.ones(k)
    levels = np.array([10, -10, 5, -5, 0])
    a = np.random.permutation(np.resize(levels, k // 512 * 4)).reshape(k // 512, 4)
    idx = np.arange(k)
    return np.exp2(a[idx // 512, idx % 128 // 32])


BF16 = ml_dtypes.bfloat16


def bf(x):
    return np.asarray(x, np.float32).astype(BF16)


def f64(x):
    return np.asarray(x).astype(np.float64)


N, DI, DO, M = 16, 512, 128, 8
NB = 19


def mix(cb, tq):
    rest = tq.shape[2:]
    y = cb.T @ np.moveaxis(tq, 1, 0).reshape(DI, -1)
    return np.moveaxis(y.reshape((DO, N) + rest), 0, 1)


def setup_inputs():
    s = mx_kscale(DI)
    g = np.concatenate([np.ones(1), np.full(9, 1.0 / np.sqrt(M)), np.full(9, 1.0 / M)])
    return {"x": bf(np.random.standard_normal((N, DI, M, M, M)) * s[None, :, None, None, None]),
            "coefs": bf(np.random.standard_normal((DI, DO, NB)) * (0.5 / np.sqrt(DI)) * g / s[:, None, None]),
            "bias": bf(np.random.standard_normal((1, DO, 1, 1, 1)) * 0.5)}


def reference(x, coefs, bias):
    x = f64(x)
    cq = mxq(f64(coefs), 0, "e4m3")
    out = mix(cq[:, :, 0], mxq(x, 1, "e4m3"))
    b = 1
    for ax in (2, 3, 4):
        mq = mxq(x.sum(axis=ax), 1, "e4m3")
        for pos in (2, 3, 4):
            out = out + np.expand_dims(mix(cq[:, :, b], mq), pos)
            b += 1
    for axes in ((2, 3), (2, 4), (3, 4)):
        vq = mxq(x.sum(axis=axes), 1, "e4m3")
        for pos in (2, 3, 4):
            shape = [N, DO, 1, 1, 1]
            shape[pos] = M
            out = out + mix(cq[:, :, b], vq).reshape(shape)
            b += 1
    return out + f64(bias)

@@ -1,0 +1,251 @@
+from contextlib import ExitStack
+
+import concourse.mybir as mybir
+
+FLOPS = 2 * 512 * 128 * (16 * 512 + 9 * 16 * 64 + 9 * 16 * 8)
+
+BF16 = mybir.dt.bfloat16
+F32 = mybir.dt.float32
+U32 = mybir.dt.uint32
+U8 = mybir.dt.uint8
+FP8X4 = mybir.dt.float8_e4m3fn_x4
+ADD = mybir.AluOpType.add
+AXIS_X = mybir.AxisListType.X
+IDENTITY = mybir.ActivationFunctionType.Identity
+
+P = 128
+PACK = 4
+NBATCH = 16
+M = 8
+MM = M * M
+W = M * M * M
+DO = 128
+NB = 19
+GN = 4
+NG = NBATCH // GN
+COEF_CHUNKS = ((0, 1), (1, 3), (3, 11), (11, 19))
+GPSIMD_A1 = True
+GPSIMD_ADDS = True
+
+
+def tile_seteq3to3_kernel(tc, x, coefs, bias, out):
+    nc = tc.nc
+    with ExitStack() as ctx:
+        keep = ctx.enter_context(tc.tile_pool(name="keep", bufs=1))
+        xg_pool = ctx.enter_context(tc.tile_pool(name="xg_pool", bufs=3))
+        xq_pool = ctx.enter_context(tc.tile_pool(name="xq_pool", bufs=8))
+        grp = ctx.enter_context(tc.tile_pool(name="grp", bufs=2))
+        tree = ctx.enter_context(tc.tile_pool(name="tree", bufs=2))
+        res = ctx.enter_context(tc.tile_pool(name="res", bufs=6))
+        ps_t = ctx.enter_context(tc.psum_pool(name="ps_t", bufs=4))
+        ps_s = ctx.enter_context(tc.psum_pool(name="ps_s", bufs=1))
+
+        xs = []
+        for n in range(NBATCH):
+            xs.append(keep.tile([P, PACK, W], BF16, name="xs%d" % n, tag="xs%d" % n))
+        cs = keep.tile([P, PACK, DO, NB], BF16, name="cs", tag="cs")
+        bias_bf = keep.tile([P, 1], BF16, name="bias_bf", tag="bias_bf")
+        bias_f = keep.tile([P, 1], F32, name="bias_f", tag="bias_f")
+
+        def load_x(n):
+            nc.sync.dma_start(out=xs[n][:], in_=x[n].rearrange("(p t) i j k -> p t (i j k)", t=PACK))
+
+        load_x(0)
+        load_x(1)
+        nc.sync.dma_start(out=cs[:], in_=coefs.rearrange("(p t) s b -> p t s b", t=PACK))
+        with nc.allow_non_contiguous_dma(reason="128 bias values, one to a partition"):
+            nc.sync.dma_start(out=bias_bf[:], in_=bias.rearrange("a s b c d -> s (a b c d)"))
+        for n in range(2, NBATCH):
+            load_x(n)
+
+        cg = keep.tile([P, NB, DO, PACK], BF16, name="cg", tag="cg", align_bytes=64)
+        cq = keep.tile([P, NB, DO], U32, name="cq", tag="cq", align_bytes=64)
+        csc = keep.tile([P, NB, DO], U8, name="csc", tag="csc", align_bytes=64)
+
+        def coef_chunk(b0, b1):
+            nc.scalar.copy(out=cg[:, b0:b1], in_=cs[:, :, :, b0:b1].rearrange("p t s b -> p b s t"))
+            nc.vector.quantize_mx(
+                out=cq[:, b0:b1].rearrange("p b s -> p (b s)").bitcast(FP8X4),
+                scales=csc[:, b0:b1].rearrange("p b s -> p (b s)"),
+                in_=cg[:, b0:b1].rearrange("p b s t -> p (b s t)"),
+            )
+
+        vb = keep.tile([P, 3, NBATCH, M, PACK], BF16, name="vb", tag="vb", align_bytes=64)
+        nc.vector.memset(vb[:], 0.0)
+
+        def mx(acc, b, rhs, rhs_scale, start, stop):
+            nc.tensor.matmul_mx(
+                out=acc,
+                lhsT=cq[:, b, :].bitcast(FP8X4),
+                lhsT_scale=csc[:, b, :],
+                rhs=rhs.bitcast(FP8X4),
+                rhs_scale=rhs_scale,
+                start=start,
+                stop=stop,
+            )
+
+        state = {}
+
+        def sums(n):
+            g, nl = divmod(n, GN)
+            if nl == 0:
+                state["af"] = grp.tile([P, 2, GN, MM, PACK], F32, name="af", tag="af")
+                state["ab"] = grp.tile([P, 3, GN, MM, PACK], BF16, name="ab", tag="ab", align_bytes=64)
+            af = state["af"]
+            ab = state["ab"]
+            xn = xs[n]
+            nc.vector.tensor_reduce(
+                out=af[:, 0, nl].rearrange("p q t -> p t q"),
+                in_=xn[:].rearrange("p t (i q) -> p t q i", i=M),
+                axis=AXIS_X,
+                op=ADD,
+            )
+            a1_out = af[:, 1, nl].rearrange("p (i k) t -> p t i k", k=M)
+            if GPSIMD_A1:
+                xv = xn[:].rearrange("p t (i r) -> p t i r", r=MM)
+                y1 = tree.tile([P, PACK, M, MM // 2], F32, name="y1", tag="y1")
+                y2 = tree.tile([P, PACK, M, MM // 4], F32, name="y2", tag="y2")
+                nc.gpsimd.tensor_tensor(out=y1[:], in0=xv[:, :, :, 0:32], in1=xv[:, :, :, 32:64], op=ADD)
+                nc.gpsimd.tensor_tensor(out=y2[:], in0=y1[:, :, :, 0:16], in1=y1[:, :, :, 16:32], op=ADD)
+                nc.gpsimd.tensor_tensor(out=a1_out, in0=y2[:, :, :, 0:8], in1=y2[:, :, :, 8:16], op=ADD)
+            else:
+                nc.vector.tensor_reduce(
+                    out=a1_out,
+                    in_=xn[:].rearrange("p t (i j k) -> p t i k j", i=M, j=M),
+                    axis=AXIS_X,
+                    op=ADD,
+                )
+            with nc.allow_low_precision(reason="float32 sum, rounded once to bfloat16 on the way out"):
+                nc.vector.tensor_reduce(
+                    out=ab[:, 2, nl].rearrange("p q t -> p t q"),
+                    in_=xn[:].rearrange("p t (q k) -> p t q k", k=M),
+                    axis=AXIS_X,
+                    op=ADD,
+                )
+            xg = xg_pool.tile([P, W, PACK], BF16, name="xg", tag="xg", align_bytes=64)
+            nc.scalar.copy(
+                out=xg[:].rearrange("p (c i) t -> p c t i", i=4),
+                in_=xn[:].rearrange("p t (c i) -> p c t i", i=4),
+            )
+            xq = xq_pool.tile([P, W], U32, name="xq", tag="xq", align_bytes=64)
+            xsc = xq_pool.tile([P, W], U8, name="xsc", tag="xsc", align_bytes=64)
+            nc.vector.quantize_mx(out=xq[:].bitcast(FP8X4), scales=xsc[:], in_=xg[:].rearrange("p w t -> p (w t)"))
+            state["xq%d" % n] = (xq, xsc)
+            if nl % 2 == 1:
+                nc.scalar.copy(out=ab[:, 0:2, nl - 1 : nl + 1], in_=af[:, 0:2, nl - 1 : nl + 1])
+
+        def group_work(g):
+            af = state["af"]
+            ab = state["ab"]
+            n0 = g * GN
+            with nc.allow_low_precision(reason="float32 sum, rounded once to bfloat16 on the way out"):
+                nc.vector.tensor_reduce(
+                    out=vb[:, 0, n0 : n0 + GN],
+                    in_=af[:, 0].rearrange("p n (j k) t -> p n k t j", k=M),
+                    axis=AXIS_X,
+                    op=ADD,
+                )
+                nc.vector.tensor_reduce(
+                    out=vb[:, 1, n0 : n0 + GN],
+                    in_=af[:, 0].rearrange("p n (j k) t -> p n j t k", k=M),
+                    axis=AXIS_X,
+                    op=ADD,
+                )
+                nc.vector.tensor_reduce(
+                    out=vb[:, 2, n0 : n0 + GN],
+                    in_=af[:, 1].rearrange("p n (i k) t -> p n i t k", k=M),
+                    axis=AXIS_X,
+                    op=ADD,
+                )
+            aq = grp.tile([P, 3, GN * MM], U32, name="aq", tag="aq", align_bytes=64)
+            asc = grp.tile([P, 3, GN * MM], U8, name="asc", tag="asc", align_bytes=64)
+            vq = grp.tile([P, 3, NBATCH * M], U32, name="vq", tag="vq", align_bytes=64)
+            vsc = grp.tile([P, 3, NBATCH * M], U8, name="vsc", tag="vsc", align_bytes=64)
+            for a in (2, 0, 1):
+                nc.vector.quantize_mx(
+                    out=aq[:, a].bitcast(FP8X4), scales=asc[:, a], in_=ab[:, a].rearrange("p n q t -> p (n q t)")
+                )
+            for a in range(3):
+                nc.vector.quantize_mx(
+                    out=vq[:, a].bitcast(FP8X4), scales=vsc[:, a], in_=vb[:, a].rearrange("p n m t -> p (n m t)")
+                )
+            t0 = []
+            for nl in range(GN):
+                acc = ps_t.tile([P, W], F32, name="t0", tag="t0")
+                xq, xsc = state["xq%d" % (n0 + nl)]
+                mx(acc[:], 0, xq[:], xsc[:], True, True)
+                t0.append(acc)
+            state["t0"] = t0
+            pp = []
+            for t in range(3):
+                acc = ps_s.tile([P, GN * MM], F32, name="pp%d" % t, tag="pp%d" % t)
+                for a in range(3):
+                    mx(acc[:], 1 + 3 * a + t, aq[:, a], asc[:, a], a == 0, a == 2)
+                pp.append(acc)
+            pq = ps_s.tile([P, 3, NBATCH * M], F32, name="pq", tag="pq")
+            for t in range(3):
+                for a in range(3):
+                    mx(pq[:, t, :], 10 + 3 * a + t, vq[:, a], vsc[:, a], a == 0, a == 2)
+            cols = slice(n0 * M, (n0 + GN) * M)
+            if g == 0:
+                nc.vector.tensor_copy(out=bias_f[:], in_=bias_bf[:])
+            qs = grp.tile([P, 3, GN * M], F32, name="qs", tag="qs")
+            nc.scalar.copy(out=qs[:, 0:2, :], in_=pq[:, 0:2, cols])
+            nc.scalar.activation(out=qs[:, 2, :], in_=pq[:, 2, cols], func=IDENTITY, bias=bias_f[:, 0:1], scale=1.0)
+            b1 = grp.tile([P, GN, MM], F32, name="b1", tag="b1")
+            b2 = grp.tile([P, GN, MM], F32, name="b2", tag="b2")
+            b3 = grp.tile([P, GN, MM], F32, name="b3", tag="b3")
+            nc.scalar.copy(out=b3[:].rearrange("p n q -> p (n q)"), in_=pp[2][:])
+            nc.vector.tensor_tensor(
+                out=b1[:].rearrange("p n (j k) -> p (n j) k", k=M),
+                in0=pp[0][:].rearrange("p (m k) -> p m k", k=M),
+                in1=qs[:, 1, :].unsqueeze(2).to_broadcast([P, GN * M, M]),
+                op=ADD,
+            )
+            nc.vector.tensor_tensor(
+                out=b2[:].rearrange("p n (i k) -> p (n i) k", k=M),
+                in0=pp[1][:].rearrange("p (m k) -> p m k", k=M),
+                in1=qs[:, 0, :].unsqueeze(2).to_broadcast([P, GN * M, M]),
+                op=ADD,
+            )
+            b1v = b1[:].rearrange("p n (j k) -> p n j k", k=M)
+            nc.vector.tensor_tensor(
+                out=b1v,
+                in0=b1v,
+                in1=qs[:, 2, :].rearrange("p (n k) -> p n k", k=M).unsqueeze(2).to_broadcast([P, GN, M, M]),
+                op=ADD,
+            )
+            state["b"] = (b1, b2, b3)
+
+        def epilogue(n):
+            g, nl = divmod(n, GN)
+            b1, b2, b3 = state["b"]
+            acc = state["t0"][nl]
+            r = res.tile([P, W], F32, name="r", tag="r")
+            nc.vector.tensor_tensor(
+                out=r[:].rearrange("p (i q) -> p i q", q=MM),
+                in0=acc[:].rearrange("p (i q) -> p i q", q=MM),
+                in1=b1[:, nl, :].unsqueeze(1).to_broadcast([P, M, MM]),
+                op=ADD,
+            )
+            eng2 = nc.gpsimd if (GPSIMD_ADDS and g < NG - 1) else nc.vector
+            eng3 = nc.gpsimd if GPSIMD_ADDS else nc.vector
+            r4 = r[:].rearrange("p (i j k) -> p i j k", j=M, k=M)
+            eng2.tensor_tensor(
+                out=r4,
+                in0=r4,
+                in1=b2[:, nl, :].rearrange("p (i k) -> p i k", k=M).unsqueeze(2).to_broadcast([P, M, M, M]),
+                op=ADD,
+            )
+            r3 = r[:].rearrange("p (m k) -> p m k", k=M)
+            eng3.tensor_tensor(out=r3, in0=r3, in1=b3[:, nl, :].unsqueeze(2).to_broadcast([P, MM, M]), op=ADD)
+            nc.sync.dma_start(out=out[n].rearrange("s i j k -> s (i j k)"), in_=r[:])
+
+        for g in range(NG):
+            for nl in range(GN):
+                sums(g * GN + nl)
+                if g == 0:
+                    coef_chunk(COEF_CHUNKS[nl][0], COEF_CHUNKS[nl][1])
+            group_work(g)
+            for nl in range(GN):
+                epilogue(g * GN + nl)

@@ -1,6 +1,7 @@
 from contextlib import ExitStack
 
 import concourse.mybir as mybir
+from concourse.masks import make_identity
 
 FLOPS = 2 * 512 * 128 * (16 * 512 + 9 * 16 * 64 + 9 * 16 * 8)
 
@@ -23,55 +24,73 @@ DO = 128
 NB = 19
 GN = 4
 NG = NBATCH // GN
-COEF_CHUNKS = ((0, 1), (1, 3), (3, 11), (11, 19))
-GPSIMD_A1 = True
-GPSIMD_ADDS = True
+GC = GN * MM
+COEF_CHUNKS = ((0, 8), (8, 16), (16, 18), (18, 19))
+A0_PLAN = (
+    (("pe", 0, 1), ("pe", 1, 1), ("pe", 2, 1), ("v", 3, 1)),
+    (("v", 0, 2), ("v", 2, 2)),
+    (("v", 0, 2), ("v", 2, 2)),
+    (("v", 0, 2), ("v", 2, 2)),
+)
+A1_PLAN = (
+    (("v", 0, 2), ("v", 2, 2)),
+    (("v", 0, 2), ("v", 2, 2)),
+    (("v", 0, 2), ("v", 2, 2)),
+    (("v", 0, 2), ("v", 2, 2)),
+)
+B2_ENGINE = "v"
+SEG = 2
 
 
 def tile_seteq3to3_kernel(tc, x, coefs, bias, out):
     nc = tc.nc
     with ExitStack() as ctx:
         keep = ctx.enter_context(tc.tile_pool(name="keep", bufs=1))
-        xg_pool = ctx.enter_context(tc.tile_pool(name="xg_pool", bufs=3))
-        xq_pool = ctx.enter_context(tc.tile_pool(name="xq_pool", bufs=8))
-        grp = ctx.enter_context(tc.tile_pool(name="grp", bufs=2))
-        tree = ctx.enter_context(tc.tile_pool(name="tree", bufs=2))
-        res = ctx.enter_context(tc.tile_pool(name="res", bufs=6))
-        ps_t = ctx.enter_context(tc.psum_pool(name="ps_t", bufs=4))
+        xs_pool = ctx.enter_context(tc.tile_pool(name="xs_pool", bufs=3))
+        cg_pool = ctx.enter_context(tc.tile_pool(name="cg_pool", bufs=2))
+        one = ctx.enter_context(tc.tile_pool(name="one", bufs=1))
+        two = ctx.enter_context(tc.tile_pool(name="two", bufs=2))
+        ps_t = ctx.enter_context(tc.psum_pool(name="ps_t", bufs=5))
         ps_s = ctx.enter_context(tc.psum_pool(name="ps_s", bufs=1))
+        engines = {"v": nc.vector, "g": nc.gpsimd}
 
-        xs = []
-        for n in range(NBATCH):
-            xs.append(keep.tile([P, PACK, W], BF16, name="xs%d" % n, tag="xs%d" % n))
         cs = keep.tile([P, PACK, DO, NB], BF16, name="cs", tag="cs")
         bias_bf = keep.tile([P, 1], BF16, name="bias_bf", tag="bias_bf")
         bias_f = keep.tile([P, 1], F32, name="bias_f", tag="bias_f")
+        xs = {}
 
-        def load_x(n):
-            nc.sync.dma_start(out=xs[n][:], in_=x[n].rearrange("(p t) i j k -> p t (i j k)", t=PACK))
+        def load_x(g):
+            xs[g] = xs_pool.tile([P, GN, PACK, W], BF16, name="xs", tag="xs")
+            for nl in range(GN):
+                nc.sync.dma_start(
+                    out=xs[g][:, nl], in_=x[g * GN + nl].rearrange("(p t) i j k -> p t (i j k)", t=PACK)
+                )
 
         load_x(0)
-        load_x(1)
         nc.sync.dma_start(out=cs[:], in_=coefs.rearrange("(p t) s b -> p t s b", t=PACK))
         with nc.allow_non_contiguous_dma(reason="128 bias values, one to a partition"):
             nc.sync.dma_start(out=bias_bf[:], in_=bias.rearrange("a s b c d -> s (a b c d)"))
-        for n in range(2, NBATCH):
-            load_x(n)
+        load_x(1)
+        load_x(2)
 
-        cg = keep.tile([P, NB, DO, PACK], BF16, name="cg", tag="cg", align_bytes=64)
+        ident = keep.tile([P, P], BF16, name="ident", tag="ident")
+        make_identity(nc, ident[:])
+        vb = keep.tile([P, 3, NBATCH, M, PACK], BF16, name="vb", tag="vb", align_bytes=64)
+        nc.vector.memset(vb[:], 0.0)
+        nc.vector.tensor_copy(out=bias_f[:], in_=bias_bf[:])
+
         cq = keep.tile([P, NB, DO], U32, name="cq", tag="cq", align_bytes=64)
         csc = keep.tile([P, NB, DO], U8, name="csc", tag="csc", align_bytes=64)
 
         def coef_chunk(b0, b1):
-            nc.scalar.copy(out=cg[:, b0:b1], in_=cs[:, :, :, b0:b1].rearrange("p t s b -> p b s t"))
+            cg = cg_pool.tile([P, 8, DO, PACK], BF16, name="cg", tag="cg", align_bytes=64)
+            nb = b1 - b0
+            nc.scalar.copy(out=cg[:, 0:nb], in_=cs[:, :, :, b0:b1].rearrange("p t s b -> p b s t"))
             nc.vector.quantize_mx(
                 out=cq[:, b0:b1].rearrange("p b s -> p (b s)").bitcast(FP8X4),
                 scales=csc[:, b0:b1].rearrange("p b s -> p (b s)"),
-                in_=cg[:, b0:b1].rearrange("p b s t -> p (b s t)"),
+                in_=cg[:, 0:nb].rearrange("p b s t -> p (b s t)"),
             )
-
-        vb = keep.tile([P, 3, NBATCH, M, PACK], BF16, name="vb", tag="vb", align_bytes=64)
-        nc.vector.memset(vb[:], 0.0)
 
         def mx(acc, b, rhs, rhs_scale, start, stop):
             nc.tensor.matmul_mx(
@@ -84,83 +103,112 @@ def tile_seteq3to3_kernel(tc, x, coefs, bias, out):
                 stop=stop,
             )
 
-        state = {}
+        st = {}
 
-        def sums(n):
-            g, nl = divmod(n, GN)
-            if nl == 0:
-                state["af"] = grp.tile([P, 2, GN, MM, PACK], F32, name="af", tag="af")
-                state["ab"] = grp.tile([P, 3, GN, MM, PACK], BF16, name="ab", tag="ab", align_bytes=64)
-            af = state["af"]
-            ab = state["ab"]
-            xn = xs[n]
-            nc.vector.tensor_reduce(
-                out=af[:, 0, nl].rearrange("p q t -> p t q"),
-                in_=xn[:].rearrange("p t (i q) -> p t q i", i=M),
-                axis=AXIS_X,
+        def regroup(g):
+            xg = one.tile([P, M, GN, MM, PACK], BF16, name="xg", tag="xg", align_bytes=64)
+            for nl in range(GN):
+                nc.scalar.copy(out=xg[:, :, nl], in_=xs[g][:, nl].rearrange("p t (i q) -> p i q t", i=M))
+            st["xg"] = xg
+
+        def tree(who, src, dst, rows, half):
+            eng = engines[who]
+            y1 = one.tile([P, SEG * 1024], F32, name="y1" + who, tag="y1" + who)
+            y2 = one.tile([P, SEG * 512], F32, name="y2" + who, tag="y2" + who)
+            v1 = y1[:, 0 : rows * half].rearrange("p (r c) -> p r c", c=half)
+            v2 = y2[:, 0 : rows * half // 2].rearrange("p (r c) -> p r c", c=half // 2)
+            eng.tensor_tensor(out=v1, in0=src[:, :, 0:half], in1=src[:, :, half : 2 * half], op=ADD)
+            eng.tensor_tensor(out=v2, in0=v1[:, :, 0 : half // 2], in1=v1[:, :, half // 2 : half], op=ADD)
+            eng.tensor_tensor(out=dst, in0=v2[:, :, 0 : half // 4], in1=v2[:, :, half // 4 : half // 2], op=ADD)
+
+        def sums(g):
+            a0f = two.tile([P, GN, PACK, MM], F32, name="a0f", tag="a0f")
+            a1f = two.tile([P, GN, PACK, MM], F32, name="a1f", tag="a1f")
+            ab = one.tile([P, 3, GN, MM, PACK], BF16, name="ab", tag="ab", align_bytes=64)
+            st["a0f"], st["a1f"], st["ab"] = a0f, a1f, ab
+            xg = xs[g]
+            for who, n0, cnt in A0_PLAN[g]:
+                if who == "pe":
+                    acc = ps_s.tile([P, PACK, MM], F32, name="pe_sum", tag="pe_sum")
+                    for i in range(M):
+                        nc.tensor.matmul(
+                            out=acc[:],
+                            lhsT=ident[:],
+                            rhs=xg[:, n0, :, i * MM : (i + 1) * MM],
+                            start=(i == 0),
+                            stop=(i == M - 1),
+                        )
+                    nc.scalar.copy(out=a0f[:, n0], in_=acc[:])
+                else:
+                    tree(
+                        who,
+                        xg[:, n0 : n0 + cnt].rearrange("p n t w -> p (n t) w"),
+                        a0f[:, n0 : n0 + cnt].rearrange("p n t q -> p (n t) q"),
+                        cnt * PACK,
+                        W // 2,
+                    )
+            for who, n0, cnt in A1_PLAN[g]:
+                tree(
+                    who,
+                    xg[:, n0 : n0 + cnt].rearrange("p n t (i r) -> p (n t i) r", r=MM),
+                    a1f[:, n0 : n0 + cnt].rearrange("p n t (i k) -> p (n t i) k", k=M),
+                    cnt * PACK * M,
+                    MM // 2,
+                )
+            with nc.allow_low_precision(reason="float32 sum, rounded once to bfloat16 on the way out"):
+                for nl in range(GN):
+                    nc.vector.tensor_reduce(
+                        out=ab[:, 2, nl].rearrange("p q t -> p t q"),
+                        in_=xg[:, nl].rearrange("p t (q k) -> p t q k", k=M),
+                        axis=AXIS_X,
+                        op=ADD,
+                    )
+
+        def casts(g):
+            nc.scalar.copy(out=st["ab"][:, 0], in_=st["a0f"][:].rearrange("p n t q -> p n q t"))
+            nc.scalar.copy(out=st["ab"][:, 1], in_=st["a1f"][:].rearrange("p n t q -> p n q t"))
+
+        def vsums(g):
+            a0f, a1f = st["a0f"], st["a1f"]
+            n0 = g * GN
+            z1 = one.tile([P, GN, PACK, MM // 2], F32, name="z1", tag="z1")
+            z2 = one.tile([P, GN, PACK, MM // 4], F32, name="z2", tag="z2")
+            nc.vector.tensor_tensor(out=z1[:], in0=a0f[:, :, :, 0:32], in1=a0f[:, :, :, 32:64], op=ADD)
+            nc.vector.tensor_tensor(out=z2[:], in0=z1[:, :, :, 0:16], in1=z1[:, :, :, 16:32], op=ADD)
+            nc.vector.tensor_tensor(
+                out=vb[:, 0, n0 : n0 + GN].rearrange("p n k t -> p n t k"),
+                in0=z2[:, :, :, 0:8],
+                in1=z2[:, :, :, 8:16],
                 op=ADD,
             )
-            a1_out = af[:, 1, nl].rearrange("p (i k) t -> p t i k", k=M)
-            if GPSIMD_A1:
-                xv = xn[:].rearrange("p t (i r) -> p t i r", r=MM)
-                y1 = tree.tile([P, PACK, M, MM // 2], F32, name="y1", tag="y1")
-                y2 = tree.tile([P, PACK, M, MM // 4], F32, name="y2", tag="y2")
-                nc.gpsimd.tensor_tensor(out=y1[:], in0=xv[:, :, :, 0:32], in1=xv[:, :, :, 32:64], op=ADD)
-                nc.gpsimd.tensor_tensor(out=y2[:], in0=y1[:, :, :, 0:16], in1=y1[:, :, :, 16:32], op=ADD)
-                nc.gpsimd.tensor_tensor(out=a1_out, in0=y2[:, :, :, 0:8], in1=y2[:, :, :, 8:16], op=ADD)
-            else:
-                nc.vector.tensor_reduce(
-                    out=a1_out,
-                    in_=xn[:].rearrange("p t (i j k) -> p t i k j", i=M, j=M),
-                    axis=AXIS_X,
-                    op=ADD,
-                )
             with nc.allow_low_precision(reason="float32 sum, rounded once to bfloat16 on the way out"):
                 nc.vector.tensor_reduce(
-                    out=ab[:, 2, nl].rearrange("p q t -> p t q"),
-                    in_=xn[:].rearrange("p t (q k) -> p t q k", k=M),
+                    out=vb[:, 1, n0 : n0 + GN].rearrange("p n j t -> p n t j"),
+                    in_=a0f[:].rearrange("p n t (j k) -> p n t j k", k=M),
                     axis=AXIS_X,
                     op=ADD,
                 )
-            xg = xg_pool.tile([P, W, PACK], BF16, name="xg", tag="xg", align_bytes=64)
-            nc.scalar.copy(
-                out=xg[:].rearrange("p (c i) t -> p c t i", i=4),
-                in_=xn[:].rearrange("p t (c i) -> p c t i", i=4),
-            )
-            xq = xq_pool.tile([P, W], U32, name="xq", tag="xq", align_bytes=64)
-            xsc = xq_pool.tile([P, W], U8, name="xsc", tag="xsc", align_bytes=64)
-            nc.vector.quantize_mx(out=xq[:].bitcast(FP8X4), scales=xsc[:], in_=xg[:].rearrange("p w t -> p (w t)"))
-            state["xq%d" % n] = (xq, xsc)
-            if nl % 2 == 1:
-                nc.scalar.copy(out=ab[:, 0:2, nl - 1 : nl + 1], in_=af[:, 0:2, nl - 1 : nl + 1])
+                nc.vector.tensor_reduce(
+                    out=vb[:, 2, n0 : n0 + GN].rearrange("p n i t -> p n t i"),
+                    in_=a1f[:].rearrange("p n t (i k) -> p n t i k", k=M),
+                    axis=AXIS_X,
+                    op=ADD,
+                )
 
-        def group_work(g):
-            af = state["af"]
-            ab = state["ab"]
-            n0 = g * GN
-            with nc.allow_low_precision(reason="float32 sum, rounded once to bfloat16 on the way out"):
-                nc.vector.tensor_reduce(
-                    out=vb[:, 0, n0 : n0 + GN],
-                    in_=af[:, 0].rearrange("p n (j k) t -> p n k t j", k=M),
-                    axis=AXIS_X,
-                    op=ADD,
+        def quant(g):
+            xg, ab = st["xg"], st["ab"]
+            xq = two.tile([P, M, GC], U32, name="xq", tag="xq", align_bytes=64)
+            xsc = two.tile([P, M, GC], U8, name="xsc", tag="xsc", align_bytes=64)
+            aq = two.tile([P, 3, GC], U32, name="aq", tag="aq", align_bytes=64)
+            asc = two.tile([P, 3, GC], U8, name="asc", tag="asc", align_bytes=64)
+            vq = two.tile([P, 3, NBATCH * M], U32, name="vq", tag="vq", align_bytes=64)
+            vsc = two.tile([P, 3, NBATCH * M], U8, name="vsc", tag="vsc", align_bytes=64)
+            for b in range(M // 2):
+                nc.vector.quantize_mx(
+                    out=xq[:, 2 * b : 2 * b + 2].rearrange("p i c -> p (i c)").bitcast(FP8X4),
+                    scales=xsc[:, 2 * b : 2 * b + 2].rearrange("p i c -> p (i c)"),
+                    in_=xg[:, 2 * b : 2 * b + 2].rearrange("p i n q t -> p (i n q t)"),
                 )
-                nc.vector.tensor_reduce(
-                    out=vb[:, 1, n0 : n0 + GN],
-                    in_=af[:, 0].rearrange("p n (j k) t -> p n j t k", k=M),
-                    axis=AXIS_X,
-                    op=ADD,
-                )
-                nc.vector.tensor_reduce(
-                    out=vb[:, 2, n0 : n0 + GN],
-                    in_=af[:, 1].rearrange("p n (i k) t -> p n i t k", k=M),
-                    axis=AXIS_X,
-                    op=ADD,
-                )
-            aq = grp.tile([P, 3, GN * MM], U32, name="aq", tag="aq", align_bytes=64)
-            asc = grp.tile([P, 3, GN * MM], U8, name="asc", tag="asc", align_bytes=64)
-            vq = grp.tile([P, 3, NBATCH * M], U32, name="vq", tag="vq", align_bytes=64)
-            vsc = grp.tile([P, 3, NBATCH * M], U8, name="vsc", tag="vsc", align_bytes=64)
             for a in (2, 0, 1):
                 nc.vector.quantize_mx(
                     out=aq[:, a].bitcast(FP8X4), scales=asc[:, a], in_=ab[:, a].rearrange("p n q t -> p (n q t)")
@@ -169,83 +217,103 @@ def tile_seteq3to3_kernel(tc, x, coefs, bias, out):
                 nc.vector.quantize_mx(
                     out=vq[:, a].bitcast(FP8X4), scales=vsc[:, a], in_=vb[:, a].rearrange("p n m t -> p (n m t)")
                 )
-            t0 = []
-            for nl in range(GN):
-                acc = ps_t.tile([P, W], F32, name="t0", tag="t0")
-                xq, xsc = state["xq%d" % (n0 + nl)]
-                mx(acc[:], 0, xq[:], xsc[:], True, True)
-                t0.append(acc)
-            state["t0"] = t0
-            pp = []
-            for t in range(3):
-                acc = ps_s.tile([P, GN * MM], F32, name="pp%d" % t, tag="pp%d" % t)
+            st["q"] = (xq, xsc, aq, asc, vq, vsc)
+
+        def pe(g):
+            xq, xsc, aq, asc, vq, vsc = st["q"]
+            pp = ps_s.tile([P, 2, GC], F32, name="pp", tag="pp")
+            for t in range(2):
                 for a in range(3):
-                    mx(acc[:], 1 + 3 * a + t, aq[:, a], asc[:, a], a == 0, a == 2)
-                pp.append(acc)
+                    mx(pp[:, t, :], 2 + 3 * a + t, aq[:, a], asc[:, a], a == 0, a == 2)
             pq = ps_s.tile([P, 3, NBATCH * M], F32, name="pq", tag="pq")
             for t in range(3):
                 for a in range(3):
                     mx(pq[:, t, :], 10 + 3 * a + t, vq[:, a], vsc[:, a], a == 0, a == 2)
-            cols = slice(n0 * M, (n0 + GN) * M)
-            if g == 0:
-                nc.vector.tensor_copy(out=bias_f[:], in_=bias_bf[:])
-            qs = grp.tile([P, 3, GN * M], F32, name="qs", tag="qs")
+            banks = []
+            for b in range(M // 2):
+                tb = ps_t.tile([P, 2, GC], F32, name="tb", tag="tb")
+                for h in range(2):
+                    mx(tb[:, h, :], 0, xq[:, 2 * b + h], xsc[:, 2 * b + h], True, False)
+                    for a in range(3):
+                        mx(tb[:, h, :], 1 + 3 * a, aq[:, a], asc[:, a], False, a == 2)
+                banks.append(tb)
+            st["ps%d" % g] = (pp, pq, banks)
+
+        def small(g):
+            pp, pq, banks = st["ps%d" % g]
+            cols = slice(g * GN * M, (g + 1) * GN * M)
+            qs = two.tile([P, 3, GN * M], F32, name="qs", tag="qs")
             nc.scalar.copy(out=qs[:, 0:2, :], in_=pq[:, 0:2, cols])
             nc.scalar.activation(out=qs[:, 2, :], in_=pq[:, 2, cols], func=IDENTITY, bias=bias_f[:, 0:1], scale=1.0)
-            b1 = grp.tile([P, GN, MM], F32, name="b1", tag="b1")
-            b2 = grp.tile([P, GN, MM], F32, name="b2", tag="b2")
-            b3 = grp.tile([P, GN, MM], F32, name="b3", tag="b3")
-            nc.scalar.copy(out=b3[:].rearrange("p n q -> p (n q)"), in_=pp[2][:])
+            b2 = two.tile([P, M, GN, M], F32, name="b2", tag="b2")
+            b3 = two.tile([P, M, GN, M], F32, name="b3", tag="b3")
+            b2v = b2[:].rearrange("p i n k -> p n i k")
             nc.vector.tensor_tensor(
-                out=b1[:].rearrange("p n (j k) -> p (n j) k", k=M),
-                in0=pp[0][:].rearrange("p (m k) -> p m k", k=M),
-                in1=qs[:, 1, :].unsqueeze(2).to_broadcast([P, GN * M, M]),
+                out=b3[:].rearrange("p i n j -> p n i j"),
+                in0=pp[:, 1, :].rearrange("p (n i j) -> p n i j", i=M, j=M),
+                in1=qs[:, 1, :].rearrange("p (n j) -> p n j", j=M).unsqueeze(2).to_broadcast([P, GN, M, M]),
                 op=ADD,
             )
             nc.vector.tensor_tensor(
-                out=b2[:].rearrange("p n (i k) -> p (n i) k", k=M),
-                in0=pp[1][:].rearrange("p (m k) -> p m k", k=M),
-                in1=qs[:, 0, :].unsqueeze(2).to_broadcast([P, GN * M, M]),
+                out=b2v,
+                in0=pp[:, 0, :].rearrange("p (n i k) -> p n i k", i=M, k=M),
+                in1=qs[:, 0, :].rearrange("p (n i) -> p n i", i=M).unsqueeze(3).to_broadcast([P, GN, M, M]),
                 op=ADD,
             )
-            b1v = b1[:].rearrange("p n (j k) -> p n j k", k=M)
             nc.vector.tensor_tensor(
-                out=b1v,
-                in0=b1v,
+                out=b2v,
+                in0=b2v,
                 in1=qs[:, 2, :].rearrange("p (n k) -> p n k", k=M).unsqueeze(2).to_broadcast([P, GN, M, M]),
                 op=ADD,
             )
-            state["b"] = (b1, b2, b3)
+            st["b%d" % g] = (b2, b3)
 
-        def epilogue(n):
-            g, nl = divmod(n, GN)
-            b1, b2, b3 = state["b"]
-            acc = state["t0"][nl]
-            r = res.tile([P, W], F32, name="r", tag="r")
-            nc.vector.tensor_tensor(
-                out=r[:].rearrange("p (i q) -> p i q", q=MM),
-                in0=acc[:].rearrange("p (i q) -> p i q", q=MM),
-                in1=b1[:, nl, :].unsqueeze(1).to_broadcast([P, M, MM]),
+        def tadd(g):
+            pp, pq, banks = st["ps%d" % g]
+            b2, b3 = st["b%d" % g]
+            r = two.tile([P, M, GN, MM], F32, name="r", tag="r")
+            for b in range(M // 2):
+                nc.vector.tensor_tensor(
+                    out=r[:, 2 * b : 2 * b + 2].rearrange("p i n (j k) -> p (i n j) k", k=M),
+                    in0=banks[b][:].rearrange("p h (m k) -> p (h m) k", k=M),
+                    in1=b3[:, 2 * b : 2 * b + 2]
+                    .rearrange("p i n j -> p (i n j)")
+                    .unsqueeze(2)
+                    .to_broadcast([P, 2 * GN * M, M]),
+                    op=ADD,
+                )
+            st["r%d" % g] = r
+
+        def finish(g):
+            b2, b3 = st["b%d" % g]
+            r = st["r%d" % g]
+            rv = r[:].rearrange("p i n (j k) -> p (i n) j k", k=M)
+            engines[B2_ENGINE].tensor_tensor(
+                out=rv,
+                in0=rv,
+                in1=b2[:].rearrange("p i n k -> p (i n) k").unsqueeze(2).to_broadcast([P, M * GN, M, M]),
                 op=ADD,
             )
-            eng2 = nc.gpsimd if (GPSIMD_ADDS and g < NG - 1) else nc.vector
-            eng3 = nc.gpsimd if GPSIMD_ADDS else nc.vector
-            r4 = r[:].rearrange("p (i j k) -> p i j k", j=M, k=M)
-            eng2.tensor_tensor(
-                out=r4,
-                in0=r4,
-                in1=b2[:, nl, :].rearrange("p (i k) -> p i k", k=M).unsqueeze(2).to_broadcast([P, M, M, M]),
-                op=ADD,
-            )
-            r3 = r[:].rearrange("p (m k) -> p m k", k=M)
-            eng3.tensor_tensor(out=r3, in0=r3, in1=b3[:, nl, :].unsqueeze(2).to_broadcast([P, MM, M]), op=ADD)
-            nc.sync.dma_start(out=out[n].rearrange("s i j k -> s (i j k)"), in_=r[:])
+            for nl in range(GN):
+                nc.sync.dma_start(out=out[g * GN + nl].rearrange("s i j k -> s i (j k)"), in_=r[:, :, nl, :])
 
         for g in range(NG):
-            for nl in range(GN):
-                sums(g * GN + nl)
-                if g == 0:
-                    coef_chunk(COEF_CHUNKS[nl][0], COEF_CHUNKS[nl][1])
-            group_work(g)
-            for nl in range(GN):
-                epilogue(g * GN + nl)
+            if g + 3 < NG + 1 and g > 0:
+                load_x(g + 2)
+            regroup(g)
+            if g == 0:
+                for b0, b1 in COEF_CHUNKS:
+                    coef_chunk(b0, b1)
+            sums(g)
+            if g > 0:
+                small(g - 1)
+                tadd(g - 1)
+            casts(g)
+            vsums(g)
+            quant(g)
+            pe(g)
+            if g > 0:
+                finish(g - 1)
+        small(NG - 1)
+        tadd(NG - 1)
+        finish(NG - 1)

@@ -27,10 +27,10 @@ NG = NBATCH // GN
 GC = GN * MM
 COEF_CHUNKS = ((0, 8), (8, 16), (16, 18), (18, 19))
 A0_PLAN = (
-    (("pe", 0, 1), ("pe", 1, 1), ("pe", 2, 1), ("v", 3, 1)),
-    (("v", 0, 2), ("v", 2, 2)),
-    (("v", 0, 2), ("v", 2, 2)),
-    (("v", 0, 2), ("v", 2, 2)),
+    (("pe", 0, 1), ("pe", 1, 1), ("pe", 2, 1), ("g", 3, 1)),
+    (("g", 0, 1), ("g", 1, 1), ("g", 2, 1), ("g", 3, 1)),
+    (("g", 0, 1), ("g", 1, 1), ("g", 2, 1), ("g", 3, 1)),
+    (("g", 0, 1), ("g", 1, 1), ("g", 2, 1), ("g", 3, 1)),
 )
 A1_PLAN = (
     (("v", 0, 2), ("v", 2, 2)),
@@ -39,7 +39,7 @@ A1_PLAN = (
     (("v", 0, 2), ("v", 2, 2)),
 )
 B2_ENGINE = "v"
-SEG = 2
+SEG = {"v": 2, "g": 1}
 
 
 def tile_seteq3to3_kernel(tc, x, coefs, bias, out):
@@ -111,15 +111,29 @@ def tile_seteq3to3_kernel(tc, x, coefs, bias, out):
                 nc.scalar.copy(out=xg[:, :, nl], in_=xs[g][:, nl].rearrange("p t (i q) -> p i q t", i=M))
             st["xg"] = xg
 
-        def tree(who, src, dst, rows, half):
+        def tree(who, lane, src, dst, rows, half):
             eng = engines[who]
-            y1 = one.tile([P, SEG * 1024], F32, name="y1" + who, tag="y1" + who)
-            y2 = one.tile([P, SEG * 512], F32, name="y2" + who, tag="y2" + who)
+            tag = who + str(lane)
+            y1 = one.tile([P, SEG[who] * 1024], F32, name="y1" + tag, tag="y1" + tag)
+            y2 = one.tile([P, SEG[who] * 512], F32, name="y2" + tag, tag="y2" + tag)
             v1 = y1[:, 0 : rows * half].rearrange("p (r c) -> p r c", c=half)
             v2 = y2[:, 0 : rows * half // 2].rearrange("p (r c) -> p r c", c=half // 2)
-            eng.tensor_tensor(out=v1, in0=src[:, :, 0:half], in1=src[:, :, half : 2 * half], op=ADD)
-            eng.tensor_tensor(out=v2, in0=v1[:, :, 0 : half // 2], in1=v1[:, :, half // 2 : half], op=ADD)
-            eng.tensor_tensor(out=dst, in0=v2[:, :, 0 : half // 4], in1=v2[:, :, half // 4 : half // 2], op=ADD)
+            return (
+                lambda: eng.tensor_tensor(out=v1, in0=src[:, :, 0:half], in1=src[:, :, half : 2 * half], op=ADD),
+                lambda: eng.tensor_tensor(out=v2, in0=v1[:, :, 0 : half // 2], in1=v1[:, :, half // 2 : half], op=ADD),
+                lambda: eng.tensor_tensor(
+                    out=dst, in0=v2[:, :, 0 : half // 4], in1=v2[:, :, half // 4 : half // 2], op=ADD
+                ),
+            )
+
+        def weave(jobs):
+            for who in ("g", "v"):
+                mine = [j for j in jobs if j[0] == who]
+                for k in range(0, len(mine), 2):
+                    pair = [tree(j[0], lane, j[1], j[2], j[3], j[4]) for lane, j in enumerate(mine[k : k + 2])]
+                    for level in range(3):
+                        for t3 in pair:
+                            t3[level]()
 
         def sums(g):
             a0f = two.tile([P, GN, PACK, MM], F32, name="a0f", tag="a0f")
@@ -127,6 +141,7 @@ def tile_seteq3to3_kernel(tc, x, coefs, bias, out):
             ab = one.tile([P, 3, GN, MM, PACK], BF16, name="ab", tag="ab", align_bytes=64)
             st["a0f"], st["a1f"], st["ab"] = a0f, a1f, ab
             xg = xs[g]
+            jobs = []
             for who, n0, cnt in A0_PLAN[g]:
                 if who == "pe":
                     acc = ps_s.tile([P, PACK, MM], F32, name="pe_sum", tag="pe_sum")
@@ -140,21 +155,26 @@ def tile_seteq3to3_kernel(tc, x, coefs, bias, out):
                         )
                     nc.scalar.copy(out=a0f[:, n0], in_=acc[:])
                 else:
-                    tree(
-                        who,
-                        xg[:, n0 : n0 + cnt].rearrange("p n t w -> p (n t) w"),
-                        a0f[:, n0 : n0 + cnt].rearrange("p n t q -> p (n t) q"),
-                        cnt * PACK,
-                        W // 2,
+                    jobs.append(
+                        (
+                            who,
+                            xg[:, n0 : n0 + cnt].rearrange("p n t w -> p (n t) w"),
+                            a0f[:, n0 : n0 + cnt].rearrange("p n t q -> p (n t) q"),
+                            cnt * PACK,
+                            W // 2,
+                        )
                     )
             for who, n0, cnt in A1_PLAN[g]:
-                tree(
-                    who,
-                    xg[:, n0 : n0 + cnt].rearrange("p n t (i r) -> p (n t i) r", r=MM),
-                    a1f[:, n0 : n0 + cnt].rearrange("p n t (i k) -> p (n t i) k", k=M),
-                    cnt * PACK * M,
-                    MM // 2,
+                jobs.append(
+                    (
+                        who,
+                        xg[:, n0 : n0 + cnt].rearrange("p n t (i r) -> p (n t i) r", r=MM),
+                        a1f[:, n0 : n0 + cnt].rearrange("p n t (i k) -> p (n t i) k", k=M),
+                        cnt * PACK * M,
+                        MM // 2,
+                    )
                 )
+            weave(jobs)
             with nc.allow_low_precision(reason="float32 sum, rounded once to bfloat16 on the way out"):
                 for nl in range(GN):
                     nc.vector.tensor_reduce(
@@ -174,13 +194,6 @@ def tile_seteq3to3_kernel(tc, x, coefs, bias, out):
             z1 = one.tile([P, GN, PACK, MM // 2], F32, name="z1", tag="z1")
             z2 = one.tile([P, GN, PACK, MM // 4], F32, name="z2", tag="z2")
             nc.vector.tensor_tensor(out=z1[:], in0=a0f[:, :, :, 0:32], in1=a0f[:, :, :, 32:64], op=ADD)
-            nc.vector.tensor_tensor(out=z2[:], in0=z1[:, :, :, 0:16], in1=z1[:, :, :, 16:32], op=ADD)
-            nc.vector.tensor_tensor(
-                out=vb[:, 0, n0 : n0 + GN].rearrange("p n k t -> p n t k"),
-                in0=z2[:, :, :, 0:8],
-                in1=z2[:, :, :, 8:16],
-                op=ADD,
-            )
             with nc.allow_low_precision(reason="float32 sum, rounded once to bfloat16 on the way out"):
                 nc.vector.tensor_reduce(
                     out=vb[:, 1, n0 : n0 + GN].rearrange("p n j t -> p n t j"),
@@ -188,12 +201,20 @@ def tile_seteq3to3_kernel(tc, x, coefs, bias, out):
                     axis=AXIS_X,
                     op=ADD,
                 )
+            nc.vector.tensor_tensor(out=z2[:], in0=z1[:, :, :, 0:16], in1=z1[:, :, :, 16:32], op=ADD)
+            with nc.allow_low_precision(reason="float32 sum, rounded once to bfloat16 on the way out"):
                 nc.vector.tensor_reduce(
                     out=vb[:, 2, n0 : n0 + GN].rearrange("p n i t -> p n t i"),
                     in_=a1f[:].rearrange("p n t (i k) -> p n t i k", k=M),
                     axis=AXIS_X,
                     op=ADD,
                 )
+            nc.vector.tensor_tensor(
+                out=vb[:, 0, n0 : n0 + GN].rearrange("p n k t -> p n t k"),
+                in0=z2[:, :, :, 0:8],
+                in1=z2[:, :, :, 8:16],
+                op=ADD,
+            )
 
         def quant(g):
             xg, ab = st["xg"], st["ab"]
@@ -249,15 +270,15 @@ def tile_seteq3to3_kernel(tc, x, coefs, bias, out):
             b3 = two.tile([P, M, GN, M], F32, name="b3", tag="b3")
             b2v = b2[:].rearrange("p i n k -> p n i k")
             nc.vector.tensor_tensor(
-                out=b3[:].rearrange("p i n j -> p n i j"),
-                in0=pp[:, 1, :].rearrange("p (n i j) -> p n i j", i=M, j=M),
-                in1=qs[:, 1, :].rearrange("p (n j) -> p n j", j=M).unsqueeze(2).to_broadcast([P, GN, M, M]),
-                op=ADD,
-            )
-            nc.vector.tensor_tensor(
                 out=b2v,
                 in0=pp[:, 0, :].rearrange("p (n i k) -> p n i k", i=M, k=M),
                 in1=qs[:, 0, :].rearrange("p (n i) -> p n i", i=M).unsqueeze(3).to_broadcast([P, GN, M, M]),
+                op=ADD,
+            )
+            nc.vector.tensor_tensor(
+                out=b3[:].rearrange("p i n j -> p n i j"),
+                in0=pp[:, 1, :].rearrange("p (n i j) -> p n i j", i=M, j=M),
+                in1=qs[:, 1, :].rearrange("p (n j) -> p n j", j=M).unsqueeze(2).to_broadcast([P, GN, M, M]),
                 op=ADD,
             )
             nc.vector.tensor_tensor(

@@ -26,71 +26,47 @@ GN = 4
 NG = NBATCH // GN
 GC = GN * MM
 COEF_CHUNKS = ((0, 8), (8, 16), (16, 18), (18, 19))
-A0_PLAN = (
-    (("pe", 0, 1), ("pe", 1, 1), ("pe", 2, 1), ("g", 3, 1)),
-    (("g", 0, 1), ("g", 1, 1), ("g", 2, 1), ("g", 3, 1)),
-    (("g", 0, 1), ("g", 1, 1), ("g", 2, 1), ("g", 3, 1)),
-    (("g", 0, 1), ("g", 1, 1), ("g", 2, 1), ("g", 3, 1)),
-)
-A1_PLAN = (
-    (("v", 0, 2), ("v", 2, 2)),
-    (("v", 0, 2), ("v", 2, 2)),
-    (("v", 0, 2), ("v", 2, 2)),
-    (("v", 0, 2), ("v", 2, 2)),
-)
-B2_ENGINE = "v"
-SEG = {"v": 2, "g": 1}
+G_A0 = ((0, 2), (2, 2), (4, 2), (6, 2))
+PE_A0 = (8, 9, 10)
+V_A0 = {2: ((11, 1),), 3: ((12, 2), (14, 2))}
+COEF_AFTER = 6
+PIN = True
 
 
 def tile_seteq3to3_kernel(tc, x, coefs, bias, out):
     nc = tc.nc
     with ExitStack() as ctx:
         keep = ctx.enter_context(tc.tile_pool(name="keep", bufs=1))
-        xs_pool = ctx.enter_context(tc.tile_pool(name="xs_pool", bufs=3))
-        cg_pool = ctx.enter_context(tc.tile_pool(name="cg_pool", bufs=2))
         one = ctx.enter_context(tc.tile_pool(name="one", bufs=1))
         two = ctx.enter_context(tc.tile_pool(name="two", bufs=2))
-        ps_t = ctx.enter_context(tc.psum_pool(name="ps_t", bufs=5))
+        ps_t = ctx.enter_context(tc.psum_pool(name="ps_t", bufs=6))
         ps_s = ctx.enter_context(tc.psum_pool(name="ps_s", bufs=1))
         engines = {"v": nc.vector, "g": nc.gpsimd}
-
-        cs = keep.tile([P, PACK, DO, NB], BF16, name="cs", tag="cs")
-        bias_bf = keep.tile([P, 1], BF16, name="bias_bf", tag="bias_bf")
-        bias_f = keep.tile([P, 1], F32, name="bias_f", tag="bias_f")
-        xs = {}
-
-        def load_x(g):
-            xs[g] = xs_pool.tile([P, GN, PACK, W], BF16, name="xs", tag="xs")
-            for nl in range(GN):
-                nc.sync.dma_start(
-                    out=xs[g][:, nl], in_=x[g * GN + nl].rearrange("(p t) i j k -> p t (i j k)", t=PACK)
-                )
-
-        load_x(0)
-        nc.sync.dma_start(out=cs[:], in_=coefs.rearrange("(p t) s b -> p t s b", t=PACK))
-        with nc.allow_non_contiguous_dma(reason="128 bias values, one to a partition"):
-            nc.sync.dma_start(out=bias_bf[:], in_=bias.rearrange("a s b c d -> s (a b c d)"))
-        load_x(1)
-        load_x(2)
+        low = "float32 sum, rounded once to bfloat16 on the way out"
 
         ident = keep.tile([P, P], BF16, name="ident", tag="ident")
         make_identity(nc, ident[:])
+        if PIN:
+            ctx.enter_context(tc.manual_schedule())
+
+        xs = keep.tile([P, NBATCH, PACK, W], BF16, name="xs", tag="xs")
+        cs = one.tile([P, PACK, DO, NB], BF16, name="cs", tag="slot0", align_bytes=64)
+        bias_bf = keep.tile([P, 1], BF16, name="bias_bf", tag="bias_bf")
+        bias_f = keep.tile([P, 1], F32, name="bias_f", tag="bias_f")
+        for n in range(NBATCH):
+            if n == COEF_AFTER:
+                nc.sync.dma_start(out=cs[:], in_=coefs.rearrange("(p t) s b -> p t s b", t=PACK))
+                with nc.allow_non_contiguous_dma(reason="128 bias values, one to a partition"):
+                    nc.sync.dma_start(out=bias_bf[:], in_=bias.rearrange("a s b c d -> s (a b c d)"))
+            nc.sync.dma_start(out=xs[:, n], in_=x[n].rearrange("(p t) i j k -> p t (i j k)", t=PACK))
+
         vb = keep.tile([P, 3, NBATCH, M, PACK], BF16, name="vb", tag="vb", align_bytes=64)
         nc.vector.memset(vb[:], 0.0)
-        nc.vector.tensor_copy(out=bias_f[:], in_=bias_bf[:])
 
         cq = keep.tile([P, NB, DO], U32, name="cq", tag="cq", align_bytes=64)
         csc = keep.tile([P, NB, DO], U8, name="csc", tag="csc", align_bytes=64)
-
-        def coef_chunk(b0, b1):
-            cg = cg_pool.tile([P, 8, DO, PACK], BF16, name="cg", tag="cg", align_bytes=64)
-            nb = b1 - b0
-            nc.scalar.copy(out=cg[:, 0:nb], in_=cs[:, :, :, b0:b1].rearrange("p t s b -> p b s t"))
-            nc.vector.quantize_mx(
-                out=cq[:, b0:b1].rearrange("p b s -> p (b s)").bitcast(FP8X4),
-                scales=csc[:, b0:b1].rearrange("p b s -> p (b s)"),
-                in_=cg[:, 0:nb].rearrange("p b s t -> p (b s t)"),
-            )
+        a0f = keep.tile([P, NBATCH, PACK, MM], F32, name="a0f", tag="a0f")
+        ab2 = keep.tile([P, NBATCH, MM, PACK], BF16, name="ab2", tag="ab2", align_bytes=64)
 
         def mx(acc, b, rhs, rhs_scale, start, stop):
             nc.tensor.matmul_mx(
@@ -108,14 +84,14 @@ def tile_seteq3to3_kernel(tc, x, coefs, bias, out):
         def regroup(g):
             xg = one.tile([P, M, GN, MM, PACK], BF16, name="xg", tag="xg", align_bytes=64)
             for nl in range(GN):
-                nc.scalar.copy(out=xg[:, :, nl], in_=xs[g][:, nl].rearrange("p t (i q) -> p i q t", i=M))
+                nc.scalar.copy(out=xg[:, :, nl], in_=xs[:, g * GN + nl].rearrange("p t (i q) -> p i q t", i=M))
             st["xg"] = xg
 
         def tree(who, lane, src, dst, rows, half):
             eng = engines[who]
             tag = who + str(lane)
-            y1 = one.tile([P, SEG[who] * 1024], F32, name="y1" + tag, tag="y1" + tag)
-            y2 = one.tile([P, SEG[who] * 512], F32, name="y2" + tag, tag="y2" + tag)
+            y1 = one.tile([P, 2048], F32, name="y1" + tag, tag="y1" + tag)
+            y2 = one.tile([P, 1024], F32, name="y2" + tag, tag="y2" + tag)
             v1 = y1[:, 0 : rows * half].rearrange("p (r c) -> p r c", c=half)
             v2 = y2[:, 0 : rows * half // 2].rearrange("p (r c) -> p r c", c=half // 2)
             return (
@@ -126,83 +102,98 @@ def tile_seteq3to3_kernel(tc, x, coefs, bias, out):
                 ),
             )
 
-        def weave(jobs):
-            for who in ("g", "v"):
-                mine = [j for j in jobs if j[0] == who]
-                for k in range(0, len(mine), 2):
-                    pair = [tree(j[0], lane, j[1], j[2], j[3], j[4]) for lane, j in enumerate(mine[k : k + 2])]
-                    for level in range(3):
-                        for t3 in pair:
-                            t3[level]()
+        def a0_job(n0, cnt):
+            return (
+                xs[:, n0 : n0 + cnt].rearrange("p n t w -> p (n t) w"),
+                a0f[:, n0 : n0 + cnt].rearrange("p n t q -> p (n t) q"),
+                cnt * PACK,
+                W // 2,
+            )
 
-        def sums(g):
-            a0f = two.tile([P, GN, PACK, MM], F32, name="a0f", tag="a0f")
-            a1f = two.tile([P, GN, PACK, MM], F32, name="a1f", tag="a1f")
-            ab = one.tile([P, 3, GN, MM, PACK], BF16, name="ab", tag="ab", align_bytes=64)
-            st["a0f"], st["a1f"], st["ab"] = a0f, a1f, ab
-            xg = xs[g]
+        def weave(jobs):
+            for k in range(0, len(jobs), 2):
+                pair = [tree("v", lane, j[0], j[1], j[2], j[3]) for lane, j in enumerate(jobs[k : k + 2])]
+                for level in range(3):
+                    for t3 in pair:
+                        t3[level]()
+
+        regroup(0)
+        cg = one.tile([P, NB, DO, PACK], BF16, name="cg", tag="slot1", align_bytes=64)
+        for b0, b1 in COEF_CHUNKS:
+            nc.scalar.copy(out=cg[:, b0:b1], in_=cs[:, :, :, b0:b1].rearrange("p t s b -> p b s t"))
+        for n0, cnt in G_A0:
+            j = a0_job(n0, cnt)
+            for call in tree("g", 0, j[0], j[1], j[2], j[3]):
+                call()
+        for n in PE_A0:
+            acc = ps_t.tile([P, PACK, MM], F32, name="pe_sum", tag="tb")
+            for i in range(M):
+                nc.tensor.matmul(
+                    out=acc[:],
+                    lhsT=ident[:],
+                    rhs=xs[:, n, :, i * MM : (i + 1) * MM],
+                    start=(i == 0),
+                    stop=(i == M - 1),
+                )
+            nc.scalar.copy(out=a0f[:, n], in_=acc[:])
+        with nc.allow_low_precision(reason=low):
+            for n in range(NBATCH):
+                nc.vector.tensor_reduce(
+                    out=ab2[:, n].rearrange("p q t -> p t q"),
+                    in_=xs[:, n].rearrange("p t (q k) -> p t q k", k=M),
+                    axis=AXIS_X,
+                    op=ADD,
+                )
+
+        nc.vector.tensor_copy(out=bias_f[:], in_=bias_bf[:])
+        for b0, b1 in COEF_CHUNKS:
+            nc.vector.quantize_mx(
+                out=cq[:, b0:b1].rearrange("p b s -> p (b s)").bitcast(FP8X4),
+                scales=csc[:, b0:b1].rearrange("p b s -> p (b s)"),
+                in_=cg[:, b0:b1].rearrange("p b s t -> p (b s t)"),
+            )
+
+        def trees(g):
+            n0 = g * GN
+            a1f = one.tile([P, GN, PACK, MM], F32, name="a1f", tag="a1f")
+            st["a1f"] = a1f
             jobs = []
-            for who, n0, cnt in A0_PLAN[g]:
-                if who == "pe":
-                    acc = ps_s.tile([P, PACK, MM], F32, name="pe_sum", tag="pe_sum")
-                    for i in range(M):
-                        nc.tensor.matmul(
-                            out=acc[:],
-                            lhsT=ident[:],
-                            rhs=xg[:, n0, :, i * MM : (i + 1) * MM],
-                            start=(i == 0),
-                            stop=(i == M - 1),
-                        )
-                    nc.scalar.copy(out=a0f[:, n0], in_=acc[:])
-                else:
-                    jobs.append(
-                        (
-                            who,
-                            xg[:, n0 : n0 + cnt].rearrange("p n t w -> p (n t) w"),
-                            a0f[:, n0 : n0 + cnt].rearrange("p n t q -> p (n t) q"),
-                            cnt * PACK,
-                            W // 2,
-                        )
-                    )
-            for who, n0, cnt in A1_PLAN[g]:
+            for h in range(0, GN, 2):
                 jobs.append(
                     (
-                        who,
-                        xg[:, n0 : n0 + cnt].rearrange("p n t (i r) -> p (n t i) r", r=MM),
-                        a1f[:, n0 : n0 + cnt].rearrange("p n t (i k) -> p (n t i) k", k=M),
-                        cnt * PACK * M,
+                        xs[:, n0 + h : n0 + h + 2].rearrange("p n t (i r) -> p (n t i) r", r=MM),
+                        a1f[:, h : h + 2].rearrange("p n t (i k) -> p (n t i) k", k=M),
+                        2 * PACK * M,
                         MM // 2,
                     )
                 )
+            for m0, cnt in V_A0.get(g, ()):
+                jobs.append(a0_job(m0, cnt))
             weave(jobs)
-            with nc.allow_low_precision(reason="float32 sum, rounded once to bfloat16 on the way out"):
-                for nl in range(GN):
-                    nc.vector.tensor_reduce(
-                        out=ab[:, 2, nl].rearrange("p q t -> p t q"),
-                        in_=xg[:, nl].rearrange("p t (q k) -> p t q k", k=M),
-                        axis=AXIS_X,
-                        op=ADD,
-                    )
 
         def casts(g):
-            nc.scalar.copy(out=st["ab"][:, 0], in_=st["a0f"][:].rearrange("p n t q -> p n q t"))
-            nc.scalar.copy(out=st["ab"][:, 1], in_=st["a1f"][:].rearrange("p n t q -> p n q t"))
+            n0 = g * GN
+            ab = one.tile([P, 2, GN, MM, PACK], BF16, name="ab", tag="ab", align_bytes=64)
+            nc.scalar.copy(out=ab[:, 0], in_=a0f[:, n0 : n0 + GN].rearrange("p n t q -> p n q t"))
+            nc.scalar.copy(out=ab[:, 1], in_=st["a1f"][:].rearrange("p n t q -> p n q t"))
+            st["ab"] = ab
 
         def vsums(g):
-            a0f, a1f = st["a0f"], st["a1f"]
+            a1f = st["a1f"]
             n0 = g * GN
+            a0g = a0f[:, n0 : n0 + GN]
             z1 = one.tile([P, GN, PACK, MM // 2], F32, name="z1", tag="z1")
             z2 = one.tile([P, GN, PACK, MM // 4], F32, name="z2", tag="z2")
-            nc.vector.tensor_tensor(out=z1[:], in0=a0f[:, :, :, 0:32], in1=a0f[:, :, :, 32:64], op=ADD)
-            with nc.allow_low_precision(reason="float32 sum, rounded once to bfloat16 on the way out"):
+            nc.vector.tensor_tensor(out=z1[:], in0=a0g[:, :, :, 0:32], in1=a0g[:, :, :, 32:64], op=ADD)
+            with nc.allow_low_precision(reason=low):
                 nc.vector.tensor_reduce(
                     out=vb[:, 1, n0 : n0 + GN].rearrange("p n j t -> p n t j"),
-                    in_=a0f[:].rearrange("p n t (j k) -> p n t j k", k=M),
+                    in_=a0g.rearrange("p n t (j k) -> p n t j k", k=M),
                     axis=AXIS_X,
                     op=ADD,
                 )
             nc.vector.tensor_tensor(out=z2[:], in0=z1[:, :, :, 0:16], in1=z1[:, :, :, 16:32], op=ADD)
-            with nc.allow_low_precision(reason="float32 sum, rounded once to bfloat16 on the way out"):
+            with nc.allow_low_precision(reason=low):
                 nc.vector.tensor_reduce(
                     out=vb[:, 2, n0 : n0 + GN].rearrange("p n i t -> p n t i"),
                     in_=a1f[:].rearrange("p n t (i k) -> p n t i k", k=M),
@@ -218,8 +209,9 @@ def tile_seteq3to3_kernel(tc, x, coefs, bias, out):
 
         def quant(g):
             xg, ab = st["xg"], st["ab"]
-            xq = two.tile([P, M, GC], U32, name="xq", tag="xq", align_bytes=64)
-            xsc = two.tile([P, M, GC], U8, name="xsc", tag="xsc", align_bytes=64)
+            n0 = g * GN
+            xq = one.tile([P, M, GC], U32, name="xq", tag="xq", align_bytes=64)
+            xsc = one.tile([P, M, GC], U8, name="xsc", tag="xsc", align_bytes=64)
             aq = two.tile([P, 3, GC], U32, name="aq", tag="aq", align_bytes=64)
             asc = two.tile([P, 3, GC], U8, name="asc", tag="asc", align_bytes=64)
             vq = two.tile([P, 3, NBATCH * M], U32, name="vq", tag="vq", align_bytes=64)
@@ -230,7 +222,12 @@ def tile_seteq3to3_kernel(tc, x, coefs, bias, out):
                     scales=xsc[:, 2 * b : 2 * b + 2].rearrange("p i c -> p (i c)"),
                     in_=xg[:, 2 * b : 2 * b + 2].rearrange("p i n q t -> p (i n q t)"),
                 )
-            for a in (2, 0, 1):
+            nc.vector.quantize_mx(
+                out=aq[:, 2].bitcast(FP8X4),
+                scales=asc[:, 2],
+                in_=ab2[:, n0 : n0 + GN].rearrange("p n q t -> p (n q t)"),
+            )
+            for a in range(2):
                 nc.vector.quantize_mx(
                     out=aq[:, a].bitcast(FP8X4), scales=asc[:, a], in_=ab[:, a].rearrange("p n q t -> p (n q t)")
                 )
@@ -240,7 +237,7 @@ def tile_seteq3to3_kernel(tc, x, coefs, bias, out):
                 )
             st["q"] = (xq, xsc, aq, asc, vq, vsc)
 
-        def pe(g):
+        def pe_small(g):
             xq, xsc, aq, asc, vq, vsc = st["q"]
             pp = ps_s.tile([P, 2, GC], F32, name="pp", tag="pp")
             for t in range(2):
@@ -250,22 +247,24 @@ def tile_seteq3to3_kernel(tc, x, coefs, bias, out):
             for t in range(3):
                 for a in range(3):
                     mx(pq[:, t, :], 10 + 3 * a + t, vq[:, a], vsc[:, a], a == 0, a == 2)
-            banks = []
-            for b in range(M // 2):
-                tb = ps_t.tile([P, 2, GC], F32, name="tb", tag="tb")
-                for h in range(2):
-                    mx(tb[:, h, :], 0, xq[:, 2 * b + h], xsc[:, 2 * b + h], True, False)
-                    for a in range(3):
-                        mx(tb[:, h, :], 1 + 3 * a, aq[:, a], asc[:, a], False, a == 2)
-                banks.append(tb)
-            st["ps%d" % g] = (pp, pq, banks)
-
-        def small(g):
-            pp, pq, banks = st["ps%d" % g]
+            st["pp"], st["pq"] = pp, pq
             cols = slice(g * GN * M, (g + 1) * GN * M)
             qs = two.tile([P, 3, GN * M], F32, name="qs", tag="qs")
             nc.scalar.copy(out=qs[:, 0:2, :], in_=pq[:, 0:2, cols])
             nc.scalar.activation(out=qs[:, 2, :], in_=pq[:, 2, cols], func=IDENTITY, bias=bias_f[:, 0:1], scale=1.0)
+            st["qs"] = qs
+
+        def pe_bank(g, b):
+            xq, xsc, aq, asc, vq, vsc = st["q"]
+            tb = ps_t.tile([P, 2, GC], F32, name="tb", tag="tb")
+            for h in range(2):
+                mx(tb[:, h, :], 0, xq[:, 2 * b + h], xsc[:, 2 * b + h], True, False)
+                for a in range(3):
+                    mx(tb[:, h, :], 1 + 3 * a, aq[:, a], asc[:, a], False, a == 2)
+            st["tb%d_%d" % (g, b)] = tb
+
+        def small(g):
+            pp, qs = st["pp"], st["qs"]
             b2 = two.tile([P, M, GN, M], F32, name="b2", tag="b2")
             b3 = two.tile([P, M, GN, M], F32, name="b3", tag="b3")
             b2v = b2[:].rearrange("p i n k -> p n i k")
@@ -287,54 +286,58 @@ def tile_seteq3to3_kernel(tc, x, coefs, bias, out):
                 in1=qs[:, 2, :].rearrange("p (n k) -> p n k", k=M).unsqueeze(2).to_broadcast([P, GN, M, M]),
                 op=ADD,
             )
-            st["b%d" % g] = (b2, b3)
+            st["b2"], st["b3"] = b2, b3
 
-        def tadd(g):
-            pp, pq, banks = st["ps%d" % g]
-            b2, b3 = st["b%d" % g]
-            r = two.tile([P, M, GN, MM], F32, name="r", tag="r")
-            for b in range(M // 2):
-                nc.vector.tensor_tensor(
-                    out=r[:, 2 * b : 2 * b + 2].rearrange("p i n (j k) -> p (i n j) k", k=M),
-                    in0=banks[b][:].rearrange("p h (m k) -> p (h m) k", k=M),
-                    in1=b3[:, 2 * b : 2 * b + 2]
-                    .rearrange("p i n j -> p (i n j)")
-                    .unsqueeze(2)
-                    .to_broadcast([P, 2 * GN * M, M]),
-                    op=ADD,
-                )
-            st["r%d" % g] = r
-
-        def finish(g):
-            b2, b3 = st["b%d" % g]
-            r = st["r%d" % g]
-            rv = r[:].rearrange("p i n (j k) -> p (i n) j k", k=M)
-            engines[B2_ENGINE].tensor_tensor(
-                out=rv,
-                in0=rv,
-                in1=b2[:].rearrange("p i n k -> p (i n) k").unsqueeze(2).to_broadcast([P, M * GN, M, M]),
+        def tadd(g, b):
+            if b == 0:
+                st["r"] = one.tile([P, M, GN, MM], F32, name="r", tag="slot%d" % (g % 2), align_bytes=64)
+            nc.vector.tensor_tensor(
+                out=st["r"][:, 2 * b : 2 * b + 2].rearrange("p i n (j k) -> p (i n j) k", k=M),
+                in0=st["tb%d_%d" % (g, b)][:].rearrange("p h (m k) -> p (h m) k", k=M),
+                in1=st["b3"][:, 2 * b : 2 * b + 2]
+                .rearrange("p i n j -> p (i n j)")
+                .unsqueeze(2)
+                .to_broadcast([P, 2 * GN * M, M]),
                 op=ADD,
             )
-            for nl in range(GN):
-                nc.sync.dma_start(out=out[g * GN + nl].rearrange("s i j k -> s i (j k)"), in_=r[:, :, nl, :])
+
+        def finish(g):
+            r, b2 = st["r"], st["b2"]
+            hm = M // 2
+            for h in range(2):
+                rv = r[:, h * hm : (h + 1) * hm].rearrange("p i n (j k) -> p (i n) j k", k=M)
+                nc.vector.tensor_tensor(
+                    out=rv,
+                    in0=rv,
+                    in1=b2[:, h * hm : (h + 1) * hm]
+                    .rearrange("p i n k -> p (i n) k")
+                    .unsqueeze(2)
+                    .to_broadcast([P, hm * GN, M, M]),
+                    op=ADD,
+                )
+                for nl in range(GN):
+                    nc.sync.dma_start(
+                        out=out[g * GN + nl, :, h * hm : (h + 1) * hm].rearrange("s i j k -> s i (j k)"),
+                        in_=r[:, h * hm : (h + 1) * hm, nl, :],
+                    )
 
         for g in range(NG):
-            if g + 3 < NG + 1 and g > 0:
-                load_x(g + 2)
-            regroup(g)
-            if g == 0:
-                for b0, b1 in COEF_CHUNKS:
-                    coef_chunk(b0, b1)
-            sums(g)
+            trees(g)
+            casts(g)
             if g > 0:
                 small(g - 1)
-                tadd(g - 1)
-            casts(g)
             vsums(g)
             quant(g)
-            pe(g)
+            pe_small(g)
+            if g + 1 < NG:
+                regroup(g + 1)
+            for b in range(M // 2):
+                pe_bank(g, b)
+                if g > 0:
+                    tadd(g - 1, b)
             if g > 0:
                 finish(g - 1)
         small(NG - 1)
-        tadd(NG - 1)
+        for b in range(M // 2):
+            tadd(NG - 1, b)
         finish(NG - 1)

@@ -26,9 +26,13 @@ GN = 4
 NG = NBATCH // GN
 GC = GN * MM
 COEF_CHUNKS = ((0, 8), (8, 16), (16, 18), (18, 19))
-G_A0 = ((0, 2), (2, 2), (4, 2), (6, 2))
+G_FIRST = ((0, 8), (8, 8), (16, 8))
+G_LATER = {0: (24, 6), 1: (44, 7), 2: (51, 7)}
+V_A0 = {1: (30, 2), 3: (58, 6)}
 PE_A0 = (8, 9, 10)
-V_A0 = {2: ((11, 1),), 3: ((12, 2), (14, 2))}
+A2_FIRST = 12
+A2_LATER = {0: (12, 13), 1: (14,), 2: (15,)}
+I32 = mybir.dt.int32
 COEF_AFTER = 6
 PIN = True
 
@@ -60,8 +64,10 @@ def tile_seteq3to3_kernel(tc, x, coefs, bias, out):
                     nc.sync.dma_start(out=bias_bf[:], in_=bias.rearrange("a s b c d -> s (a b c d)"))
             nc.sync.dma_start(out=xs[:, n], in_=x[n].rearrange("(p t) i j k -> p t (i j k)", t=PACK))
 
-        vb = keep.tile([P, 3, NBATCH, M, PACK], BF16, name="vb", tag="vb", align_bytes=64)
-        nc.vector.memset(vb[:], 0.0)
+        vq = keep.tile([P, 3, P], U32, name="vq", tag="vq", align_bytes=64)
+        vsc = keep.tile([P, 3, P], U8, name="vsc", tag="vsc", align_bytes=64)
+        nc.vector.memset(vq[:].bitcast(I32), 0)
+        nc.vector.memset(vsc[:].bitcast(I32), 0)
 
         cq = keep.tile([P, NB, DO], U32, name="cq", tag="cq", align_bytes=64)
         csc = keep.tile([P, NB, DO], U8, name="csc", tag="csc", align_bytes=64)
@@ -87,11 +93,10 @@ def tile_seteq3to3_kernel(tc, x, coefs, bias, out):
                 nc.scalar.copy(out=xg[:, :, nl], in_=xs[:, g * GN + nl].rearrange("p t (i q) -> p i q t", i=M))
             st["xg"] = xg
 
-        def tree(who, lane, src, dst, rows, half):
+        def tree(who, tag1, tag2, src, dst, rows, half):
             eng = engines[who]
-            tag = who + str(lane)
-            y1 = one.tile([P, 2048], F32, name="y1" + tag, tag="y1" + tag)
-            y2 = one.tile([P, 1024], F32, name="y2" + tag, tag="y2" + tag)
+            y1 = one.tile([P, rows * half], F32, name="y1" + who, tag=tag1)
+            y2 = one.tile([P, rows * half // 2], F32, name="y2" + who, tag=tag2)
             v1 = y1[:, 0 : rows * half].rearrange("p (r c) -> p r c", c=half)
             v2 = y2[:, 0 : rows * half // 2].rearrange("p (r c) -> p r c", c=half // 2)
             return (
@@ -102,29 +107,40 @@ def tile_seteq3to3_kernel(tc, x, coefs, bias, out):
                 ),
             )
 
-        def a0_job(n0, cnt):
+        def a0_job(row0, rows):
             return (
-                xs[:, n0 : n0 + cnt].rearrange("p n t w -> p (n t) w"),
-                a0f[:, n0 : n0 + cnt].rearrange("p n t q -> p (n t) q"),
-                cnt * PACK,
+                xs[:].rearrange("p n t w -> p (n t) w")[:, row0 : row0 + rows],
+                a0f[:].rearrange("p n t q -> p (n t) q")[:, row0 : row0 + rows],
+                rows,
                 W // 2,
             )
 
+        def g_tree(row0, rows):
+            j = a0_job(row0, rows)
+            for call in tree("g", "y2lane1", "y1lane1", j[0], j[1], j[2], j[3]):
+                call()
+
         def weave(jobs):
-            for k in range(0, len(jobs), 2):
-                pair = [tree("v", lane, j[0], j[1], j[2], j[3]) for lane, j in enumerate(jobs[k : k + 2])]
-                for level in range(3):
-                    for t3 in pair:
-                        t3[level]()
+            calls = [tree("v", "y1lane%d" % j[0], "y2lane%d" % j[0], j[1], j[2], j[3], j[4]) for j in jobs]
+            for level in range(3):
+                for t3 in calls:
+                    t3[level]()
+
+        def a2(n):
+            with nc.allow_low_precision(reason=low):
+                nc.vector.tensor_reduce(
+                    out=ab2[:, n].rearrange("p q t -> p t q"),
+                    in_=xs[:, n].rearrange("p t (q k) -> p t q k", k=M),
+                    axis=AXIS_X,
+                    op=ADD,
+                )
 
         regroup(0)
         cg = one.tile([P, NB, DO, PACK], BF16, name="cg", tag="slot1", align_bytes=64)
         for b0, b1 in COEF_CHUNKS:
             nc.scalar.copy(out=cg[:, b0:b1], in_=cs[:, :, :, b0:b1].rearrange("p t s b -> p b s t"))
-        for n0, cnt in G_A0:
-            j = a0_job(n0, cnt)
-            for call in tree("g", 0, j[0], j[1], j[2], j[3]):
-                call()
+        for row0, rows in G_FIRST:
+            g_tree(row0, rows)
         for n in PE_A0:
             acc = ps_t.tile([P, PACK, MM], F32, name="pe_sum", tag="tb")
             for i in range(M):
@@ -136,14 +152,8 @@ def tile_seteq3to3_kernel(tc, x, coefs, bias, out):
                     stop=(i == M - 1),
                 )
             nc.scalar.copy(out=a0f[:, n], in_=acc[:])
-        with nc.allow_low_precision(reason=low):
-            for n in range(NBATCH):
-                nc.vector.tensor_reduce(
-                    out=ab2[:, n].rearrange("p q t -> p t q"),
-                    in_=xs[:, n].rearrange("p t (q k) -> p t q k", k=M),
-                    axis=AXIS_X,
-                    op=ADD,
-                )
+        for n in range(A2_FIRST):
+            a2(n)
 
         nc.vector.tensor_copy(out=bias_f[:], in_=bias_bf[:])
         for b0, b1 in COEF_CHUNKS:
@@ -158,17 +168,18 @@ def tile_seteq3to3_kernel(tc, x, coefs, bias, out):
             a1f = one.tile([P, GN, PACK, MM], F32, name="a1f", tag="a1f")
             st["a1f"] = a1f
             jobs = []
+            if g in V_A0:
+                jobs.append((2,) + a0_job(V_A0[g][0], V_A0[g][1]))
             for h in range(0, GN, 2):
                 jobs.append(
                     (
+                        h // 2,
                         xs[:, n0 + h : n0 + h + 2].rearrange("p n t (i r) -> p (n t i) r", r=MM),
                         a1f[:, h : h + 2].rearrange("p n t (i k) -> p (n t i) k", k=M),
                         2 * PACK * M,
                         MM // 2,
                     )
                 )
-            for m0, cnt in V_A0.get(g, ()):
-                jobs.append(a0_job(m0, cnt))
             weave(jobs)
 
         def casts(g):
@@ -178,50 +189,59 @@ def tile_seteq3to3_kernel(tc, x, coefs, bias, out):
             nc.scalar.copy(out=ab[:, 1], in_=st["a1f"][:].rearrange("p n t q -> p n q t"))
             st["ab"] = ab
 
-        def vsums(g):
-            a1f = st["a1f"]
+        def vred(g):
+            n0 = g * GN
+            vb = two.tile([P, 3, GN, M, PACK], BF16, name="vb", tag="vb", align_bytes=64)
+            st["vb"] = vb
+            with nc.allow_low_precision(reason=low):
+                nc.vector.tensor_reduce(
+                    out=vb[:, 1].rearrange("p n j t -> p n t j"),
+                    in_=a0f[:, n0 : n0 + GN].rearrange("p n t (j k) -> p n t j k", k=M),
+                    axis=AXIS_X,
+                    op=ADD,
+                )
+                nc.vector.tensor_reduce(
+                    out=vb[:, 2].rearrange("p n i t -> p n t i"),
+                    in_=st["a1f"][:].rearrange("p n t (i k) -> p n t i k", k=M),
+                    axis=AXIS_X,
+                    op=ADD,
+                )
+
+        def ztree(g):
             n0 = g * GN
             a0g = a0f[:, n0 : n0 + GN]
+            vb = st["vb"]
             z1 = one.tile([P, GN, PACK, MM // 2], F32, name="z1", tag="z1")
             z2 = one.tile([P, GN, PACK, MM // 4], F32, name="z2", tag="z2")
-            nc.vector.tensor_tensor(out=z1[:], in0=a0g[:, :, :, 0:32], in1=a0g[:, :, :, 32:64], op=ADD)
-            with nc.allow_low_precision(reason=low):
-                nc.vector.tensor_reduce(
-                    out=vb[:, 1, n0 : n0 + GN].rearrange("p n j t -> p n t j"),
-                    in_=a0g.rearrange("p n t (j k) -> p n t j k", k=M),
-                    axis=AXIS_X,
-                    op=ADD,
-                )
-            nc.vector.tensor_tensor(out=z2[:], in0=z1[:, :, :, 0:16], in1=z1[:, :, :, 16:32], op=ADD)
-            with nc.allow_low_precision(reason=low):
-                nc.vector.tensor_reduce(
-                    out=vb[:, 2, n0 : n0 + GN].rearrange("p n i t -> p n t i"),
-                    in_=a1f[:].rearrange("p n t (i k) -> p n t i k", k=M),
-                    axis=AXIS_X,
-                    op=ADD,
-                )
-            nc.vector.tensor_tensor(
-                out=vb[:, 0, n0 : n0 + GN].rearrange("p n k t -> p n t k"),
-                in0=z2[:, :, :, 0:8],
-                in1=z2[:, :, :, 8:16],
-                op=ADD,
-            )
+            return [
+                lambda: nc.vector.tensor_tensor(out=z1[:], in0=a0g[:, :, :, 0:32], in1=a0g[:, :, :, 32:64], op=ADD),
+                lambda: nc.vector.tensor_tensor(out=z2[:], in0=z1[:, :, :, 0:16], in1=z1[:, :, :, 16:32], op=ADD),
+                lambda: nc.vector.tensor_tensor(
+                    out=vb[:, 0].rearrange("p n k t -> p n t k"), in0=z2[:, :, :, 0:8], in1=z2[:, :, :, 8:16], op=ADD
+                ),
+            ]
 
-        def quant(g):
-            xg, ab = st["xg"], st["ab"]
-            n0 = g * GN
+        def quant_x(g):
+            xg = st["xg"]
             xq = one.tile([P, M, GC], U32, name="xq", tag="xq", align_bytes=64)
             xsc = one.tile([P, M, GC], U8, name="xsc", tag="xsc", align_bytes=64)
-            aq = two.tile([P, 3, GC], U32, name="aq", tag="aq", align_bytes=64)
-            asc = two.tile([P, 3, GC], U8, name="asc", tag="asc", align_bytes=64)
-            vq = two.tile([P, 3, NBATCH * M], U32, name="vq", tag="vq", align_bytes=64)
-            vsc = two.tile([P, 3, NBATCH * M], U8, name="vsc", tag="vsc", align_bytes=64)
-            for b in range(M // 2):
-                nc.vector.quantize_mx(
+            st["xq"] = (xq, xsc)
+
+            def call(b):
+                return lambda: nc.vector.quantize_mx(
                     out=xq[:, 2 * b : 2 * b + 2].rearrange("p i c -> p (i c)").bitcast(FP8X4),
                     scales=xsc[:, 2 * b : 2 * b + 2].rearrange("p i c -> p (i c)"),
                     in_=xg[:, 2 * b : 2 * b + 2].rearrange("p i n q t -> p (i n q t)"),
                 )
+
+            return [call(b) for b in range(M // 2)]
+
+        def quant_av(g):
+            ab, vb = st["ab"], st["vb"]
+            n0 = g * GN
+            xq, xsc = st["xq"]
+            aq = two.tile([P, 3, GC], U32, name="aq", tag="aq", align_bytes=64)
+            asc = two.tile([P, 3, GC], U8, name="asc", tag="asc", align_bytes=64)
             nc.vector.quantize_mx(
                 out=aq[:, 2].bitcast(FP8X4),
                 scales=asc[:, 2],
@@ -233,7 +253,9 @@ def tile_seteq3to3_kernel(tc, x, coefs, bias, out):
                 )
             for a in range(3):
                 nc.vector.quantize_mx(
-                    out=vq[:, a].bitcast(FP8X4), scales=vsc[:, a], in_=vb[:, a].rearrange("p n m t -> p (n m t)")
+                    out=vq[:, a, 0 : GN * M].bitcast(FP8X4),
+                    scales=vsc[:, a, 0 : GN * M],
+                    in_=vb[:, a].rearrange("p n m t -> p (n m t)"),
                 )
             st["q"] = (xq, xsc, aq, asc, vq, vsc)
 
@@ -243,12 +265,12 @@ def tile_seteq3to3_kernel(tc, x, coefs, bias, out):
             for t in range(2):
                 for a in range(3):
                     mx(pp[:, t, :], 2 + 3 * a + t, aq[:, a], asc[:, a], a == 0, a == 2)
-            pq = ps_s.tile([P, 3, NBATCH * M], F32, name="pq", tag="pq")
+            pq = ps_s.tile([P, 3, P], F32, name="pq", tag="pq")
             for t in range(3):
                 for a in range(3):
                     mx(pq[:, t, :], 10 + 3 * a + t, vq[:, a], vsc[:, a], a == 0, a == 2)
             st["pp"], st["pq"] = pp, pq
-            cols = slice(g * GN * M, (g + 1) * GN * M)
+            cols = slice(0, GN * M)
             qs = two.tile([P, 3, GN * M], F32, name="qs", tag="qs")
             nc.scalar.copy(out=qs[:, 0:2, :], in_=pq[:, 0:2, cols])
             nc.scalar.activation(out=qs[:, 2, :], in_=pq[:, 2, cols], func=IDENTITY, bias=bias_f[:, 0:1], scale=1.0)
@@ -280,13 +302,13 @@ def tile_seteq3to3_kernel(tc, x, coefs, bias, out):
                 in1=qs[:, 1, :].rearrange("p (n j) -> p n j", j=M).unsqueeze(2).to_broadcast([P, GN, M, M]),
                 op=ADD,
             )
-            nc.vector.tensor_tensor(
+            st["b2"], st["b3"] = b2, b3
+            return lambda: nc.vector.tensor_tensor(
                 out=b2v,
                 in0=b2v,
                 in1=qs[:, 2, :].rearrange("p (n k) -> p n k", k=M).unsqueeze(2).to_broadcast([P, GN, M, M]),
                 op=ADD,
             )
-            st["b2"], st["b3"] = b2, b3
 
         def tadd(g, b):
             if b == 0:
@@ -304,7 +326,8 @@ def tile_seteq3to3_kernel(tc, x, coefs, bias, out):
         def finish(g):
             r, b2 = st["r"], st["b2"]
             hm = M // 2
-            for h in range(2):
+
+            def half(h):
                 rv = r[:, h * hm : (h + 1) * hm].rearrange("p i n (j k) -> p (i n) j k", k=M)
                 nc.vector.tensor_tensor(
                     out=rv,
@@ -321,23 +344,43 @@ def tile_seteq3to3_kernel(tc, x, coefs, bias, out):
                         in_=r[:, h * hm : (h + 1) * hm, nl, :],
                     )
 
+            return [lambda: half(0), lambda: half(1)]
+
         for g in range(NG):
+            last = g == NG - 1
             trees(g)
             casts(g)
+            if g in G_LATER:
+                g_tree(G_LATER[g][0], G_LATER[g][1])
+            fill = []
             if g > 0:
-                small(g - 1)
-            vsums(g)
-            quant(g)
+                fill.append(small(g - 1))
+                if not last:
+                    for b in range(M // 2):
+                        tadd(g - 1, b)
+                    fill.extend(finish(g - 1))
+            vred(g)
+            for n in A2_LATER.get(g, ()):
+                a2(n)
+            fill.extend(quant_x(g))
+            for k, z in enumerate(ztree(g)):
+                z()
+                fill[k]()
+            for f in fill[3:]:
+                f()
+            quant_av(g)
             pe_small(g)
-            if g + 1 < NG:
+            if not last:
                 regroup(g + 1)
             for b in range(M // 2):
                 pe_bank(g, b)
-                if g > 0:
+                if last:
                     tadd(g - 1, b)
-            if g > 0:
-                finish(g - 1)
-        small(NG - 1)
+            if last:
+                for f in finish(g - 1):
+                    f()
+        small(NG - 1)()
         for b in range(M // 2):
             tadd(NG - 1, b)
-        finish(NG - 1)
+        for f in finish(NG - 1):
+            f()

@@ -7,6 +7,7 @@ FLOPS = 2 * 512 * 128 * (16 * 512 + 9 * 16 * 64 + 9 * 16 * 8)
 
 BF16 = mybir.dt.bfloat16
 F32 = mybir.dt.float32
+I32 = mybir.dt.int32
 U32 = mybir.dt.uint32
 U8 = mybir.dt.uint8
 FP8X4 = mybir.dt.float8_e4m3fn_x4
@@ -26,15 +27,15 @@ GN = 4
 NG = NBATCH // GN
 GC = GN * MM
 COEF_CHUNKS = ((0, 8), (8, 16), (16, 18), (18, 19))
-G_FIRST = ((0, 8), (8, 8), (16, 8))
-G_LATER = {0: (24, 6), 1: (44, 7), 2: (51, 7)}
-V_A0 = {1: (30, 2), 3: (58, 6)}
-PE_A0 = (8, 9, 10)
-A2_FIRST = 12
-A2_LATER = {0: (12, 13), 1: (14,), 2: (15,)}
-I32 = mybir.dt.int32
 COEF_AFTER = 6
-PIN = True
+G_JOBS = (
+    ((0, 0, 2), (0, 2, 2)),
+    ((0, 4, 2), (0, 6, 2)),
+    ((0, 11, 1), (1, 11, 1)),
+    ((0, 12, 2), (0, 14, 2), (1, 12, 2), (1, 14, 1)),
+)
+V_A1 = (((0, 2), (2, 2)), ((4, 2), (6, 2)), ((8, 2), (10, 1)), ((15, 1),))
+PE_A0 = (8, 9, 10)
 
 
 def tile_seteq3to3_kernel(tc, x, coefs, bias, out):
@@ -45,15 +46,15 @@ def tile_seteq3to3_kernel(tc, x, coefs, bias, out):
         two = ctx.enter_context(tc.tile_pool(name="two", bufs=2))
         ps_t = ctx.enter_context(tc.psum_pool(name="ps_t", bufs=6))
         ps_s = ctx.enter_context(tc.psum_pool(name="ps_s", bufs=1))
-        engines = {"v": nc.vector, "g": nc.gpsimd}
         low = "float32 sum, rounded once to bfloat16 on the way out"
 
         ident = keep.tile([P, P], BF16, name="ident", tag="ident")
         make_identity(nc, ident[:])
-        if PIN:
-            ctx.enter_context(tc.manual_schedule())
+        ctx.enter_context(tc.manual_schedule())
 
-        xs = keep.tile([P, NBATCH, PACK, W], BF16, name="xs", tag="xs")
+        xs = [
+            one.tile([P, GN, PACK, W], BF16, name="xs%d" % g, tag="xs%d" % g, align_bytes=64) for g in range(NG)
+        ]
         cs = one.tile([P, PACK, DO, NB], BF16, name="cs", tag="slot0", align_bytes=64)
         bias_bf = keep.tile([P, 1], BF16, name="bias_bf", tag="bias_bf")
         bias_f = keep.tile([P, 1], F32, name="bias_f", tag="bias_f")
@@ -62,7 +63,9 @@ def tile_seteq3to3_kernel(tc, x, coefs, bias, out):
                 nc.sync.dma_start(out=cs[:], in_=coefs.rearrange("(p t) s b -> p t s b", t=PACK))
                 with nc.allow_non_contiguous_dma(reason="128 bias values, one to a partition"):
                     nc.sync.dma_start(out=bias_bf[:], in_=bias.rearrange("a s b c d -> s (a b c d)"))
-            nc.sync.dma_start(out=xs[:, n], in_=x[n].rearrange("(p t) i j k -> p t (i j k)", t=PACK))
+            nc.sync.dma_start(
+                out=xs[n // GN][:, n % GN], in_=x[n].rearrange("(p t) i j k -> p t (i j k)", t=PACK)
+            )
 
         vq = keep.tile([P, 3, P], U32, name="vq", tag="vq", align_bytes=64)
         vsc = keep.tile([P, 3, P], U8, name="vsc", tag="vsc", align_bytes=64)
@@ -71,8 +74,9 @@ def tile_seteq3to3_kernel(tc, x, coefs, bias, out):
 
         cq = keep.tile([P, NB, DO], U32, name="cq", tag="cq", align_bytes=64)
         csc = keep.tile([P, NB, DO], U8, name="csc", tag="csc", align_bytes=64)
-        a0f = keep.tile([P, NBATCH, PACK, MM], F32, name="a0f", tag="a0f")
-        ab2 = keep.tile([P, NBATCH, MM, PACK], BF16, name="ab2", tag="ab2", align_bytes=64)
+        af = keep.tile([P, 2, NBATCH, PACK, MM], F32, name="af", tag="af")
+        ab = keep.tile([P, 3, NBATCH, MM, PACK], BF16, name="ab", tag="ab", align_bytes=64)
+        vb = keep.tile([P, NG, 3, GN, M, PACK], BF16, name="vb", tag="vb", align_bytes=64)
 
         def mx(acc, b, rhs, rhs_scale, start, stop):
             nc.tensor.matmul_mx(
@@ -86,74 +90,125 @@ def tile_seteq3to3_kernel(tc, x, coefs, bias, out):
             )
 
         st = {}
+        xgs = {}
 
         def regroup(g):
-            xg = one.tile([P, M, GN, MM, PACK], BF16, name="xg", tag="xg", align_bytes=64)
+            tag = "xg0" if g == 0 else "xs%d" % (g - 1)
+            xg = one.tile([P, M, GN, MM, PACK], BF16, name="xg", tag=tag, align_bytes=64)
             for nl in range(GN):
-                nc.scalar.copy(out=xg[:, :, nl], in_=xs[:, g * GN + nl].rearrange("p t (i q) -> p i q t", i=M))
-            st["xg"] = xg
+                nc.scalar.copy(out=xg[:, :, nl], in_=xs[g][:, nl].rearrange("p t (i q) -> p i q t", i=M))
+            xgs[g] = xg
 
-        def tree(who, tag1, tag2, src, dst, rows, half):
-            eng = engines[who]
-            y1 = one.tile([P, rows * half], F32, name="y1" + who, tag=tag1)
-            y2 = one.tile([P, rows * half // 2], F32, name="y2" + who, tag=tag2)
+        def g_tree(a, n0, cnt):
+            xv = xs[n0 // GN][:, n0 % GN : n0 % GN + cnt]
+            if a == 0:
+                src, rows, half = xv.rearrange("p n t w -> p (n t) w"), cnt * PACK, W // 2
+                dst = af[:, 0, n0 : n0 + cnt].rearrange("p n t q -> p (n t) q")
+            else:
+                src, rows, half = xv.rearrange("p n t (i r) -> p (n t i) r", r=MM), cnt * PACK * M, MM // 2
+                dst = af[:, 1, n0 : n0 + cnt].rearrange("p n t (i k) -> p (n t i) k", k=M)
+            y1 = one.tile([P, 2048], F32, name="y1g", tag="y1g", align_bytes=64)
+            y2 = one.tile([P, 1024], F32, name="y2g", tag="y2g", align_bytes=64)
             v1 = y1[:, 0 : rows * half].rearrange("p (r c) -> p r c", c=half)
             v2 = y2[:, 0 : rows * half // 2].rearrange("p (r c) -> p r c", c=half // 2)
-            return (
-                lambda: eng.tensor_tensor(out=v1, in0=src[:, :, 0:half], in1=src[:, :, half : 2 * half], op=ADD),
-                lambda: eng.tensor_tensor(out=v2, in0=v1[:, :, 0 : half // 2], in1=v1[:, :, half // 2 : half], op=ADD),
-                lambda: eng.tensor_tensor(
-                    out=dst, in0=v2[:, :, 0 : half // 4], in1=v2[:, :, half // 4 : half // 2], op=ADD
-                ),
-            )
-
-        def a0_job(row0, rows):
-            return (
-                xs[:].rearrange("p n t w -> p (n t) w")[:, row0 : row0 + rows],
-                a0f[:].rearrange("p n t q -> p (n t) q")[:, row0 : row0 + rows],
-                rows,
-                W // 2,
-            )
-
-        def g_tree(row0, rows):
-            j = a0_job(row0, rows)
-            for call in tree("g", "y2lane1", "y1lane1", j[0], j[1], j[2], j[3]):
-                call()
-
-        def weave(jobs):
-            calls = [tree("v", "y1lane%d" % j[0], "y2lane%d" % j[0], j[1], j[2], j[3], j[4]) for j in jobs]
-            for level in range(3):
-                for t3 in calls:
-                    t3[level]()
+            nc.gpsimd.tensor_tensor(out=v1, in0=src[:, :, 0:half], in1=src[:, :, half : 2 * half], op=ADD)
+            nc.gpsimd.tensor_tensor(out=v2, in0=v1[:, :, 0 : half // 2], in1=v1[:, :, half // 2 : half], op=ADD)
+            nc.gpsimd.tensor_tensor(out=dst, in0=v2[:, :, 0 : half // 4], in1=v2[:, :, half // 4 : half // 2], op=ADD)
 
         def a2(n):
             with nc.allow_low_precision(reason=low):
                 nc.vector.tensor_reduce(
-                    out=ab2[:, n].rearrange("p q t -> p t q"),
-                    in_=xs[:, n].rearrange("p t (q k) -> p t q k", k=M),
+                    out=ab[:, 2, n].rearrange("p q t -> p t q"),
+                    in_=xs[n // GN][:, n % GN].rearrange("p t (q k) -> p t q k", k=M),
                     axis=AXIS_X,
                     op=ADD,
                 )
+
+        def v_a1(segments):
+            halves = []
+            for lane, (n0, cnt) in enumerate(segments):
+                y = one.tile([P, 2 * GC * PACK // 2], F32, name="yv%d" % lane, tag="yv%d" % lane)
+                yv = y[:, 0 : cnt * 512]
+                nc.vector.tensor_reduce(
+                    out=yv.rearrange("p (r k) -> p r k", k=M),
+                    in_=xs[n0 // GN][:, n0 % GN : n0 % GN + cnt].rearrange(
+                        "p n t (i h j k) -> p (n t i h) k j", h=2, j=4, k=M
+                    ),
+                    axis=AXIS_X,
+                    op=ADD,
+                )
+                halves.append((yv, n0, cnt))
+            for yv, n0, cnt in halves:
+                nc.vector.tensor_reduce(
+                    out=af[:, 1, n0 : n0 + cnt].rearrange("p n t (i k) -> p (n t i) k", k=M),
+                    in_=yv.rearrange("p (r h k) -> p r k h", h=2, k=M),
+                    axis=AXIS_X,
+                    op=ADD,
+                )
+
+        def vsums(g):
+            n0 = g * GN
+            a0g = af[:, 0, n0 : n0 + GN]
+            z = one.tile([P, GN * PACK * 2 * M], F32, name="z", tag="z")
+            nc.vector.tensor_reduce(
+                out=z[:].rearrange("p (r k) -> p r k", k=M),
+                in_=a0g.rearrange("p n t (h j k) -> p (n t h) k j", h=2, j=4, k=M),
+                axis=AXIS_X,
+                op=ADD,
+            )
+            with nc.allow_low_precision(reason=low):
+                nc.vector.tensor_reduce(
+                    out=vb[:, g, 1].rearrange("p n j t -> p n t j"),
+                    in_=a0g.rearrange("p n t (j k) -> p n t j k", k=M),
+                    axis=AXIS_X,
+                    op=ADD,
+                )
+                nc.vector.tensor_reduce(
+                    out=vb[:, g, 2].rearrange("p n i t -> p n t i"),
+                    in_=af[:, 1, n0 : n0 + GN].rearrange("p n t (i k) -> p n t i k", k=M),
+                    axis=AXIS_X,
+                    op=ADD,
+                )
+                nc.vector.tensor_reduce(
+                    out=vb[:, g, 0].rearrange("p n k t -> p n t k"),
+                    in_=z[:].rearrange("p (n t h k) -> p n t k h", t=PACK, h=2, k=M),
+                    axis=AXIS_X,
+                    op=ADD,
+                )
+
+        def casts(g):
+            n0 = g * GN
+            for a in range(2):
+                nc.scalar.copy(out=ab[:, a, n0 : n0 + GN], in_=af[:, a, n0 : n0 + GN].rearrange("p n t q -> p n q t"))
 
         regroup(0)
         cg = one.tile([P, NB, DO, PACK], BF16, name="cg", tag="slot1", align_bytes=64)
         for b0, b1 in COEF_CHUNKS:
             nc.scalar.copy(out=cg[:, b0:b1], in_=cs[:, :, :, b0:b1].rearrange("p t s b -> p b s t"))
-        for row0, rows in G_FIRST:
-            g_tree(row0, rows)
         for n in PE_A0:
             acc = ps_t.tile([P, PACK, MM], F32, name="pe_sum", tag="tb")
             for i in range(M):
                 nc.tensor.matmul(
                     out=acc[:],
                     lhsT=ident[:],
-                    rhs=xs[:, n, :, i * MM : (i + 1) * MM],
+                    rhs=xs[n // GN][:, n % GN, :, i * MM : (i + 1) * MM],
                     start=(i == 0),
                     stop=(i == M - 1),
                 )
-            nc.scalar.copy(out=a0f[:, n], in_=acc[:])
-        for n in range(A2_FIRST):
-            a2(n)
+            nc.scalar.copy(out=af[:, 0, n], in_=acc[:])
+        for g in range(NG):
+            for a, n0, cnt in G_JOBS[g]:
+                g_tree(a, n0, cnt)
+            for n in range(g * GN, (g + 1) * GN):
+                a2(n)
+            v_a1(V_A1[g])
+            if g > 0:
+                vsums(g - 1)
+            if g + 1 < NG:
+                casts(g)
+                regroup(g + 1)
+        casts(NG - 1)
+        vsums(NG - 1)
 
         nc.vector.tensor_copy(out=bias_f[:], in_=bias_bf[:])
         for b0, b1 in COEF_CHUNKS:
@@ -163,104 +218,38 @@ def tile_seteq3to3_kernel(tc, x, coefs, bias, out):
                 in_=cg[:, b0:b1].rearrange("p b s t -> p (b s t)"),
             )
 
-        def trees(g):
-            n0 = g * GN
-            a1f = one.tile([P, GN, PACK, MM], F32, name="a1f", tag="a1f")
-            st["a1f"] = a1f
-            jobs = []
-            if g in V_A0:
-                jobs.append((2,) + a0_job(V_A0[g][0], V_A0[g][1]))
-            for h in range(0, GN, 2):
-                jobs.append(
-                    (
-                        h // 2,
-                        xs[:, n0 + h : n0 + h + 2].rearrange("p n t (i r) -> p (n t i) r", r=MM),
-                        a1f[:, h : h + 2].rearrange("p n t (i k) -> p (n t i) k", k=M),
-                        2 * PACK * M,
-                        MM // 2,
-                    )
-                )
-            weave(jobs)
-
-        def casts(g):
-            n0 = g * GN
-            ab = one.tile([P, 2, GN, MM, PACK], BF16, name="ab", tag="ab", align_bytes=64)
-            nc.scalar.copy(out=ab[:, 0], in_=a0f[:, n0 : n0 + GN].rearrange("p n t q -> p n q t"))
-            nc.scalar.copy(out=ab[:, 1], in_=st["a1f"][:].rearrange("p n t q -> p n q t"))
-            st["ab"] = ab
-
-        def vred(g):
-            n0 = g * GN
-            vb = two.tile([P, 3, GN, M, PACK], BF16, name="vb", tag="vb", align_bytes=64)
-            st["vb"] = vb
-            with nc.allow_low_precision(reason=low):
-                nc.vector.tensor_reduce(
-                    out=vb[:, 1].rearrange("p n j t -> p n t j"),
-                    in_=a0f[:, n0 : n0 + GN].rearrange("p n t (j k) -> p n t j k", k=M),
-                    axis=AXIS_X,
-                    op=ADD,
-                )
-                nc.vector.tensor_reduce(
-                    out=vb[:, 2].rearrange("p n i t -> p n t i"),
-                    in_=st["a1f"][:].rearrange("p n t (i k) -> p n t i k", k=M),
-                    axis=AXIS_X,
-                    op=ADD,
-                )
-
-        def ztree(g):
-            n0 = g * GN
-            a0g = a0f[:, n0 : n0 + GN]
-            vb = st["vb"]
-            z1 = one.tile([P, GN, PACK, MM // 2], F32, name="z1", tag="z1")
-            z2 = one.tile([P, GN, PACK, MM // 4], F32, name="z2", tag="z2")
-            return [
-                lambda: nc.vector.tensor_tensor(out=z1[:], in0=a0g[:, :, :, 0:32], in1=a0g[:, :, :, 32:64], op=ADD),
-                lambda: nc.vector.tensor_tensor(out=z2[:], in0=z1[:, :, :, 0:16], in1=z1[:, :, :, 16:32], op=ADD),
-                lambda: nc.vector.tensor_tensor(
-                    out=vb[:, 0].rearrange("p n k t -> p n t k"), in0=z2[:, :, :, 0:8], in1=z2[:, :, :, 8:16], op=ADD
-                ),
-            ]
-
         def quant_x(g):
-            xg = st["xg"]
-            xq = one.tile([P, M, GC], U32, name="xq", tag="xq", align_bytes=64)
-            xsc = one.tile([P, M, GC], U8, name="xsc", tag="xsc", align_bytes=64)
-            st["xq"] = (xq, xsc)
-
-            def call(b):
-                return lambda: nc.vector.quantize_mx(
+            xg = xgs[g]
+            xq = one.tile([P, M, GC], U32, name="xq", tag="y1g", align_bytes=64)
+            xsc = one.tile([P, M, GC], U8, name="xsc", tag="y2g", align_bytes=64)
+            for b in range(M // 2):
+                nc.vector.quantize_mx(
                     out=xq[:, 2 * b : 2 * b + 2].rearrange("p i c -> p (i c)").bitcast(FP8X4),
                     scales=xsc[:, 2 * b : 2 * b + 2].rearrange("p i c -> p (i c)"),
                     in_=xg[:, 2 * b : 2 * b + 2].rearrange("p i n q t -> p (i n q t)"),
                 )
-
-            return [call(b) for b in range(M // 2)]
+            st["xq"] = (xq, xsc)
 
         def quant_av(g):
-            ab, vb = st["ab"], st["vb"]
             n0 = g * GN
-            xq, xsc = st["xq"]
             aq = two.tile([P, 3, GC], U32, name="aq", tag="aq", align_bytes=64)
             asc = two.tile([P, 3, GC], U8, name="asc", tag="asc", align_bytes=64)
-            nc.vector.quantize_mx(
-                out=aq[:, 2].bitcast(FP8X4),
-                scales=asc[:, 2],
-                in_=ab2[:, n0 : n0 + GN].rearrange("p n q t -> p (n q t)"),
-            )
-            for a in range(2):
+            for a in range(3):
                 nc.vector.quantize_mx(
-                    out=aq[:, a].bitcast(FP8X4), scales=asc[:, a], in_=ab[:, a].rearrange("p n q t -> p (n q t)")
+                    out=aq[:, a].bitcast(FP8X4),
+                    scales=asc[:, a],
+                    in_=ab[:, a, n0 : n0 + GN].rearrange("p n q t -> p (n q t)"),
                 )
             for a in range(3):
                 nc.vector.quantize_mx(
                     out=vq[:, a, 0 : GN * M].bitcast(FP8X4),
                     scales=vsc[:, a, 0 : GN * M],
-                    in_=vb[:, a].rearrange("p n m t -> p (n m t)"),
+                    in_=vb[:, g, a].rearrange("p n m t -> p (n m t)"),
                 )
-            st["q"] = (xq, xsc, aq, asc, vq, vsc)
+            st["aq"] = (aq, asc)
 
         def pe_small(g):
-            xq, xsc, aq, asc, vq, vsc = st["q"]
+            aq, asc = st["aq"]
             pp = ps_s.tile([P, 2, GC], F32, name="pp", tag="pp")
             for t in range(2):
                 for a in range(3):
@@ -269,15 +258,15 @@ def tile_seteq3to3_kernel(tc, x, coefs, bias, out):
             for t in range(3):
                 for a in range(3):
                     mx(pq[:, t, :], 10 + 3 * a + t, vq[:, a], vsc[:, a], a == 0, a == 2)
-            st["pp"], st["pq"] = pp, pq
             cols = slice(0, GN * M)
             qs = two.tile([P, 3, GN * M], F32, name="qs", tag="qs")
             nc.scalar.copy(out=qs[:, 0:2, :], in_=pq[:, 0:2, cols])
             nc.scalar.activation(out=qs[:, 2, :], in_=pq[:, 2, cols], func=IDENTITY, bias=bias_f[:, 0:1], scale=1.0)
-            st["qs"] = qs
+            st["pp"], st["qs"] = pp, qs
 
         def pe_bank(g, b):
-            xq, xsc, aq, asc, vq, vsc = st["q"]
+            xq, xsc = st["xq"]
+            aq, asc = st["aq"]
             tb = ps_t.tile([P, 2, GC], F32, name="tb", tag="tb")
             for h in range(2):
                 mx(tb[:, h, :], 0, xq[:, 2 * b + h], xsc[:, 2 * b + h], True, False)
@@ -302,13 +291,13 @@ def tile_seteq3to3_kernel(tc, x, coefs, bias, out):
                 in1=qs[:, 1, :].rearrange("p (n j) -> p n j", j=M).unsqueeze(2).to_broadcast([P, GN, M, M]),
                 op=ADD,
             )
-            st["b2"], st["b3"] = b2, b3
-            return lambda: nc.vector.tensor_tensor(
+            nc.vector.tensor_tensor(
                 out=b2v,
                 in0=b2v,
                 in1=qs[:, 2, :].rearrange("p (n k) -> p n k", k=M).unsqueeze(2).to_broadcast([P, GN, M, M]),
                 op=ADD,
             )
+            st["b2_%d" % g], st["b3_%d" % g] = b2, b3
 
         def tadd(g, b):
             if b == 0:
@@ -316,7 +305,7 @@ def tile_seteq3to3_kernel(tc, x, coefs, bias, out):
             nc.vector.tensor_tensor(
                 out=st["r"][:, 2 * b : 2 * b + 2].rearrange("p i n (j k) -> p (i n j) k", k=M),
                 in0=st["tb%d_%d" % (g, b)][:].rearrange("p h (m k) -> p (h m) k", k=M),
-                in1=st["b3"][:, 2 * b : 2 * b + 2]
+                in1=st["b3_%d" % g][:, 2 * b : 2 * b + 2]
                 .rearrange("p i n j -> p (i n j)")
                 .unsqueeze(2)
                 .to_broadcast([P, 2 * GN * M, M]),
@@ -324,10 +313,9 @@ def tile_seteq3to3_kernel(tc, x, coefs, bias, out):
             )
 
         def finish(g):
-            r, b2 = st["r"], st["b2"]
+            r, b2 = st["r"], st["b2_%d" % g]
             hm = M // 2
-
-            def half(h):
+            for h in range(2):
                 rv = r[:, h * hm : (h + 1) * hm].rearrange("p i n (j k) -> p (i n) j k", k=M)
                 nc.vector.tensor_tensor(
                     out=rv,
@@ -344,43 +332,17 @@ def tile_seteq3to3_kernel(tc, x, coefs, bias, out):
                         in_=r[:, h * hm : (h + 1) * hm, nl, :],
                     )
 
-            return [lambda: half(0), lambda: half(1)]
-
         for g in range(NG):
-            last = g == NG - 1
-            trees(g)
-            casts(g)
-            if g in G_LATER:
-                g_tree(G_LATER[g][0], G_LATER[g][1])
-            fill = []
-            if g > 0:
-                fill.append(small(g - 1))
-                if not last:
-                    for b in range(M // 2):
-                        tadd(g - 1, b)
-                    fill.extend(finish(g - 1))
-            vred(g)
-            for n in A2_LATER.get(g, ()):
-                a2(n)
-            fill.extend(quant_x(g))
-            for k, z in enumerate(ztree(g)):
-                z()
-                fill[k]()
-            for f in fill[3:]:
-                f()
             quant_av(g)
             pe_small(g)
-            if not last:
-                regroup(g + 1)
+            quant_x(g)
+            small(g)
             for b in range(M // 2):
                 pe_bank(g, b)
-                if last:
+                if g > 0:
                     tadd(g - 1, b)
-            if last:
-                for f in finish(g - 1):
-                    f()
-        small(NG - 1)()
+            if g > 0:
+                finish(g - 1)
         for b in range(M // 2):
             tadd(NG - 1, b)
-        for f in finish(NG - 1):
-            f()
+        finish(NG - 1)

@@ -12,6 +12,7 @@ U32 = mybir.dt.uint32
 U8 = mybir.dt.uint8
 FP8X4 = mybir.dt.float8_e4m3fn_x4
 ADD = mybir.AluOpType.add
+MULT = mybir.AluOpType.mult
 AXIS_X = mybir.AxisListType.X
 IDENTITY = mybir.ActivationFunctionType.Identity
 
@@ -27,15 +28,9 @@ GN = 4
 NG = NBATCH // GN
 GC = GN * MM
 COEF_CHUNKS = ((0, 8), (8, 16), (16, 18), (18, 19))
-COEF_AFTER = 6
-G_JOBS = (
-    ((0, 0, 2), (0, 2, 2)),
-    ((0, 4, 2), (0, 6, 2)),
-    ((0, 11, 1), (1, 11, 1)),
-    ((0, 12, 2), (0, 14, 2), (1, 12, 2), (1, 14, 1)),
-)
-V_A1 = (((0, 2), (2, 2)), ((4, 2), (6, 2)), ((8, 2), (10, 1)), ((15, 1),))
-PE_A0 = (8, 9, 10)
+CS = 32
+XBUFS = 8
+LEAD = 3
 
 
 def tile_seteq3to3_kernel(tc, x, coefs, bias, out):
@@ -44,39 +39,60 @@ def tile_seteq3to3_kernel(tc, x, coefs, bias, out):
         keep = ctx.enter_context(tc.tile_pool(name="keep", bufs=1))
         one = ctx.enter_context(tc.tile_pool(name="one", bufs=1))
         two = ctx.enter_context(tc.tile_pool(name="two", bufs=2))
-        ps_t = ctx.enter_context(tc.psum_pool(name="ps_t", bufs=6))
+        three = ctx.enter_context(tc.tile_pool(name="three", bufs=3))
+        xin = ctx.enter_context(tc.tile_pool(name="xin", bufs=XBUFS))
+        ps_1 = ctx.enter_context(tc.psum_pool(name="ps_1", bufs=2))
+        ps_a = ctx.enter_context(tc.psum_pool(name="ps_a", bufs=2))
         ps_s = ctx.enter_context(tc.psum_pool(name="ps_s", bufs=1))
+        ps_t = ctx.enter_context(tc.psum_pool(name="ps_t", bufs=2))
         low = "float32 sum, rounded once to bfloat16 on the way out"
 
-        ident = keep.tile([P, P], BF16, name="ident", tag="ident")
+        ident = keep.tile([P, P], F32, name="ident", tag="ident")
         make_identity(nc, ident[:])
         ctx.enter_context(tc.manual_schedule())
 
-        xs = [
-            one.tile([P, GN, PACK, W], BF16, name="xs%d" % g, tag="xs%d" % g, align_bytes=64) for g in range(NG)
-        ]
-        cs = one.tile([P, PACK, DO, NB], BF16, name="cs", tag="slot0", align_bytes=64)
+        xs, xts, pts, pas, xgs, abs_, vbs, a0s, st = {}, {}, {}, {}, {}, {}, {}, {}, {}
+
+        def load(n):
+            xs[n] = xin.tile([P, PACK, W], BF16, name="xs", tag="xs", align_bytes=64)
+            nc.sync.dma_start(out=xs[n][:], in_=x[n].rearrange("(p t) i j k -> p t (i j k)", t=PACK))
+
+        css = [keep.tile([P, PACK, CS, NB], BF16, name="cs%d" % c, tag="cs%d" % c) for c in range(DO // CS)]
+        cg = keep.tile([P, NB, DO, PACK], BF16, name="cg", tag="cg", align_bytes=64)
         bias_bf = keep.tile([P, 1], BF16, name="bias_bf", tag="bias_bf")
         bias_f = keep.tile([P, 1], F32, name="bias_f", tag="bias_f")
-        for n in range(NBATCH):
-            if n == COEF_AFTER:
-                nc.sync.dma_start(out=cs[:], in_=coefs.rearrange("(p t) s b -> p t s b", t=PACK))
-                with nc.allow_non_contiguous_dma(reason="128 bias values, one to a partition"):
-                    nc.sync.dma_start(out=bias_bf[:], in_=bias.rearrange("a s b c d -> s (a b c d)"))
+
+        def cload(c):
             nc.sync.dma_start(
-                out=xs[n // GN][:, n % GN], in_=x[n].rearrange("(p t) i j k -> p t (i j k)", t=PACK)
+                out=css[c][:], in_=coefs.rearrange("(p t) s b -> p t s b", t=PACK)[:, :, c * CS : (c + 1) * CS, :]
+            )
+
+        def cil(c):
+            nc.gpsimd.tensor_scalar(
+                out=cg[:, :, c * CS : (c + 1) * CS, :],
+                in0=css[c][:].rearrange("p t s b -> p b s t"),
+                scalar1=1.0,
+                scalar2=0.0,
+                op0=MULT,
+                op1=ADD,
             )
 
         vq = keep.tile([P, 3, P], U32, name="vq", tag="vq", align_bytes=64)
         vsc = keep.tile([P, 3, P], U8, name="vsc", tag="vsc", align_bytes=64)
-        nc.vector.memset(vq[:].bitcast(I32), 0)
-        nc.vector.memset(vsc[:].bitcast(I32), 0)
-
         cq = keep.tile([P, NB, DO], U32, name="cq", tag="cq", align_bytes=64)
         csc = keep.tile([P, NB, DO], U8, name="csc", tag="csc", align_bytes=64)
-        af = keep.tile([P, 2, NBATCH, PACK, MM], F32, name="af", tag="af")
-        ab = keep.tile([P, 3, NBATCH, MM, PACK], BF16, name="ab", tag="ab", align_bytes=64)
-        vb = keep.tile([P, NG, 3, GN, M, PACK], BF16, name="vb", tag="vb", align_bytes=64)
+        smat = keep.tile([P, 2, 2, M], BF16, name="smat", tag="smat")
+        smat1 = keep.tile([P, 2, M], BF16, name="smat1", tag="smat1")
+
+        def group_tiles(g):
+            if g not in abs_:
+                abs_[g] = three.tile([P, 3, GN, MM, PACK], BF16, name="ab", tag="ab", align_bytes=64)
+            return abs_[g]
+
+        def vb_tile(g):
+            if g not in vbs:
+                vbs[g] = two.tile([P, 3, GN, M, PACK], BF16, name="vb", tag="vb", align_bytes=64)
+            return vbs[g]
 
         def mx(acc, b, rhs, rhs_scale, start, stop):
             nc.tensor.matmul_mx(
@@ -89,167 +105,158 @@ def tile_seteq3to3_kernel(tc, x, coefs, bias, out):
                 stop=stop,
             )
 
-        st = {}
-        xgs = {}
+        def a2r(n):
+            ab = group_tiles(n // GN)
+            with nc.allow_low_precision(reason=low):
+                nc.vector.tensor_reduce(
+                    out=ab[:, 2, n % GN].rearrange("p q t -> p t q"),
+                    in_=xs[n][:].rearrange("p t (q k) -> p t q k", k=M),
+                    axis=AXIS_X,
+                    op=ADD,
+                )
 
-        def regroup(g):
-            tag = "xg0" if g == 0 else "xs%d" % (g - 1)
-            xg = one.tile([P, M, GN, MM, PACK], BF16, name="xg", tag=tag, align_bytes=64)
-            for nl in range(GN):
-                nc.scalar.copy(out=xg[:, :, nl], in_=xs[g][:, nl].rearrange("p t (i q) -> p i q t", i=M))
-            xgs[g] = xg
+        def g_tree(n):
+            src = xs[n]
+            y1 = one.tile([P, PACK, W // 2], F32, name="y1g", tag="y1g")
+            y2 = one.tile([P, PACK, W // 4], F32, name="y2g", tag="y2g")
+            a0 = two.tile([P, PACK, MM], F32, name="a0f", tag="a0f")
+            nc.gpsimd.tensor_tensor(out=y1[:], in0=src[:, :, 0 : W // 2], in1=src[:, :, W // 2 : W], op=ADD)
+            nc.gpsimd.tensor_tensor(out=y2[:], in0=y1[:, :, 0 : W // 4], in1=y1[:, :, W // 4 : W // 2], op=ADD)
+            nc.gpsimd.tensor_tensor(out=a0[:], in0=y2[:, :, 0:MM], in1=y2[:, :, MM : 2 * MM], op=ADD)
+            a0s[n] = a0
 
-        def g_tree(a, n0, cnt):
-            xv = xs[n0 // GN][:, n0 % GN : n0 % GN + cnt]
-            if a == 0:
-                src, rows, half = xv.rearrange("p n t w -> p (n t) w"), cnt * PACK, W // 2
-                dst = af[:, 0, n0 : n0 + cnt].rearrange("p n t q -> p (n t) q")
+        def t1(n):
+            words = xs[n][:].rearrange("p t w -> p (t w)").bitcast(F32)
+            xts[n] = three.tile([P, 2, 4, P, 2], BF16, name="xt", tag="xt", align_bytes=64)
+            for th in range(2):
+                pt = ps_1.tile([P, 4, P], F32, name="pt", tag="pt")
+                for kh in range(4):
+                    nc.tensor.transpose(pt[:, kh, :], words[:, th * 512 + kh : (th + 1) * 512 : 4], ident[:])
+                pts[(n, th)] = pt
+
+        def evac1(n, th):
+            nc.scalar.copy(
+                out=xts[n][:, th].rearrange("p k m e -> p (k m e)").bitcast(F32),
+                in_=pts[(n, th)][:].rearrange("p k m -> p (k m)"),
+            )
+
+        def sums(n):
+            full = n % GN != 0
+            width = 32 if full else 16
+            rhs = smat[:].rearrange("p l a y -> p (l a y)") if full else smat1[:].rearrange("p l y -> p (l y)")
+            pa = ps_a.tile([P, 512], F32, name="pa", tag="pa")
+            for th in range(2):
+                for kh in range(4):
+                    for e in range(2):
+                        col = ((kh * 2 + e) * 2 + th) * width
+                        nc.tensor.matmul(
+                            out=pa[:, col : col + width], lhsT=xts[n][:, th, kh, :, e], rhs=rhs, start=True, stop=True
+                        )
+            pas[n] = pa
+
+        def aevac(n):
+            ab, nl, pa = group_tiles(n // GN), n % GN, pas[n]
+            if nl != 0:
+                nc.scalar.copy(
+                    out=ab[:, 0:2, nl].rearrange("p a (y k) t -> p a y k t", k=M),
+                    in_=pa[:].rearrange("p (k t a y) -> p a y k t", k=M, t=PACK, a=2),
+                )
             else:
-                src, rows, half = xv.rearrange("p n t (i r) -> p (n t i) r", r=MM), cnt * PACK * M, MM // 2
-                dst = af[:, 1, n0 : n0 + cnt].rearrange("p n t (i k) -> p (n t i) k", k=M)
-            y1 = one.tile([P, 2048], F32, name="y1g", tag="y1g", align_bytes=64)
-            y2 = one.tile([P, 1024], F32, name="y2g", tag="y2g", align_bytes=64)
-            v1 = y1[:, 0 : rows * half].rearrange("p (r c) -> p r c", c=half)
-            v2 = y2[:, 0 : rows * half // 2].rearrange("p (r c) -> p r c", c=half // 2)
-            nc.gpsimd.tensor_tensor(out=v1, in0=src[:, :, 0:half], in1=src[:, :, half : 2 * half], op=ADD)
-            nc.gpsimd.tensor_tensor(out=v2, in0=v1[:, :, 0 : half // 2], in1=v1[:, :, half // 2 : half], op=ADD)
-            nc.gpsimd.tensor_tensor(out=dst, in0=v2[:, :, 0 : half // 4], in1=v2[:, :, half // 4 : half // 2], op=ADD)
+                nc.scalar.copy(
+                    out=ab[:, 1, nl].rearrange("p (y k) t -> p y k t", k=M),
+                    in_=pa[:, 0:256].rearrange("p (k t y) -> p y k t", k=M, t=PACK),
+                )
 
-        def a2(n):
+        def cast(n):
+            nc.scalar.copy(out=group_tiles(n // GN)[:, 0, n % GN], in_=a0s[n][:].rearrange("p t q -> p q t"))
+
+        def v1(n):
             with nc.allow_low_precision(reason=low):
                 nc.vector.tensor_reduce(
-                    out=ab[:, 2, n].rearrange("p q t -> p t q"),
-                    in_=xs[n // GN][:, n % GN].rearrange("p t (q k) -> p t q k", k=M),
+                    out=vb_tile(n // GN)[:, 1, n % GN].rearrange("p j t -> p t j"),
+                    in_=a0s[n][:].rearrange("p t (j k) -> p t j k", k=M),
                     axis=AXIS_X,
                     op=ADD,
                 )
 
-        def v_a1(segments):
-            halves = []
-            for lane, (n0, cnt) in enumerate(segments):
-                y = one.tile([P, 2 * GC * PACK // 2], F32, name="yv%d" % lane, tag="yv%d" % lane)
-                yv = y[:, 0 : cnt * 512]
-                nc.vector.tensor_reduce(
-                    out=yv.rearrange("p (r k) -> p r k", k=M),
-                    in_=xs[n0 // GN][:, n0 % GN : n0 % GN + cnt].rearrange(
-                        "p n t (i h j k) -> p (n t i h) k j", h=2, j=4, k=M
-                    ),
-                    axis=AXIS_X,
-                    op=ADD,
-                )
-                halves.append((yv, n0, cnt))
-            for yv, n0, cnt in halves:
-                nc.vector.tensor_reduce(
-                    out=af[:, 1, n0 : n0 + cnt].rearrange("p n t (i k) -> p (n t i) k", k=M),
-                    in_=yv.rearrange("p (r h k) -> p r k h", h=2, k=M),
-                    axis=AXIS_X,
-                    op=ADD,
-                )
-
-        def vsums(g):
-            n0 = g * GN
-            a0g = af[:, 0, n0 : n0 + GN]
-            z = one.tile([P, GN * PACK * 2 * M], F32, name="z", tag="z")
-            nc.vector.tensor_reduce(
-                out=z[:].rearrange("p (r k) -> p r k", k=M),
-                in_=a0g.rearrange("p n t (h j k) -> p (n t h) k j", h=2, j=4, k=M),
-                axis=AXIS_X,
-                op=ADD,
-            )
+        def vsums(n):
+            vb, nl, pa = vb_tile(n // GN), n % GN, pas[n]
             with nc.allow_low_precision(reason=low):
-                nc.vector.tensor_reduce(
-                    out=vb[:, g, 1].rearrange("p n j t -> p n t j"),
-                    in_=a0g.rearrange("p n t (j k) -> p n t j k", k=M),
-                    axis=AXIS_X,
-                    op=ADD,
-                )
-                nc.vector.tensor_reduce(
-                    out=vb[:, g, 2].rearrange("p n i t -> p n t i"),
-                    in_=af[:, 1, n0 : n0 + GN].rearrange("p n t (i k) -> p n t i k", k=M),
-                    axis=AXIS_X,
-                    op=ADD,
-                )
-                nc.vector.tensor_reduce(
-                    out=vb[:, g, 0].rearrange("p n k t -> p n t k"),
-                    in_=z[:].rearrange("p (n t h k) -> p n t k h", t=PACK, h=2, k=M),
-                    axis=AXIS_X,
-                    op=ADD,
-                )
+                if nl != 0:
+                    nc.vector.tensor_reduce(
+                        out=vb[:, 1:3, nl].rearrange("p a y t -> p t a y"),
+                        in_=pa[:].rearrange("p (k t a y) -> p t a y k", k=M, t=PACK, a=2),
+                        axis=AXIS_X,
+                        op=ADD,
+                    )
+                    nc.vector.tensor_reduce(
+                        out=vb[:, 0, nl].rearrange("p k t -> p t k"),
+                        in_=pa[:].rearrange("p (k t a y) -> p a t k y", k=M, t=PACK, a=2)[:, 0],
+                        axis=AXIS_X,
+                        op=ADD,
+                    )
+                else:
+                    nc.vector.tensor_reduce(
+                        out=vb[:, 2, nl].rearrange("p y t -> p t y"),
+                        in_=pa[:, 0:256].rearrange("p (k t y) -> p t y k", k=M, t=PACK),
+                        axis=AXIS_X,
+                        op=ADD,
+                    )
+                    nc.vector.tensor_reduce(
+                        out=vb[:, 0, nl].rearrange("p k t -> p t k"),
+                        in_=pa[:, 0:256].rearrange("p (k t y) -> p t k y", k=M, t=PACK),
+                        axis=AXIS_X,
+                        op=ADD,
+                    )
 
-        def casts(g):
-            n0 = g * GN
-            for a in range(2):
-                nc.scalar.copy(out=ab[:, a, n0 : n0 + GN], in_=af[:, a, n0 : n0 + GN].rearrange("p n t q -> p n q t"))
+        def il(n):
+            g = n // GN
+            if g not in xgs:
+                xgs[g] = two.tile([P, M, GN, MM, PACK], BF16, name="xg", tag="xg", align_bytes=64)
+            nc.scalar.copy(out=xgs[g][:, :, n % GN], in_=xs[n][:].rearrange("p t (i q) -> p i q t", i=M))
 
-        regroup(0)
-        cg = one.tile([P, NB, DO, PACK], BF16, name="cg", tag="slot1", align_bytes=64)
-        for b0, b1 in COEF_CHUNKS:
-            nc.scalar.copy(out=cg[:, b0:b1], in_=cs[:, :, :, b0:b1].rearrange("p t s b -> p b s t"))
-        for n in PE_A0:
-            acc = ps_t.tile([P, PACK, MM], F32, name="pe_sum", tag="tb")
-            for i in range(M):
-                nc.tensor.matmul(
-                    out=acc[:],
-                    lhsT=ident[:],
-                    rhs=xs[n // GN][:, n % GN, :, i * MM : (i + 1) * MM],
-                    start=(i == 0),
-                    stop=(i == M - 1),
+        def quant_c():
+            nc.vector.tensor_copy(out=bias_f[:], in_=bias_bf[:])
+            for b0, b1 in COEF_CHUNKS:
+                nc.vector.quantize_mx(
+                    out=cq[:, b0:b1].rearrange("p b s -> p (b s)").bitcast(FP8X4),
+                    scales=csc[:, b0:b1].rearrange("p b s -> p (b s)"),
+                    in_=cg[:, b0:b1].rearrange("p b s t -> p (b s t)"),
                 )
-            nc.scalar.copy(out=af[:, 0, n], in_=acc[:])
-        for g in range(NG):
-            for a, n0, cnt in G_JOBS[g]:
-                g_tree(a, n0, cnt)
-            for n in range(g * GN, (g + 1) * GN):
-                a2(n)
-            v_a1(V_A1[g])
-            if g > 0:
-                vsums(g - 1)
-            if g + 1 < NG:
-                casts(g)
-                regroup(g + 1)
-        casts(NG - 1)
-        vsums(NG - 1)
-
-        nc.vector.tensor_copy(out=bias_f[:], in_=bias_bf[:])
-        for b0, b1 in COEF_CHUNKS:
-            nc.vector.quantize_mx(
-                out=cq[:, b0:b1].rearrange("p b s -> p (b s)").bitcast(FP8X4),
-                scales=csc[:, b0:b1].rearrange("p b s -> p (b s)"),
-                in_=cg[:, b0:b1].rearrange("p b s t -> p (b s t)"),
-            )
 
         def quant_x(g):
             xg = xgs[g]
-            xq = one.tile([P, M, GC], U32, name="xq", tag="y1g", align_bytes=64)
-            xsc = one.tile([P, M, GC], U8, name="xsc", tag="y2g", align_bytes=64)
-            for b in range(M // 2):
+            xq = two.tile([P, M, GC], U32, name="xq", tag="xq", align_bytes=64)
+            xsc = two.tile([P, M, GC], U8, name="xsc", tag="xsc", align_bytes=64)
+            hm = M // 2
+            for b in range(2):
                 nc.vector.quantize_mx(
-                    out=xq[:, 2 * b : 2 * b + 2].rearrange("p i c -> p (i c)").bitcast(FP8X4),
-                    scales=xsc[:, 2 * b : 2 * b + 2].rearrange("p i c -> p (i c)"),
-                    in_=xg[:, 2 * b : 2 * b + 2].rearrange("p i n q t -> p (i n q t)"),
+                    out=xq[:, hm * b : hm * (b + 1)].rearrange("p i c -> p (i c)").bitcast(FP8X4),
+                    scales=xsc[:, hm * b : hm * (b + 1)].rearrange("p i c -> p (i c)"),
+                    in_=xg[:, hm * b : hm * (b + 1)].rearrange("p i n q t -> p (i n q t)"),
                 )
-            st["xq"] = (xq, xsc)
+            st["xq%d" % g] = (xq, xsc)
 
         def quant_av(g):
-            n0 = g * GN
+            ab, vb = abs_[g], vbs[g]
             aq = two.tile([P, 3, GC], U32, name="aq", tag="aq", align_bytes=64)
             asc = two.tile([P, 3, GC], U8, name="asc", tag="asc", align_bytes=64)
             for a in range(3):
                 nc.vector.quantize_mx(
                     out=aq[:, a].bitcast(FP8X4),
                     scales=asc[:, a],
-                    in_=ab[:, a, n0 : n0 + GN].rearrange("p n q t -> p (n q t)"),
+                    in_=ab[:, a].rearrange("p n q t -> p (n q t)"),
                 )
             for a in range(3):
                 nc.vector.quantize_mx(
                     out=vq[:, a, 0 : GN * M].bitcast(FP8X4),
                     scales=vsc[:, a, 0 : GN * M],
-                    in_=vb[:, g, a].rearrange("p n m t -> p (n m t)"),
+                    in_=vb[:, a].rearrange("p n m t -> p (n m t)"),
                 )
-            st["aq"] = (aq, asc)
+            st["aq%d" % g] = (aq, asc)
 
         def pe_small(g):
-            aq, asc = st["aq"]
+            aq, asc = st["aq%d" % g]
             pp = ps_s.tile([P, 2, GC], F32, name="pp", tag="pp")
             for t in range(2):
                 for a in range(3):
@@ -258,15 +265,19 @@ def tile_seteq3to3_kernel(tc, x, coefs, bias, out):
             for t in range(3):
                 for a in range(3):
                     mx(pq[:, t, :], 10 + 3 * a + t, vq[:, a], vsc[:, a], a == 0, a == 2)
+            st["pp"], st["pq"] = pp, pq
+
+        def qs_evac(g):
+            pq = st["pq"]
             cols = slice(0, GN * M)
             qs = two.tile([P, 3, GN * M], F32, name="qs", tag="qs")
             nc.scalar.copy(out=qs[:, 0:2, :], in_=pq[:, 0:2, cols])
             nc.scalar.activation(out=qs[:, 2, :], in_=pq[:, 2, cols], func=IDENTITY, bias=bias_f[:, 0:1], scale=1.0)
-            st["pp"], st["qs"] = pp, qs
+            st["qs"] = qs
 
         def pe_bank(g, b):
-            xq, xsc = st["xq"]
-            aq, asc = st["aq"]
+            xq, xsc = st["xq%d" % g]
+            aq, asc = st["aq%d" % g]
             tb = ps_t.tile([P, 2, GC], F32, name="tb", tag="tb")
             for h in range(2):
                 mx(tb[:, h, :], 0, xq[:, 2 * b + h], xsc[:, 2 * b + h], True, False)
@@ -301,9 +312,9 @@ def tile_seteq3to3_kernel(tc, x, coefs, bias, out):
 
         def tadd(g, b):
             if b == 0:
-                st["r"] = one.tile([P, M, GN, MM], F32, name="r", tag="slot%d" % (g % 2), align_bytes=64)
+                st["r%d" % g] = two.tile([P, M, GN, MM], F32, name="r", tag="r", align_bytes=64)
             nc.vector.tensor_tensor(
-                out=st["r"][:, 2 * b : 2 * b + 2].rearrange("p i n (j k) -> p (i n j) k", k=M),
+                out=st["r%d" % g][:, 2 * b : 2 * b + 2].rearrange("p i n (j k) -> p (i n j) k", k=M),
                 in0=st["tb%d_%d" % (g, b)][:].rearrange("p h (m k) -> p (h m) k", k=M),
                 in1=st["b3_%d" % g][:, 2 * b : 2 * b + 2]
                 .rearrange("p i n j -> p (i n j)")
@@ -312,37 +323,106 @@ def tile_seteq3to3_kernel(tc, x, coefs, bias, out):
                 op=ADD,
             )
 
-        def finish(g):
-            r, b2 = st["r"], st["b2_%d" % g]
+        def finish(g, h):
+            r, b2 = st["r%d" % g], st["b2_%d" % g]
             hm = M // 2
-            for h in range(2):
-                rv = r[:, h * hm : (h + 1) * hm].rearrange("p i n (j k) -> p (i n) j k", k=M)
-                nc.vector.tensor_tensor(
-                    out=rv,
-                    in0=rv,
-                    in1=b2[:, h * hm : (h + 1) * hm]
-                    .rearrange("p i n k -> p (i n) k")
-                    .unsqueeze(2)
-                    .to_broadcast([P, hm * GN, M, M]),
-                    op=ADD,
+            rv = r[:, h * hm : (h + 1) * hm].rearrange("p i n (j k) -> p (i n) j k", k=M)
+            nc.vector.tensor_tensor(
+                out=rv,
+                in0=rv,
+                in1=b2[:, h * hm : (h + 1) * hm]
+                .rearrange("p i n k -> p (i n) k")
+                .unsqueeze(2)
+                .to_broadcast([P, hm * GN, M, M]),
+                op=ADD,
+            )
+            for nl in range(GN):
+                nc.sync.dma_start(
+                    out=out[g * GN + nl, :, h * hm : (h + 1) * hm].rearrange("s i j k -> s i (j k)"),
+                    in_=r[:, h * hm : (h + 1) * hm, nl, :],
                 )
-                for nl in range(GN):
-                    nc.sync.dma_start(
-                        out=out[g * GN + nl, :, h * hm : (h + 1) * hm].rearrange("s i j k -> s i (j k)"),
-                        in_=r[:, h * hm : (h + 1) * hm, nl, :],
-                    )
 
-        for g in range(NG):
-            quant_av(g)
-            pe_small(g)
-            quant_x(g)
-            small(g)
-            for b in range(M // 2):
-                pe_bank(g, b)
-                if g > 0:
-                    tadd(g - 1, b)
-            if g > 0:
-                finish(g - 1)
-        for b in range(M // 2):
-            tadd(NG - 1, b)
-        finish(NG - 1)
+        load(0)
+        load(1)
+        for c in range(DO // CS):
+            cload(c)
+            load(2 + c)
+        with nc.allow_non_contiguous_dma(reason="128 bias values, one to a partition"):
+            nc.sync.dma_start(out=bias_bf[:], in_=bias.rearrange("a s b c d -> s (a b c d)"))
+        for n in range(6, XBUFS):
+            load(n)
+
+        nc.vector.memset(vq[:].bitcast(I32), 0)
+        nc.vector.memset(vsc[:].bitcast(I32), 0)
+        with nc.allow_low_precision(reason="sums of zeros and a one"):
+            nc.vector.tensor_reduce(
+                out=smat[:, :, 0, :], in_=ident[:].rearrange("p (l i j) -> p l j i", l=2, i=M), axis=AXIS_X, op=ADD
+            )
+            nc.vector.tensor_reduce(
+                out=smat[:, :, 1, :], in_=ident[:].rearrange("p (l i j) -> p l i j", l=2, i=M), axis=AXIS_X, op=ADD
+            )
+            nc.vector.tensor_reduce(
+                out=smat1[:], in_=ident[:].rearrange("p (l i j) -> p l i j", l=2, i=M), axis=AXIS_X, op=ADD
+            )
+        for n in range(LEAD):
+            a2r(n)
+
+        def slot(n):
+            if n < NBATCH:
+                if n % GN == 0:
+                    g_tree(n)
+                if n == 0:
+                    for c in range(DO // CS):
+                        cil(c)
+                t1(n)
+            if 1 <= n <= NBATCH:
+                sums(n - 1)
+            if n < NBATCH:
+                evac1(n, 0)
+                evac1(n, 1)
+            if 1 <= n <= NBATCH:
+                aevac(n - 1)
+            if n < NBATCH:
+                il(n)
+            if 1 <= n <= NBATCH and (n - 1) % GN == 2:
+                cast(n - 3)
+                v1(n - 3)
+            if 0 <= n - 2 < NBATCH:
+                vsums(n - 2)
+            if n + LEAD < NBATCH:
+                a2r(n + LEAD)
+            if n + XBUFS < NBATCH:
+                load(n + XBUFS)
+
+        def phase(g, k):
+            if k == 0:
+                quant_x(g)
+            elif k == 1:
+                if g == 0:
+                    quant_c()
+                quant_av(g)
+            elif k == 2:
+                pe_small(g)
+                pe_bank(g, 0)
+                pe_bank(g, 1)
+                qs_evac(g)
+            elif k == 3:
+                small(g)
+                tadd(g, 0)
+                pe_bank(g, 2)
+                tadd(g, 1)
+                pe_bank(g, 3)
+            elif k == 4:
+                tadd(g, 2)
+                tadd(g, 3)
+                finish(g, 0)
+            else:
+                finish(g, 1)
+
+        for s in range(GN * NG + 10):
+            if s <= NBATCH + 1:
+                slot(s)
+            for g in range(NG):
+                k = s - (GN * g + GN)
+                if 0 <= k <= 5:
+                    phase(g, k)

@@ -130,8 +130,9 @@ def tile_seteq3to3_kernel(tc, x, coefs, bias, out):
             xts[n] = three.tile([P, 2, 4, P, 2], BF16, name="xt", tag="xt", align_bytes=64)
             for th in range(2):
                 pt = ps_1.tile([P, 4, P], F32, name="pt", tag="pt")
-                for kh in range(4):
-                    nc.tensor.transpose(pt[:, kh, :], words[:, th * 512 + kh : (th + 1) * 512 : 4], ident[:])
+                for b in range(4):
+                    t, kl = 2 * th + b // 2, b % 2
+                    nc.tensor.transpose(pt[:, b, :], words[:, t * 256 + kl : (t + 1) * 256 : 2], ident[:])
                 pts[(n, th)] = pt
 
         def evac1(n, th):
@@ -146,11 +147,12 @@ def tile_seteq3to3_kernel(tc, x, coefs, bias, out):
             rhs = smat[:].rearrange("p l a y -> p (l a y)") if full else smat1[:].rearrange("p l y -> p (l y)")
             pa = ps_a.tile([P, 512], F32, name="pa", tag="pa")
             for th in range(2):
-                for kh in range(4):
+                for b in range(4):
                     for e in range(2):
-                        col = ((kh * 2 + e) * 2 + th) * width
+                        t, kl = 2 * th + b // 2, b % 2
+                        col = (t * 4 + kl * 2 + e) * width
                         nc.tensor.matmul(
-                            out=pa[:, col : col + width], lhsT=xts[n][:, th, kh, :, e], rhs=rhs, start=True, stop=True
+                            out=pa[:, col : col + width], lhsT=xts[n][:, th, b, :, e], rhs=rhs, start=True, stop=True
                         )
             pas[n] = pa
 
@@ -158,13 +160,13 @@ def tile_seteq3to3_kernel(tc, x, coefs, bias, out):
             ab, nl, pa = group_tiles(n // GN), n % GN, pas[n]
             if nl != 0:
                 nc.scalar.copy(
-                    out=ab[:, 0:2, nl].rearrange("p a (y k) t -> p a y k t", k=M),
-                    in_=pa[:].rearrange("p (k t a y) -> p a y k t", k=M, t=PACK, a=2),
+                    out=ab[:, 0:2, nl].rearrange("p a (y h c) t -> p a y h c t", h=2, c=4),
+                    in_=pa[:].rearrange("p (t c h a y) -> p a y h c t", t=PACK, c=4, h=2, a=2),
                 )
             else:
                 nc.scalar.copy(
-                    out=ab[:, 1, nl].rearrange("p (y k) t -> p y k t", k=M),
-                    in_=pa[:, 0:256].rearrange("p (k t y) -> p y k t", k=M, t=PACK),
+                    out=ab[:, 1, nl].rearrange("p (y h c) t -> p y h c t", h=2, c=4),
+                    in_=pa[:, 0:256].rearrange("p (t c h y) -> p y h c t", t=PACK, c=4, h=2),
                 )
 
         def cast(n):
@@ -185,26 +187,26 @@ def tile_seteq3to3_kernel(tc, x, coefs, bias, out):
                 if nl != 0:
                     nc.vector.tensor_reduce(
                         out=vb[:, 1:3, nl].rearrange("p a y t -> p t a y"),
-                        in_=pa[:].rearrange("p (k t a y) -> p t a y k", k=M, t=PACK, a=2),
+                        in_=pa[:].rearrange("p (t k a y) -> p t a y k", k=M, t=PACK, a=2),
                         axis=AXIS_X,
                         op=ADD,
                     )
                     nc.vector.tensor_reduce(
-                        out=vb[:, 0, nl].rearrange("p k t -> p t k"),
-                        in_=pa[:].rearrange("p (k t a y) -> p a t k y", k=M, t=PACK, a=2)[:, 0],
+                        out=vb[:, 0, nl].rearrange("p (h c) t -> p t c h", h=2),
+                        in_=pa[:].rearrange("p (t c h a y) -> p a t c h y", t=PACK, c=4, h=2, a=2)[:, 0],
                         axis=AXIS_X,
                         op=ADD,
                     )
                 else:
                     nc.vector.tensor_reduce(
                         out=vb[:, 2, nl].rearrange("p y t -> p t y"),
-                        in_=pa[:, 0:256].rearrange("p (k t y) -> p t y k", k=M, t=PACK),
+                        in_=pa[:, 0:256].rearrange("p (t k y) -> p t y k", k=M, t=PACK),
                         axis=AXIS_X,
                         op=ADD,
                     )
                     nc.vector.tensor_reduce(
-                        out=vb[:, 0, nl].rearrange("p k t -> p t k"),
-                        in_=pa[:, 0:256].rearrange("p (k t y) -> p t k y", k=M, t=PACK),
+                        out=vb[:, 0, nl].rearrange("p (h c) t -> p t c h", h=2),
+                        in_=pa[:, 0:256].rearrange("p (t c h y) -> p t c h y", t=PACK, c=4, h=2),
                         axis=AXIS_X,
                         op=ADD,
                     )
@@ -356,13 +358,13 @@ def tile_seteq3to3_kernel(tc, x, coefs, bias, out):
         nc.vector.memset(vsc[:].bitcast(I32), 0)
         with nc.allow_low_precision(reason="sums of zeros and a one"):
             nc.vector.tensor_reduce(
-                out=smat[:, :, 0, :], in_=ident[:].rearrange("p (l i j) -> p l j i", l=2, i=M), axis=AXIS_X, op=ADD
+                out=smat[:, :, 0, :], in_=ident[:].rearrange("p (i j h) -> p h j i", i=M, j=M), axis=AXIS_X, op=ADD
             )
             nc.vector.tensor_reduce(
-                out=smat[:, :, 1, :], in_=ident[:].rearrange("p (l i j) -> p l i j", l=2, i=M), axis=AXIS_X, op=ADD
+                out=smat[:, :, 1, :], in_=ident[:].rearrange("p (i j h) -> p h i j", i=M, j=M), axis=AXIS_X, op=ADD
             )
             nc.vector.tensor_reduce(
-                out=smat1[:], in_=ident[:].rearrange("p (l i j) -> p l i j", l=2, i=M), axis=AXIS_X, op=ADD
+                out=smat1[:], in_=ident[:].rearrange("p (i j h) -> p h i j", i=M, j=M), axis=AXIS_X, op=ADD
             )
         for n in range(LEAD):
             a2r(n)

@@ -31,6 +31,7 @@ COEF_CHUNKS = ((0, 8), (8, 16), (16, 18), (18, 19))
 CS = 32
 XBUFS = 8
 LEAD = 3
+QSET = (6, 7, 10, 11, 14, 15)
 
 
 def tile_seteq3to3_kernel(tc, x, coefs, bias, out):
@@ -49,6 +50,8 @@ def tile_seteq3to3_kernel(tc, x, coefs, bias, out):
 
         ident = keep.tile([P, P], F32, name="ident", tag="ident")
         make_identity(nc, ident[:])
+        ident_b = keep.tile([P, P], BF16, name="ident_b", tag="ident_b")
+        make_identity(nc, ident_b[:])
         ctx.enter_context(tc.manual_schedule())
 
         xs, xts, pts, pas, xgs, abs_, vbs, a0s, st = {}, {}, {}, {}, {}, {}, {}, {}, {}
@@ -83,6 +86,8 @@ def tile_seteq3to3_kernel(tc, x, coefs, bias, out):
         csc = keep.tile([P, NB, DO], U8, name="csc", tag="csc", align_bytes=64)
         smat = keep.tile([P, 2, 2, M], BF16, name="smat", tag="smat")
         smat1 = keep.tile([P, 2, M], BF16, name="smat1", tag="smat1")
+        smatq = keep.tile([P, 2, 2, M], BF16, name="smatq", tag="smatq")
+        tok = keep.tile([P, 1], F32, name="tok", tag="tok")
 
         def group_tiles(g):
             if g not in abs_:
@@ -119,13 +124,25 @@ def tile_seteq3to3_kernel(tc, x, coefs, bias, out):
             src = xs[n]
             y1 = one.tile([P, PACK, W // 2], F32, name="y1g", tag="y1g")
             y2 = one.tile([P, PACK, W // 4], F32, name="y2g", tag="y2g")
-            a0 = two.tile([P, PACK, MM], F32, name="a0f", tag="a0f")
+            a0 = three.tile([P, PACK, MM], F32, name="a0f", tag="a0f")
             nc.gpsimd.tensor_tensor(out=y1[:], in0=src[:, :, 0 : W // 2], in1=src[:, :, W // 2 : W], op=ADD)
             nc.gpsimd.tensor_tensor(out=y2[:], in0=y1[:, :, 0 : W // 4], in1=y1[:, :, W // 4 : W // 2], op=ADD)
             nc.gpsimd.tensor_tensor(out=a0[:], in0=y2[:, :, 0:MM], in1=y2[:, :, MM : 2 * MM], op=ADD)
             a0s[n] = a0
+            st["y1g"] = y1
 
         def t1(n):
+            if n in QSET:
+                xts[n] = three.tile([P, PACK, 4, P], BF16, name="xt", tag="xt", align_bytes=64)
+                for th in range(2):
+                    pt = ps_1.tile([P, 2, 4, P], BF16, name="pt", tag="pt")
+                    for tl in range(2):
+                        for wb in range(4):
+                            nc.tensor.transpose(
+                                pt[:, tl, wb, :], xs[n][:, 2 * th + tl, wb * P : (wb + 1) * P], ident_b[:]
+                            )
+                    pts[(n, th)] = pt
+                return
             words = xs[n][:].rearrange("p t w -> p (t w)").bitcast(F32)
             xts[n] = three.tile([P, 2, 4, P, 2], BF16, name="xt", tag="xt", align_bytes=64)
             for th in range(2):
@@ -136,12 +153,32 @@ def tile_seteq3to3_kernel(tc, x, coefs, bias, out):
                 pts[(n, th)] = pt
 
         def evac1(n, th):
+            if n in QSET:
+                nc.scalar.copy(
+                    out=xts[n][:, 2 * th : 2 * th + 2].rearrange("p t w m -> p (t w m)").bitcast(F32),
+                    in_=pts[(n, th)][:].rearrange("p t w m -> p (t w m)").bitcast(F32),
+                )
+                return
             nc.scalar.copy(
                 out=xts[n][:, th].rearrange("p k m e -> p (k m e)").bitcast(F32),
                 in_=pts[(n, th)][:].rearrange("p k m -> p (k m)"),
             )
 
         def sums(n):
+            if n in QSET:
+                pa = ps_a.tile([P, 512], F32, name="pa", tag="pa")
+                for t in range(PACK):
+                    for wb in range(4):
+                        col = (t * 4 + wb) * 32
+                        nc.tensor.matmul(
+                            out=pa[:, col : col + 32],
+                            lhsT=xts[n][:, t, wb, :],
+                            rhs=smatq[:].rearrange("p l a y -> p (l a y)"),
+                            start=True,
+                            stop=True,
+                        )
+                pas[n] = pa
+                return
             full = n % GN != 0
             width = 32 if full else 16
             rhs = smat[:].rearrange("p l a y -> p (l a y)") if full else smat1[:].rearrange("p l y -> p (l y)")
@@ -158,7 +195,12 @@ def tile_seteq3to3_kernel(tc, x, coefs, bias, out):
 
         def aevac(n):
             ab, nl, pa = group_tiles(n // GN), n % GN, pas[n]
-            if nl != 0:
+            if n in QSET:
+                nc.scalar.copy(
+                    out=ab[:, 1:3, nl].rearrange("p a (i y) t -> p a i y t", y=M),
+                    in_=pa[:].rearrange("p (t i a y) -> p a i y t", t=PACK, i=M, a=2),
+                )
+            elif nl != 0:
                 nc.scalar.copy(
                     out=ab[:, 0:2, nl].rearrange("p a (y h c) t -> p a y h c t", h=2, c=4),
                     in_=pa[:].rearrange("p (t c h a y) -> p a y h c t", t=PACK, c=4, h=2, a=2),
@@ -184,7 +226,20 @@ def tile_seteq3to3_kernel(tc, x, coefs, bias, out):
         def vsums(n):
             vb, nl, pa = vb_tile(n // GN), n % GN, pas[n]
             with nc.allow_low_precision(reason=low):
-                if nl != 0:
+                if n in QSET:
+                    nc.vector.tensor_reduce(
+                        out=vb[:, 0:2, nl].rearrange("p a y t -> p t a y"),
+                        in_=pa[:].rearrange("p (t i a y) -> p t a y i", t=PACK, i=M, a=2),
+                        axis=AXIS_X,
+                        op=ADD,
+                    )
+                    nc.vector.tensor_reduce(
+                        out=vb[:, 2, nl].rearrange("p i t -> p t i"),
+                        in_=pa[:].rearrange("p (t i a y) -> p a t i y", t=PACK, i=M, a=2)[:, 0],
+                        axis=AXIS_X,
+                        op=ADD,
+                    )
+                elif nl != 0:
                     nc.vector.tensor_reduce(
                         out=vb[:, 1:3, nl].rearrange("p a y t -> p t a y"),
                         in_=pa[:].rearrange("p (t k a y) -> p t a y k", k=M, t=PACK, a=2),
@@ -366,14 +421,24 @@ def tile_seteq3to3_kernel(tc, x, coefs, bias, out):
             nc.vector.tensor_reduce(
                 out=smat1[:], in_=ident[:].rearrange("p (i j h) -> p h i j", i=M, j=M), axis=AXIS_X, op=ADD
             )
+            nc.vector.tensor_reduce(
+                out=smatq[:, :, 0, :], in_=ident[:].rearrange("p (l j k) -> p l k j", l=2, j=M), axis=AXIS_X, op=ADD
+            )
+            nc.vector.tensor_reduce(
+                out=smatq[:, :, 1, :], in_=ident[:].rearrange("p (l j k) -> p l j k", l=2, j=M), axis=AXIS_X, op=ADD
+            )
         for n in range(LEAD):
             a2r(n)
 
+        def g_jobs(g):
+            for n in range(GN * g, GN * g + GN):
+                if n % GN == 0 or n in QSET:
+                    g_tree(n)
+
         def slot(n):
             if n < NBATCH:
-                if n % GN == 0:
-                    g_tree(n)
                 if n == 0:
+                    g_jobs(0)
                     for c in range(DO // CS):
                         cil(c)
                 t1(n)
@@ -386,23 +451,28 @@ def tile_seteq3to3_kernel(tc, x, coefs, bias, out):
                 aevac(n - 1)
             if n < NBATCH:
                 il(n)
-            if 1 <= n <= NBATCH and (n - 1) % GN == 2:
-                cast(n - 3)
-                v1(n - 3)
+            if n > GN and n % GN == 1:
+                for m in range(n - GN - 1, n - 1):
+                    if m % GN == 0 or m in QSET:
+                        cast(m)
+                v1(n - GN - 1)
             if 0 <= n - 2 < NBATCH:
                 vsums(n - 2)
-            if n + LEAD < NBATCH:
+            if n + LEAD < NBATCH and n + LEAD not in QSET:
                 a2r(n + LEAD)
-            if n + XBUFS < NBATCH:
-                load(n + XBUFS)
 
         def phase(g, k):
-            if k == 0:
+            if k == 1:
+                if g > 0:
+                    finish(g - 1, 0)
+                    finish(g - 1, 1)
                 quant_x(g)
-            elif k == 1:
                 if g == 0:
                     quant_c()
                 quant_av(g)
+                if g + 1 < NG:
+                    nc.vector.tensor_copy(out=tok[:], in_=st["y1g"][:, 0, 0:1])
+                    g_jobs(g + 1)
             elif k == 2:
                 pe_small(g)
                 pe_bank(g, 0)
@@ -417,8 +487,8 @@ def tile_seteq3to3_kernel(tc, x, coefs, bias, out):
             elif k == 4:
                 tadd(g, 2)
                 tadd(g, 3)
+            elif k == 5 and g == NG - 1:
                 finish(g, 0)
-            else:
                 finish(g, 1)
 
         for s in range(GN * NG + 10):
@@ -428,3 +498,5 @@ def tile_seteq3to3_kernel(tc, x, coefs, bias, out):
                 k = s - (GN * g + GN)
                 if 0 <= k <= 5:
                     phase(g, k)
+            if s >= 2 and s - 2 + XBUFS < NBATCH:
+                load(s - 2 + XBUFS)

@@ -31,7 +31,7 @@ COEF_CHUNKS = ((0, 8), (8, 16), (16, 18), (18, 19))
 CS = 32
 XBUFS = 8
 LEAD = 3
-QSET = (6, 7, 10, 11, 14, 15)
+QSET = (5, 7, 9, 11, 13)
 
 
 def tile_seteq3to3_kernel(tc, x, coefs, bias, out):
@@ -42,6 +42,7 @@ def tile_seteq3to3_kernel(tc, x, coefs, bias, out):
         two = ctx.enter_context(tc.tile_pool(name="two", bufs=2))
         three = ctx.enter_context(tc.tile_pool(name="three", bufs=3))
         xin = ctx.enter_context(tc.tile_pool(name="xin", bufs=XBUFS))
+        gout = ctx.enter_context(tc.tile_pool(name="gout", bufs=6))
         ps_1 = ctx.enter_context(tc.psum_pool(name="ps_1", bufs=2))
         ps_a = ctx.enter_context(tc.psum_pool(name="ps_a", bufs=2))
         ps_s = ctx.enter_context(tc.psum_pool(name="ps_s", bufs=1))
@@ -87,7 +88,6 @@ def tile_seteq3to3_kernel(tc, x, coefs, bias, out):
         smat = keep.tile([P, 2, 2, M], BF16, name="smat", tag="smat")
         smat1 = keep.tile([P, 2, M], BF16, name="smat1", tag="smat1")
         smatq = keep.tile([P, 2, 2, M], BF16, name="smatq", tag="smatq")
-        tok = keep.tile([P, 1], F32, name="tok", tag="tok")
 
         def group_tiles(g):
             if g not in abs_:
@@ -124,12 +124,11 @@ def tile_seteq3to3_kernel(tc, x, coefs, bias, out):
             src = xs[n]
             y1 = one.tile([P, PACK, W // 2], F32, name="y1g", tag="y1g")
             y2 = one.tile([P, PACK, W // 4], F32, name="y2g", tag="y2g")
-            a0 = three.tile([P, PACK, MM], F32, name="a0f", tag="a0f")
+            a0 = gout.tile([P, PACK, MM], F32, name="a0f", tag="a0f")
             nc.gpsimd.tensor_tensor(out=y1[:], in0=src[:, :, 0 : W // 2], in1=src[:, :, W // 2 : W], op=ADD)
             nc.gpsimd.tensor_tensor(out=y2[:], in0=y1[:, :, 0 : W // 4], in1=y1[:, :, W // 4 : W // 2], op=ADD)
             nc.gpsimd.tensor_tensor(out=a0[:], in0=y2[:, :, 0:MM], in1=y2[:, :, MM : 2 * MM], op=ADD)
             a0s[n] = a0
-            st["y1g"] = y1
 
         def t1(n):
             if n in QSET:
@@ -430,15 +429,11 @@ def tile_seteq3to3_kernel(tc, x, coefs, bias, out):
         for n in range(LEAD):
             a2r(n)
 
-        def g_jobs(g):
-            for n in range(GN * g, GN * g + GN):
-                if n % GN == 0 or n in QSET:
-                    g_tree(n)
-
         def slot(n):
             if n < NBATCH:
+                if n % GN == 0 or n in QSET:
+                    g_tree(n)
                 if n == 0:
-                    g_jobs(0)
                     for c in range(DO // CS):
                         cil(c)
                 t1(n)
@@ -460,43 +455,39 @@ def tile_seteq3to3_kernel(tc, x, coefs, bias, out):
                 vsums(n - 2)
             if n + LEAD < NBATCH and n + LEAD not in QSET:
                 a2r(n + LEAD)
+            if n + XBUFS < NBATCH:
+                load(n + XBUFS)
 
         def phase(g, k):
-            if k == 1:
-                if g > 0:
-                    finish(g - 1, 0)
-                    finish(g - 1, 1)
+            if k == 0:
                 quant_x(g)
+            elif k == 1:
                 if g == 0:
                     quant_c()
                 quant_av(g)
-                if g + 1 < NG:
-                    nc.vector.tensor_copy(out=tok[:], in_=st["y1g"][:, 0, 0:1])
-                    g_jobs(g + 1)
             elif k == 2:
                 pe_small(g)
                 pe_bank(g, 0)
-                pe_bank(g, 1)
                 qs_evac(g)
             elif k == 3:
                 small(g)
                 tadd(g, 0)
-                pe_bank(g, 2)
-                tadd(g, 1)
-                pe_bank(g, 3)
+                pe_bank(g, 1)
             elif k == 4:
+                tadd(g, 1)
+                pe_bank(g, 2)
+            elif k == 5:
                 tadd(g, 2)
-                tadd(g, 3)
-            elif k == 5 and g == NG - 1:
+                pe_bank(g, 3)
                 finish(g, 0)
+            else:
+                tadd(g, 3)
                 finish(g, 1)
 
-        for s in range(GN * NG + 10):
+        for s in range(GN * NG + 11):
             if s <= NBATCH + 1:
                 slot(s)
             for g in range(NG):
                 k = s - (GN * g + GN)
-                if 0 <= k <= 5:
+                if 0 <= k <= 6:
                     phase(g, k)
-            if s >= 2 and s - 2 + XBUFS < NBATCH:
-                load(s - 2 + XBUFS)

@@ -265,11 +265,13 @@ def tile_seteq3to3_kernel(tc, x, coefs, bias, out):
                         op=ADD,
                     )
 
-        def il(n):
+        def il(n, i0=0, i1=M):
             g = n // GN
             if g not in xgs:
                 xgs[g] = two.tile([P, M, GN, MM, PACK], BF16, name="xg", tag="xg", align_bytes=64)
-            nc.scalar.copy(out=xgs[g][:, :, n % GN], in_=xs[n][:].rearrange("p t (i q) -> p i q t", i=M))
+            nc.scalar.copy(
+                out=xgs[g][:, i0:i1, n % GN], in_=xs[n][:].rearrange("p t (i q) -> p i q t", i=M)[:, i0:i1]
+            )
 
         def quant_c():
             nc.vector.tensor_copy(out=bias_f[:], in_=bias_bf[:])
@@ -280,18 +282,20 @@ def tile_seteq3to3_kernel(tc, x, coefs, bias, out):
                     in_=cg[:, b0:b1].rearrange("p b s t -> p (b s t)"),
                 )
 
-        def quant_x(g):
+        def quant_x(g, halves=(0, 1)):
             xg = xgs[g]
-            xq = two.tile([P, M, GC], U32, name="xq", tag="xq", align_bytes=64)
-            xsc = two.tile([P, M, GC], U8, name="xsc", tag="xsc", align_bytes=64)
+            if halves[0] == 0:
+                xq = two.tile([P, M, GC], U32, name="xq", tag="xq", align_bytes=64)
+                xsc = two.tile([P, M, GC], U8, name="xsc", tag="xsc", align_bytes=64)
+                st["xq%d" % g] = (xq, xsc)
+            xq, xsc = st["xq%d" % g]
             hm = M // 2
-            for b in range(2):
+            for b in halves:
                 nc.vector.quantize_mx(
                     out=xq[:, hm * b : hm * (b + 1)].rearrange("p i c -> p (i c)").bitcast(FP8X4),
                     scales=xsc[:, hm * b : hm * (b + 1)].rearrange("p i c -> p (i c)"),
                     in_=xg[:, hm * b : hm * (b + 1)].rearrange("p i n q t -> p (i n q t)"),
                 )
-            st["xq%d" % g] = (xq, xsc)
 
         def quant_av(g):
             ab, vb = abs_[g], vbs[g]
@@ -334,7 +338,12 @@ def tile_seteq3to3_kernel(tc, x, coefs, bias, out):
         def pe_bank(g, b):
             xq, xsc = st["xq%d" % g]
             aq, asc = st["aq%d" % g]
-            tb = ps_t.tile([P, 2, GC], F32, name="tb", tag="tb")
+            if g < NG - 1:
+                tb = ps_t.tile([P, 2, GC], F32, name="tb", tag="tb")
+            elif b < 2:
+                tb = ps_a.tile([P, 2, GC], F32, name="pa", tag="pa")
+            else:
+                tb = ps_1.tile([P, 2, GC], F32, name="pt", tag="pt")
             for h in range(2):
                 mx(tb[:, h, :], 0, xq[:, 2 * b + h], xsc[:, 2 * b + h], True, False)
                 for a in range(3):
@@ -378,6 +387,40 @@ def tile_seteq3to3_kernel(tc, x, coefs, bias, out):
                 .to_broadcast([P, 2 * GN * M, M]),
                 op=ADD,
             )
+
+        def cbuild(g, h):
+            hm = M // 2
+            if h == 0:
+                st["c"] = one.tile([P, M, GN, MM], F32, name="cfull", tag="cfull")
+            nc.vector.tensor_tensor(
+                out=st["c"][:, h * hm : (h + 1) * hm].rearrange("p i n (j k) -> p (i n) j k", k=M),
+                in0=st["b3_%d" % g][:, h * hm : (h + 1) * hm]
+                .rearrange("p i n j -> p (i n) j")
+                .unsqueeze(3)
+                .to_broadcast([P, hm * GN, M, M]),
+                in1=st["b2_%d" % g][:, h * hm : (h + 1) * hm]
+                .rearrange("p i n k -> p (i n) k")
+                .unsqueeze(2)
+                .to_broadcast([P, hm * GN, M, M]),
+                op=ADD,
+            )
+
+        def tadd_c(g, b):
+            if b == 0:
+                st["r%d" % g] = two.tile([P, M, GN, MM], F32, name="r", tag="r", align_bytes=64)
+            r = st["r%d" % g]
+            nc.vector.tensor_tensor(
+                out=r[:, 2 * b : 2 * b + 2].rearrange("p i n q -> p (i n q)"),
+                in0=st["tb%d_%d" % (g, b)][:].rearrange("p h m -> p (h m)"),
+                in1=st["c"][:, 2 * b : 2 * b + 2].rearrange("p i n q -> p (i n q)"),
+                op=ADD,
+            )
+            for nl in range(GN):
+                queue = nc.sync if nl % 2 == 0 else nc.scalar
+                queue.dma_start(
+                    out=out[g * GN + nl, :, 2 * b : 2 * b + 2].rearrange("s i j k -> s i (j k)"),
+                    in_=r[:, 2 * b : 2 * b + 2, nl, :],
+                )
 
         def finish(g, h):
             r, b2 = st["r%d" % g], st["b2_%d" % g]
@@ -444,13 +487,20 @@ def tile_seteq3to3_kernel(tc, x, coefs, bias, out):
                 evac1(n, 1)
             if 1 <= n <= NBATCH:
                 aevac(n - 1)
-            if n < NBATCH:
+            if n < NBATCH - GN:
                 il(n)
+            elif n < NBATCH:
+                il(n, 0, M // 2)
+            elif n == NBATCH:
+                il(NBATCH - GN, M // 2, M)
             if n > GN and n % GN == 1:
                 for m in range(n - GN - 1, n - 1):
                     if m % GN == 0 or m in QSET:
                         cast(m)
                 v1(n - GN - 1)
+            if n == NBATCH + 1:
+                for m in range(NBATCH - GN + 1, NBATCH):
+                    il(m, M // 2, M)
             if 0 <= n - 2 < NBATCH:
                 vsums(n - 2)
             if n + LEAD < NBATCH and n + LEAD not in QSET:
@@ -459,16 +509,35 @@ def tile_seteq3to3_kernel(tc, x, coefs, bias, out):
                 load(n + XBUFS)
 
         def phase(g, k):
-            if k == 0:
+            last = g == NG - 1
+            if k == 0 and last:
+                quant_x(g, (0,))
+            elif k == 0:
                 quant_x(g)
             elif k == 1:
                 if g == 0:
                     quant_c()
                 quant_av(g)
+            elif k == 2 and last:
+                pe_small(g)
+                pe_bank(g, 0)
+                pe_bank(g, 1)
+                qs_evac(g)
+            elif k == 3 and last:
+                quant_x(g, (1,))
+                pe_bank(g, 2)
+                pe_bank(g, 3)
+                small(g)
+                for h in range(2):
+                    cbuild(g, h)
+                    tadd_c(g, 2 * h)
+                    tadd_c(g, 2 * h + 1)
             elif k == 2:
                 pe_small(g)
                 pe_bank(g, 0)
                 qs_evac(g)
+            elif last:
+                return
             elif k == 3:
                 small(g)
                 tadd(g, 0)
@@ -487,7 +556,7 @@ def tile_seteq3to3_kernel(tc, x, coefs, bias, out):
         for s in range(GN * NG + 11):
             if s <= NBATCH + 1:
                 slot(s)
-            for g in range(NG):
+            for g in range(NG) if s <= NBATCH else range(NG - 1, -1, -1):
                 k = s - (GN * g + GN)
                 if 0 <= k <= 6:
                     phase(g, k)

@@ -532,20 +532,20 @@ def tile_seteq3to3_kernel(tc, x, coefs, bias, out):
                     cbuild(g, h)
                     tadd_c(g, 2 * h)
                     tadd_c(g, 2 * h + 1)
-            elif k == 2:
+            elif last or k == 2:
+                return
+            elif k == 3:
                 pe_small(g)
                 pe_bank(g, 0)
                 qs_evac(g)
-            elif last:
-                return
-            elif k == 3:
+            elif k == 4:
                 small(g)
                 tadd(g, 0)
                 pe_bank(g, 1)
-            elif k == 4:
+            elif k == 5:
                 tadd(g, 1)
                 pe_bank(g, 2)
-            elif k == 5:
+            elif k == 6:
                 tadd(g, 2)
                 pe_bank(g, 3)
                 finish(g, 0)
@@ -556,7 +556,7 @@ def tile_seteq3to3_kernel(tc, x, coefs, bias, out):
         for s in range(GN * NG + 11):
             if s <= NBATCH + 1:
                 slot(s)
-            for g in range(NG) if s <= NBATCH else range(NG - 1, -1, -1):
+            for g in range(NG) if s != NBATCH + 1 else range(NG - 1, -1, -1):
                 k = s - (GN * g + GN)
-                if 0 <= k <= 6:
+                if 0 <= k <= 7:
                     phase(g, k)

@@ -31,6 +31,8 @@ COEF_CHUNKS = ((0, 8), (8, 16), (16, 18), (18, 19))
 CS = 32
 XBUFS = 8
 LEAD = 3
+CIL_GPSIMD = (0, 1)
+CIL_STEP = {0: (0, 1), 3: (2,), 4: (3,)}
 QSET = (5, 7, 9, 11, 13)
 
 
@@ -72,14 +74,12 @@ def tile_seteq3to3_kernel(tc, x, coefs, bias, out):
             )
 
         def cil(c):
-            nc.gpsimd.tensor_scalar(
-                out=cg[:, :, c * CS : (c + 1) * CS, :],
-                in0=css[c][:].rearrange("p t s b -> p b s t"),
-                scalar1=1.0,
-                scalar2=0.0,
-                op0=MULT,
-                op1=ADD,
-            )
+            dst = cg[:, :, c * CS : (c + 1) * CS, :]
+            src = css[c][:].rearrange("p t s b -> p b s t")
+            if c in CIL_GPSIMD:
+                nc.gpsimd.tensor_scalar(out=dst, in0=src, scalar1=1.0, scalar2=0.0, op0=MULT, op1=ADD)
+            else:
+                nc.vector.tensor_copy(out=dst, in_=src)
 
         vq = keep.tile([P, 3, P], U32, name="vq", tag="vq", align_bytes=64)
         vsc = keep.tile([P, 3, P], U8, name="vsc", tag="vsc", align_bytes=64)
@@ -330,9 +330,9 @@ def tile_seteq3to3_kernel(tc, x, coefs, bias, out):
         def qs_evac(g):
             pq = st["pq"]
             cols = slice(0, GN * M)
-            qs = two.tile([P, 3, GN * M], F32, name="qs", tag="qs")
-            nc.scalar.copy(out=qs[:, 0:2, :], in_=pq[:, 0:2, cols])
-            nc.scalar.activation(out=qs[:, 2, :], in_=pq[:, 2, cols], func=IDENTITY, bias=bias_f[:, 0:1], scale=1.0)
+            qs = two.tile([P, 2, GN * M], F32, name="qs", tag="qs")
+            nc.scalar.copy(out=qs[:, 1, :], in_=pq[:, 1, cols])
+            nc.scalar.activation(out=qs[:, 0, :], in_=pq[:, 0, cols], func=IDENTITY, bias=bias_f[:, 0:1], scale=1.0)
             st["qs"] = qs
 
         def pe_bank(g, b):
@@ -351,13 +351,14 @@ def tile_seteq3to3_kernel(tc, x, coefs, bias, out):
             st["tb%d_%d" % (g, b)] = tb
 
         def small(g):
-            pp, qs = st["pp"], st["qs"]
+            pp, pq, qs = st["pp"], st["pq"], st["qs"]
+            bv = two.tile([P, GN, M, M], F32, name="bv", tag="bv")
             b2 = two.tile([P, M, GN, M], F32, name="b2", tag="b2")
             b3 = two.tile([P, M, GN, M], F32, name="b3", tag="b3")
             b2v = b2[:].rearrange("p i n k -> p n i k")
             nc.vector.tensor_tensor(
-                out=b2v,
-                in0=pp[:, 0, :].rearrange("p (n i k) -> p n i k", i=M, k=M),
+                out=bv[:],
+                in0=pq[:, 2, 0 : GN * M].rearrange("p (n k) -> p n k", k=M).unsqueeze(2).to_broadcast([P, GN, M, M]),
                 in1=qs[:, 0, :].rearrange("p (n i) -> p n i", i=M).unsqueeze(3).to_broadcast([P, GN, M, M]),
                 op=ADD,
             )
@@ -369,8 +370,8 @@ def tile_seteq3to3_kernel(tc, x, coefs, bias, out):
             )
             nc.vector.tensor_tensor(
                 out=b2v,
-                in0=b2v,
-                in1=qs[:, 2, :].rearrange("p (n k) -> p n k", k=M).unsqueeze(2).to_broadcast([P, GN, M, M]),
+                in0=pp[:, 0, :].rearrange("p (n i k) -> p n i k", i=M, k=M),
+                in1=bv[:],
                 op=ADD,
             )
             st["b2_%d" % g], st["b3_%d" % g] = b2, b3
@@ -470,15 +471,15 @@ def tile_seteq3to3_kernel(tc, x, coefs, bias, out):
                 out=smatq[:, :, 1, :], in_=ident[:].rearrange("p (l j k) -> p l j k", l=2, j=M), axis=AXIS_X, op=ADD
             )
         for n in range(LEAD):
-            a2r(n)
+            if n not in QSET:
+                a2r(n)
 
         def slot(n):
             if n < NBATCH:
                 if n % GN == 0 or n in QSET:
                     g_tree(n)
-                if n == 0:
-                    for c in range(DO // CS):
-                        cil(c)
+                for c in CIL_STEP.get(n, ()):
+                    cil(c)
                 t1(n)
             if 1 <= n <= NBATCH:
                 sums(n - 1)

@@ -29,10 +29,11 @@ NG = NBATCH // GN
 GC = GN * MM
 COEF_CHUNKS = ((0, 8), (8, 16), (16, 18), (18, 19))
 CS = 32
-XBUFS = 8
-LEAD = 3
+XBUFS = 12
+LEAD = 6
 CIL_GPSIMD = (0, 1)
-CIL_STEP = {0: (0, 1), 3: (2,), 4: (3,)}
+CIL_SCALAR = (2,)
+CIL_STEP = {0: (0, 1), 2: (2,), 4: (3,)}
 QSET = (5, 7, 9, 11, 13)
 
 
@@ -78,6 +79,8 @@ def tile_seteq3to3_kernel(tc, x, coefs, bias, out):
             src = css[c][:].rearrange("p t s b -> p b s t")
             if c in CIL_GPSIMD:
                 nc.gpsimd.tensor_scalar(out=dst, in0=src, scalar1=1.0, scalar2=0.0, op0=MULT, op1=ADD)
+            elif c in CIL_SCALAR:
+                nc.scalar.copy(out=dst, in_=src)
             else:
                 nc.vector.tensor_copy(out=dst, in_=src)
 

@@ -34,6 +34,7 @@ LEAD = 6
 CIL_GPSIMD = (0, 1)
 CIL_SCALAR = (2,)
 CIL_STEP = {0: (0, 1), 2: (2,), 4: (3,)}
+HALF = (0, 4, 8)
 QSET = (5, 7, 9, 11, 13)
 
 
@@ -127,9 +128,17 @@ def tile_seteq3to3_kernel(tc, x, coefs, bias, out):
             src = xs[n]
             y1 = one.tile([P, PACK, W // 2], F32, name="y1g", tag="y1g")
             y2 = one.tile([P, PACK, W // 4], F32, name="y2g", tag="y2g")
-            a0 = gout.tile([P, PACK, MM], F32, name="a0f", tag="a0f")
             nc.gpsimd.tensor_tensor(out=y1[:], in0=src[:, :, 0 : W // 2], in1=src[:, :, W // 2 : W], op=ADD)
             nc.gpsimd.tensor_tensor(out=y2[:], in0=y1[:, :, 0 : W // 4], in1=y1[:, :, W // 4 : W // 2], op=ADD)
+            if n in QSET:
+                nc.gpsimd.tensor_tensor(
+                    out=group_tiles(n // GN)[:, 0, n % GN],
+                    in0=y2[:, :, 0:MM].rearrange("p t q -> p q t"),
+                    in1=y2[:, :, MM : 2 * MM].rearrange("p t q -> p q t"),
+                    op=ADD,
+                )
+                return
+            a0 = gout.tile([P, PACK, MM], F32, name="a0f", tag="a0f")
             nc.gpsimd.tensor_tensor(out=a0[:], in0=y2[:, :, 0:MM], in1=y2[:, :, MM : 2 * MM], op=ADD)
             a0s[n] = a0
 
@@ -181,7 +190,7 @@ def tile_seteq3to3_kernel(tc, x, coefs, bias, out):
                         )
                 pas[n] = pa
                 return
-            full = n % GN != 0
+            full = n not in HALF
             width = 32 if full else 16
             rhs = smat[:].rearrange("p l a y -> p (l a y)") if full else smat1[:].rearrange("p l y -> p (l y)")
             pa = ps_a.tile([P, 512], F32, name="pa", tag="pa")
@@ -202,7 +211,7 @@ def tile_seteq3to3_kernel(tc, x, coefs, bias, out):
                     out=ab[:, 1:3, nl].rearrange("p a (i y) t -> p a i y t", y=M),
                     in_=pa[:].rearrange("p (t i a y) -> p a i y t", t=PACK, i=M, a=2),
                 )
-            elif nl != 0:
+            elif n not in HALF:
                 nc.scalar.copy(
                     out=ab[:, 0:2, nl].rearrange("p a (y h c) t -> p a y h c t", h=2, c=4),
                     in_=pa[:].rearrange("p (t c h a y) -> p a y h c t", t=PACK, c=4, h=2, a=2),
@@ -241,7 +250,7 @@ def tile_seteq3to3_kernel(tc, x, coefs, bias, out):
                         axis=AXIS_X,
                         op=ADD,
                     )
-                elif nl != 0:
+                elif n not in HALF:
                     nc.vector.tensor_reduce(
                         out=vb[:, 1:3, nl].rearrange("p a y t -> p t a y"),
                         in_=pa[:].rearrange("p (t k a y) -> p t a y k", k=M, t=PACK, a=2),
@@ -479,7 +488,7 @@ def tile_seteq3to3_kernel(tc, x, coefs, bias, out):
 
         def slot(n):
             if n < NBATCH:
-                if n % GN == 0 or n in QSET:
+                if n in HALF or n in QSET:
                     g_tree(n)
                 for c in CIL_STEP.get(n, ()):
                     cil(c)
@@ -499,9 +508,9 @@ def tile_seteq3to3_kernel(tc, x, coefs, bias, out):
                 il(NBATCH - GN, M // 2, M)
             if n > GN and n % GN == 1:
                 for m in range(n - GN - 1, n - 1):
-                    if m % GN == 0 or m in QSET:
+                    if m in HALF:
                         cast(m)
-                v1(n - GN - 1)
+                        v1(m)
             if n == NBATCH + 1:
                 for m in range(NBATCH - GN + 1, NBATCH):
                     il(m, M // 2, M)

@@ -118,8 +118,8 @@ def tile_seteq3to3_kernel(tc, x, coefs, bias, out):
             ab = group_tiles(n // GN)
             with nc.allow_low_precision(reason=low):
                 nc.vector.tensor_reduce(
-                    out=ab[:, 2, n % GN].rearrange("p q t -> p t q"),
-                    in_=xs[n][:].rearrange("p t (q k) -> p t q k", k=M),
+                    out=ab[:, 2, n % GN],
+                    in_=xs[n][:].rearrange("p t (q k) -> p q t k", k=M),
                     axis=AXIS_X,
                     op=ADD,
                 )
@@ -228,8 +228,8 @@ def tile_seteq3to3_kernel(tc, x, coefs, bias, out):
         def v1(n):
             with nc.allow_low_precision(reason=low):
                 nc.vector.tensor_reduce(
-                    out=vb_tile(n // GN)[:, 1, n % GN].rearrange("p j t -> p t j"),
-                    in_=a0s[n][:].rearrange("p t (j k) -> p t j k", k=M),
+                    out=vb_tile(n // GN)[:, 1, n % GN],
+                    in_=a0s[n][:].rearrange("p t (j k) -> p j t k", k=M),
                     axis=AXIS_X,
                     op=ADD,
                 )
@@ -239,40 +239,40 @@ def tile_seteq3to3_kernel(tc, x, coefs, bias, out):
             with nc.allow_low_precision(reason=low):
                 if n in QSET:
                     nc.vector.tensor_reduce(
-                        out=vb[:, 0:2, nl].rearrange("p a y t -> p t a y"),
-                        in_=pa[:].rearrange("p (t i a y) -> p t a y i", t=PACK, i=M, a=2),
+                        out=vb[:, 0:2, nl],
+                        in_=pa[:].rearrange("p (t i a y) -> p a y t i", t=PACK, i=M, a=2),
                         axis=AXIS_X,
                         op=ADD,
                     )
                     nc.vector.tensor_reduce(
-                        out=vb[:, 2, nl].rearrange("p i t -> p t i"),
-                        in_=pa[:].rearrange("p (t i a y) -> p a t i y", t=PACK, i=M, a=2)[:, 0],
+                        out=vb[:, 2, nl],
+                        in_=pa[:].rearrange("p (t i a y) -> p a i t y", t=PACK, i=M, a=2)[:, 0],
                         axis=AXIS_X,
                         op=ADD,
                     )
                 elif n not in HALF:
                     nc.vector.tensor_reduce(
-                        out=vb[:, 1:3, nl].rearrange("p a y t -> p t a y"),
-                        in_=pa[:].rearrange("p (t k a y) -> p t a y k", k=M, t=PACK, a=2),
+                        out=vb[:, 1:3, nl],
+                        in_=pa[:].rearrange("p (t k a y) -> p a y t k", k=M, t=PACK, a=2),
                         axis=AXIS_X,
                         op=ADD,
                     )
                     nc.vector.tensor_reduce(
-                        out=vb[:, 0, nl].rearrange("p (h c) t -> p t c h", h=2),
-                        in_=pa[:].rearrange("p (t c h a y) -> p a t c h y", t=PACK, c=4, h=2, a=2)[:, 0],
+                        out=vb[:, 0, nl].rearrange("p (h c) t -> p h c t", h=2),
+                        in_=pa[:].rearrange("p (t c h a y) -> p a h c t y", t=PACK, c=4, h=2, a=2)[:, 0],
                         axis=AXIS_X,
                         op=ADD,
                     )
                 else:
                     nc.vector.tensor_reduce(
-                        out=vb[:, 2, nl].rearrange("p y t -> p t y"),
-                        in_=pa[:, 0:256].rearrange("p (t k y) -> p t y k", k=M, t=PACK),
+                        out=vb[:, 2, nl],
+                        in_=pa[:, 0:256].rearrange("p (t k y) -> p y t k", k=M, t=PACK),
                         axis=AXIS_X,
                         op=ADD,
                     )
                     nc.vector.tensor_reduce(
-                        out=vb[:, 0, nl].rearrange("p (h c) t -> p t c h", h=2),
-                        in_=pa[:, 0:256].rearrange("p (t c h y) -> p t c h y", t=PACK, c=4, h=2),
+                        out=vb[:, 0, nl].rearrange("p (h c) t -> p h c t", h=2),
+                        in_=pa[:, 0:256].rearrange("p (t c h y) -> p h c t y", t=PACK, c=4, h=2),
                         axis=AXIS_X,
                         op=ADD,
                     )

@@ -282,7 +282,8 @@ def tile_seteq3to3_kernel(tc, x, coefs, bias, out):
             if g not in xgs:
                 xgs[g] = two.tile([P, M, GN, MM, PACK], BF16, name="xg", tag="xg", align_bytes=64)
             nc.scalar.copy(
-                out=xgs[g][:, i0:i1, n % GN], in_=xs[n][:].rearrange("p t (i q) -> p i q t", i=M)[:, i0:i1]
+                out=xgs[g][:, i0:i1, n % GN].rearrange("p i (c u) t -> p i c t u", u=4),
+                in_=xs[n][:].rearrange("p t (i c u) -> p i c t u", i=M, u=4)[:, i0:i1],
             )
 
         def quant_c():

@@ -35,7 +35,7 @@ CIL_GPSIMD = (0, 1)
 CIL_SCALAR = (2,)
 CIL_STEP = {0: (0, 1), 2: (2,), 4: (3,)}
 HALF = (0, 4, 8)
-QSET = (5, 7, 9, 11, 13)
+QSET = (5, 7, 9, 11)
 
 
 def tile_seteq3to3_kernel(tc, x, coefs, bias, out):

from contextlib import ExitStack

import concourse.mybir as mybir
from concourse.masks import make_identity

FLOPS = 2 * 512 * 128 * (16 * 512 + 9 * 16 * 64 + 9 * 16 * 8)

BF16 = mybir.dt.bfloat16
F32 = mybir.dt.float32
I32 = mybir.dt.int32
U32 = mybir.dt.uint32
U8 = mybir.dt.uint8
FP8X4 = mybir.dt.float8_e4m3fn_x4
ADD = mybir.AluOpType.add
MULT = mybir.AluOpType.mult
AXIS_X = mybir.AxisListType.X
IDENTITY = mybir.ActivationFunctionType.Identity

P = 128
PACK = 4
NBATCH = 16
M = 8
MM = M * M
W = M * M * M
DO = 128
NB = 19
GN = 4
NG = NBATCH // GN
GC = GN * MM
COEF_CHUNKS = ((0, 8), (8, 16), (16, 18), (18, 19))
CS = 32
XBUFS = 12
LEAD = 6
CIL_GPSIMD = (0, 1)
CIL_SCALAR = (2,)
CIL_STEP = {0: (0, 1), 2: (2,), 4: (3,)}
HALF = (0, 4, 8)
QSET = (5, 7, 9, 11)


def tile_seteq3to3_kernel(tc, x, coefs, bias, out):
    nc = tc.nc
    with ExitStack() as ctx:
        keep = ctx.enter_context(tc.tile_pool(name="keep", bufs=1))
        one = ctx.enter_context(tc.tile_pool(name="one", bufs=1))
        two = ctx.enter_context(tc.tile_pool(name="two", bufs=2))
        three = ctx.enter_context(tc.tile_pool(name="three", bufs=3))
        xin = ctx.enter_context(tc.tile_pool(name="xin", bufs=XBUFS))
        gout = ctx.enter_context(tc.tile_pool(name="gout", bufs=6))
        ps_1 = ctx.enter_context(tc.psum_pool(name="ps_1", bufs=2))
        ps_a = ctx.enter_context(tc.psum_pool(name="ps_a", bufs=2))
        ps_s = ctx.enter_context(tc.psum_pool(name="ps_s", bufs=1))
        ps_t = ctx.enter_context(tc.psum_pool(name="ps_t", bufs=2))
        low = "float32 sum, rounded once to bfloat16 on the way out"

        ident = keep.tile([P, P], F32, name="ident", tag="ident")
        make_identity(nc, ident[:])
        ident_b = keep.tile([P, P], BF16, name="ident_b", tag="ident_b")
        make_identity(nc, ident_b[:])
        ctx.enter_context(tc.manual_schedule())

        xs, xts, pts, pas, xgs, abs_, vbs, a0s, st = {}, {}, {}, {}, {}, {}, {}, {}, {}

        def load(n):
            xs[n] = xin.tile([P, PACK, W], BF16, name="xs", tag="xs", align_bytes=64)
            nc.sync.dma_start(out=xs[n][:], in_=x[n].rearrange("(p t) i j k -> p t (i j k)", t=PACK))

        css = [keep.tile([P, PACK, CS, NB], BF16, name="cs%d" % c, tag="cs%d" % c) for c in range(DO // CS)]
        cg = keep.tile([P, NB, DO, PACK], BF16, name="cg", tag="cg", align_bytes=64)
        bias_bf = keep.tile([P, 1], BF16, name="bias_bf", tag="bias_bf")
        bias_f = keep.tile([P, 1], F32, name="bias_f", tag="bias_f")

        def cload(c):
            nc.sync.dma_start(
                out=css[c][:], in_=coefs.rearrange("(p t) s b -> p t s b", t=PACK)[:, :, c * CS : (c + 1) * CS, :]
            )

        def cil(c):
            dst = cg[:, :, c * CS : (c + 1) * CS, :]
            src = css[c][:].rearrange("p t s b -> p b s t")
            if c in CIL_GPSIMD:
                nc.gpsimd.tensor_scalar(out=dst, in0=src, scalar1=1.0, scalar2=0.0, op0=MULT, op1=ADD)
            elif c in CIL_SCALAR:
                nc.scalar.copy(out=dst, in_=src)
            else:
                nc.vector.tensor_copy(out=dst, in_=src)

        vq = keep.tile([P, 3, P], U32, name="vq", tag="vq", align_bytes=64)
        vsc = keep.tile([P, 3, P], U8, name="vsc", tag="vsc", align_bytes=64)
        cq = keep.tile([P, NB, DO], U32, name="cq", tag="cq", align_bytes=64)
        csc = keep.tile([P, NB, DO], U8, name="csc", tag="csc", align_bytes=64)
        smat = keep.tile([P, 2, 2, M], BF16, name="smat", tag="smat")
        smat1 = keep.tile([P, 2, M], BF16, name="smat1", tag="smat1")
        smatq = keep.tile([P, 2, 2, M], BF16, name="smatq", tag="smatq")

        def group_tiles(g):
            if g not in abs_:
                abs_[g] = three.tile([P, 3, GN, MM, PACK], BF16, name="ab", tag="ab", align_bytes=64)
            return abs_[g]

        def vb_tile(g):
            if g not in vbs:
                vbs[g] = two.tile([P, 3, GN, M, PACK], BF16, name="vb", tag="vb", align_bytes=64)
            return vbs[g]

        def mx(acc, b, rhs, rhs_scale, start, stop):
            nc.tensor.matmul_mx(
                out=acc,
                lhsT=cq[:, b, :].bitcast(FP8X4),
                lhsT_scale=csc[:, b, :],
                rhs=rhs.bitcast(FP8X4),
                rhs_scale=rhs_scale,
                start=start,
                stop=stop,
            )

        def a2r(n):
            ab = group_tiles(n // GN)
            with nc.allow_low_precision(reason=low):
                nc.vector.tensor_reduce(
                    out=ab[:, 2, n % GN],
                    in_=xs[n][:].rearrange("p t (q k) -> p q t k", k=M),
                    axis=AXIS_X,
                    op=ADD,
                )

        def g_tree(n):
            src = xs[n]
            y1 = one.tile([P, PACK, W // 2], F32, name="y1g", tag="y1g")
            y2 = one.tile([P, PACK, W // 4], F32, name="y2g", tag="y2g")
            nc.gpsimd.tensor_tensor(out=y1[:], in0=src[:, :, 0 : W // 2], in1=src[:, :, W // 2 : W], op=ADD)
            nc.gpsimd.tensor_tensor(out=y2[:], in0=y1[:, :, 0 : W // 4], in1=y1[:, :, W // 4 : W // 2], op=ADD)
            if n in QSET:
                nc.gpsimd.tensor_tensor(
                    out=group_tiles(n // GN)[:, 0, n % GN],
                    in0=y2[:, :, 0:MM].rearrange("p t q -> p q t"),
                    in1=y2[:, :, MM : 2 * MM].rearrange("p t q -> p q t"),
                    op=ADD,
                )
                return
            a0 = gout.tile([P, PACK, MM], F32, name="a0f", tag="a0f")
            nc.gpsimd.tensor_tensor(out=a0[:], in0=y2[:, :, 0:MM], in1=y2[:, :, MM : 2 * MM], op=ADD)
            a0s[n] = a0

        def t1(n):
            if n in QSET:
                xts[n] = three.tile([P, PACK, 4, P], BF16, name="xt", tag="xt", align_bytes=64)
                for th in range(2):
                    pt = ps_1.tile([P, 2, 4, P], BF16, name="pt", tag="pt")
                    for tl in range(2):
                        for wb in range(4):
                            nc.tensor.transpose(
                                pt[:, tl, wb, :], xs[n][:, 2 * th + tl, wb * P : (wb + 1) * P], ident_b[:]
                            )
                    pts[(n, th)] = pt
                return
            words = xs[n][:].rearrange("p t w -> p (t w)").bitcast(F32)
            xts[n] = three.tile([P, 2, 4, P, 2], BF16, name="xt", tag="xt", align_bytes=64)
            for th in range(2):
                pt = ps_1.tile([P, 4, P], F32, name="pt", tag="pt")
                for b in range(4):
                    t, kl = 2 * th + b // 2, b % 2
                    nc.tensor.transpose(pt[:, b, :], words[:, t * 256 + kl : (t + 1) * 256 : 2], ident[:])
                pts[(n, th)] = pt

        def evac1(n, th):
            if n in QSET:
                nc.scalar.copy(
                    out=xts[n][:, 2 * th : 2 * th + 2].rearrange("p t w m -> p (t w m)").bitcast(F32),
                    in_=pts[(n, th)][:].rearrange("p t w m -> p (t w m)").bitcast(F32),
                )
                return
            nc.scalar.copy(
                out=xts[n][:, th].rearrange("p k m e -> p (k m e)").bitcast(F32),
                in_=pts[(n, th)][:].rearrange("p k m -> p (k m)"),
            )

        def sums(n):
            if n in QSET:
                pa = ps_a.tile([P, 512], F32, name="pa", tag="pa")
                for t in range(PACK):
                    for wb in range(4):
                        col = (t * 4 + wb) * 32
                        nc.tensor.matmul(
                            out=pa[:, col : col + 32],
                            lhsT=xts[n][:, t, wb, :],
                            rhs=smatq[:].rearrange("p l a y -> p (l a y)"),
                            start=True,
                            stop=True,
                        )
                pas[n] = pa
                return
            full = n not in HALF
            width = 32 if full else 16
            rhs = smat[:].rearrange("p l a y -> p (l a y)") if full else smat1[:].rearrange("p l y -> p (l y)")
            pa = ps_a.tile([P, 512], F32, name="pa", tag="pa")
            for th in range(2):
                for b in range(4):
                    for e in range(2):
                        t, kl = 2 * th + b // 2, b % 2
                        col = (t * 4 + kl * 2 + e) * width
                        nc.tensor.matmul(
                            out=pa[:, col : col + width], lhsT=xts[n][:, th, b, :, e], rhs=rhs, start=True, stop=True
                        )
            pas[n] = pa

        def aevac(n):
            ab, nl, pa = group_tiles(n // GN), n % GN, pas[n]
            if n in QSET:
                nc.scalar.copy(
                    out=ab[:, 1:3, nl].rearrange("p a (i y) t -> p a i y t", y=M),
                    in_=pa[:].rearrange("p (t i a y) -> p a i y t", t=PACK, i=M, a=2),
                )
            elif n not in HALF:
                nc.scalar.copy(
                    out=ab[:, 0:2, nl].rearrange("p a (y h c) t -> p a y h c t", h=2, c=4),
                    in_=pa[:].rearrange("p (t c h a y) -> p a y h c t", t=PACK, c=4, h=2, a=2),
                )
            else:
                nc.scalar.copy(
                    out=ab[:, 1, nl].rearrange("p (y h c) t -> p y h c t", h=2, c=4),
                    in_=pa[:, 0:256].rearrange("p (t c h y) -> p y h c t", t=PACK, c=4, h=2),
                )

        def cast(n):
            nc.scalar.copy(out=group_tiles(n // GN)[:, 0, n % GN], in_=a0s[n][:].rearrange("p t q -> p q t"))

        def v1(n):
            with nc.allow_low_precision(reason=low):
                nc.vector.tensor_reduce(
                    out=vb_tile(n // GN)[:, 1, n % GN],
                    in_=a0s[n][:].rearrange("p t (j k) -> p j t k", k=M),
                    axis=AXIS_X,
                    op=ADD,
                )

        def vsums(n):
            vb, nl, pa = vb_tile(n // GN), n % GN, pas[n]
            with nc.allow_low_precision(reason=low):
                if n in QSET:
                    nc.vector.tensor_reduce(
                        out=vb[:, 0:2, nl],
                        in_=pa[:].rearrange("p (t i a y) -> p a y t i", t=PACK, i=M, a=2),
                        axis=AXIS_X,
                        op=ADD,
                    )
                    nc.vector.tensor_reduce(
                        out=vb[:, 2, nl],
                        in_=pa[:].rearrange("p (t i a y) -> p a i t y", t=PACK, i=M, a=2)[:, 0],
                        axis=AXIS_X,
                        op=ADD,
                    )
                elif n not in HALF:
                    nc.vector.tensor_reduce(
                        out=vb[:, 1:3, nl],
                        in_=pa[:].rearrange("p (t k a y) -> p a y t k", k=M, t=PACK, a=2),
                        axis=AXIS_X,
                        op=ADD,
                    )
                    nc.vector.tensor_reduce(
                        out=vb[:, 0, nl].rearrange("p (h c) t -> p h c t", h=2),
                        in_=pa[:].rearrange("p (t c h a y) -> p a h c t y", t=PACK, c=4, h=2, a=2)[:, 0],
                        axis=AXIS_X,
                        op=ADD,
                    )
                else:
                    nc.vector.tensor_reduce(
                        out=vb[:, 2, nl],
                        in_=pa[:, 0:256].rearrange("p (t k y) -> p y t k", k=M, t=PACK),
                        axis=AXIS_X,
                        op=ADD,
                    )
                    nc.vector.tensor_reduce(
                        out=vb[:, 0, nl].rearrange("p (h c) t -> p h c t", h=2),
                        in_=pa[:, 0:256].rearrange("p (t c h y) -> p h c t y", t=PACK, c=4, h=2),
                        axis=AXIS_X,
                        op=ADD,
                    )

        def il(n, i0=0, i1=M):
            g = n // GN
            if g not in xgs:
                xgs[g] = two.tile([P, M, GN, MM, PACK], BF16, name="xg", tag="xg", align_bytes=64)
            nc.scalar.copy(
                out=xgs[g][:, i0:i1, n % GN].rearrange("p i (c u) t -> p i c t u", u=4),
                in_=xs[n][:].rearrange("p t (i c u) -> p i c t u", i=M, u=4)[:, i0:i1],
            )

        def quant_c():
            nc.vector.tensor_copy(out=bias_f[:], in_=bias_bf[:])
            for b0, b1 in COEF_CHUNKS:
                nc.vector.quantize_mx(
                    out=cq[:, b0:b1].rearrange("p b s -> p (b s)").bitcast(FP8X4),
                    scales=csc[:, b0:b1].rearrange("p b s -> p (b s)"),
                    in_=cg[:, b0:b1].rearrange("p b s t -> p (b s t)"),
                )

        def quant_x(g, halves=(0, 1)):
            xg = xgs[g]
            if halves[0] == 0:
                xq = two.tile([P, M, GC], U32, name="xq", tag="xq", align_bytes=64)
                xsc = two.tile([P, M, GC], U8, name="xsc", tag="xsc", align_bytes=64)
                st["xq%d" % g] = (xq, xsc)
            xq, xsc = st["xq%d" % g]
            hm = M // 2
            for b in halves:
                nc.vector.quantize_mx(
                    out=xq[:, hm * b : hm * (b + 1)].rearrange("p i c -> p (i c)").bitcast(FP8X4),
                    scales=xsc[:, hm * b : hm * (b + 1)].rearrange("p i c -> p (i c)"),
                    in_=xg[:, hm * b : hm * (b + 1)].rearrange("p i n q t -> p (i n q t)"),
                )

        def quant_av(g):
            ab, vb = abs_[g], vbs[g]
            aq = two.tile([P, 3, GC], U32, name="aq", tag="aq", align_bytes=64)
            asc = two.tile([P, 3, GC], U8, name="asc", tag="asc", align_bytes=64)
            for a in range(3):
                nc.vector.quantize_mx(
                    out=aq[:, a].bitcast(FP8X4),
                    scales=asc[:, a],
                    in_=ab[:, a].rearrange("p n q t -> p (n q t)"),
                )
            for a in range(3):
                nc.vector.quantize_mx(
                    out=vq[:, a, 0 : GN * M].bitcast(FP8X4),
                    scales=vsc[:, a, 0 : GN * M],
                    in_=vb[:, a].rearrange("p n m t -> p (n m t)"),
                )
            st["aq%d" % g] = (aq, asc)

        def pe_small(g):
            aq, asc = st["aq%d" % g]
            pp = ps_s.tile([P, 2, GC], F32, name="pp", tag="pp")
            for t in range(2):
                for a in range(3):
                    mx(pp[:, t, :], 2 + 3 * a + t, aq[:, a], asc[:, a], a == 0, a == 2)
            pq = ps_s.tile([P, 3, P], F32, name="pq", tag="pq")
            for t in range(3):
                for a in range(3):
                    mx(pq[:, t, :], 10 + 3 * a + t, vq[:, a], vsc[:, a], a == 0, a == 2)
            st["pp"], st["pq"] = pp, pq

        def qs_evac(g):
            pq = st["pq"]
            cols = slice(0, GN * M)
            qs = two.tile([P, 2, GN * M], F32, name="qs", tag="qs")
            nc.scalar.copy(out=qs[:, 1, :], in_=pq[:, 1, cols])
            nc.scalar.activation(out=qs[:, 0, :], in_=pq[:, 0, cols], func=IDENTITY, bias=bias_f[:, 0:1], scale=1.0)
            st["qs"] = qs

        def pe_bank(g, b):
            xq, xsc = st["xq%d" % g]
            aq, asc = st["aq%d" % g]
            if g < NG - 1:
                tb = ps_t.tile([P, 2, GC], F32, name="tb", tag="tb")
            elif b < 2:
                tb = ps_a.tile([P, 2, GC], F32, name="pa", tag="pa")
            else:
                tb = ps_1.tile([P, 2, GC], F32, name="pt", tag="pt")
            for h in range(2):
                mx(tb[:, h, :], 0, xq[:, 2 * b + h], xsc[:, 2 * b + h], True, False)
                for a in range(3):
                    mx(tb[:, h, :], 1 + 3 * a, aq[:, a], asc[:, a], False, a == 2)
            st["tb%d_%d" % (g, b)] = tb

        def small(g):
            pp, pq, qs = st["pp"], st["pq"], st["qs"]
            bv = two.tile([P, GN, M, M], F32, name="bv", tag="bv")
            b2 = two.tile([P, M, GN, M], F32, name="b2", tag="b2")
            b3 = two.tile([P, M, GN, M], F32, name="b3", tag="b3")
            b2v = b2[:].rearrange("p i n k -> p n i k")
            nc.vector.tensor_tensor(
                out=bv[:],
                in0=pq[:, 2, 0 : GN * M].rearrange("p (n k) -> p n k", k=M).unsqueeze(2).to_broadcast([P, GN, M, M]),
                in1=qs[:, 0, :].rearrange("p (n i) -> p n i", i=M).unsqueeze(3).to_broadcast([P, GN, M, M]),
                op=ADD,
            )
            nc.vector.tensor_tensor(
                out=b3[:].rearrange("p i n j -> p n i j"),
                in0=pp[:, 1, :].rearrange("p (n i j) -> p n i j", i=M, j=M),
                in1=qs[:, 1, :].rearrange("p (n j) -> p n j", j=M).unsqueeze(2).to_broadcast([P, GN, M, M]),
                op=ADD,
            )
            nc.vector.tensor_tensor(
                out=b2v,
                in0=pp[:, 0, :].rearrange("p (n i k) -> p n i k", i=M, k=M),
                in1=bv[:],
                op=ADD,
            )
            st["b2_%d" % g], st["b3_%d" % g] = b2, b3

        def tadd(g, b):
            if b == 0:
                st["r%d" % g] = two.tile([P, M, GN, MM], F32, name="r", tag="r", align_bytes=64)
            nc.vector.tensor_tensor(
                out=st["r%d" % g][:, 2 * b : 2 * b + 2].rearrange("p i n (j k) -> p (i n j) k", k=M),
                in0=st["tb%d_%d" % (g, b)][:].rearrange("p h (m k) -> p (h m) k", k=M),
                in1=st["b3_%d" % g][:, 2 * b : 2 * b + 2]
                .rearrange("p i n j -> p (i n j)")
                .unsqueeze(2)
                .to_broadcast([P, 2 * GN * M, M]),
                op=ADD,
            )

        def cbuild(g, h):
            hm = M // 2
            if h == 0:
                st["c"] = one.tile([P, M, GN, MM], F32, name="cfull", tag="cfull")
            nc.vector.tensor_tensor(
                out=st["c"][:, h * hm : (h + 1) * hm].rearrange("p i n (j k) -> p (i n) j k", k=M),
                in0=st["b3_%d" % g][:, h * hm : (h + 1) * hm]
                .rearrange("p i n j -> p (i n) j")
                .unsqueeze(3)
                .to_broadcast([P, hm * GN, M, M]),
                in1=st["b2_%d" % g][:, h * hm : (h + 1) * hm]
                .rearrange("p i n k -> p (i n) k")
                .unsqueeze(2)
                .to_broadcast([P, hm * GN, M, M]),
                op=ADD,
            )

        def tadd_c(g, b):
            if b == 0:
                st["r%d" % g] = two.tile([P, M, GN, MM], F32, name="r", tag="r", align_bytes=64)
            r = st["r%d" % g]
            nc.vector.tensor_tensor(
                out=r[:, 2 * b : 2 * b + 2].rearrange("p i n q -> p (i n q)"),
                in0=st["tb%d_%d" % (g, b)][:].rearrange("p h m -> p (h m)"),
                in1=st["c"][:, 2 * b : 2 * b + 2].rearrange("p i n q -> p (i n q)"),
                op=ADD,
            )
            for nl in range(GN):
                queue = nc.sync if nl % 2 == 0 else nc.scalar
                queue.dma_start(
                    out=out[g * GN + nl, :, 2 * b : 2 * b + 2].rearrange("s i j k -> s i (j k)"),
                    in_=r[:, 2 * b : 2 * b + 2, nl, :],
                )

        def finish(g, h):
            r, b2 = st["r%d" % g], st["b2_%d" % g]
            hm = M // 2
            rv = r[:, h * hm : (h + 1) * hm].rearrange("p i n (j k) -> p (i n) j k", k=M)
            nc.vector.tensor_tensor(
                out=rv,
                in0=rv,
                in1=b2[:, h * hm : (h + 1) * hm]
                .rearrange("p i n k -> p (i n) k")
                .unsqueeze(2)
                .to_broadcast([P, hm * GN, M, M]),
                op=ADD,
            )
            for nl in range(GN):
                nc.sync.dma_start(
                    out=out[g * GN + nl, :, h * hm : (h + 1) * hm].rearrange("s i j k -> s i (j k)"),
                    in_=r[:, h * hm : (h + 1) * hm, nl, :],
                )

        load(0)
        load(1)
        for c in range(DO // CS):
            cload(c)
            load(2 + c)
        with nc.allow_non_contiguous_dma(reason="128 bias values, one to a partition"):
            nc.sync.dma_start(out=bias_bf[:], in_=bias.rearrange("a s b c d -> s (a b c d)"))
        for n in range(6, XBUFS):
            load(n)

        nc.vector.memset(vq[:].bitcast(I32), 0)
        nc.vector.memset(vsc[:].bitcast(I32), 0)
        with nc.allow_low_precision(reason="sums of zeros and a one"):
            nc.vector.tensor_reduce(
                out=smat[:, :, 0, :], in_=ident[:].rearrange("p (i j h) -> p h j i", i=M, j=M), axis=AXIS_X, op=ADD
            )
            nc.vector.tensor_reduce(
                out=smat[:, :, 1, :], in_=ident[:].rearrange("p (i j h) -> p h i j", i=M, j=M), axis=AXIS_X, op=ADD
            )
            nc.vector.tensor_reduce(
                out=smat1[:], in_=ident[:].rearrange("p (i j h) -> p h i j", i=M, j=M), axis=AXIS_X, op=ADD
            )
            nc.vector.tensor_reduce(
                out=smatq[:, :, 0, :], in_=ident[:].rearrange("p (l j k) -> p l k j", l=2, j=M), axis=AXIS_X, op=ADD
            )
            nc.vector.tensor_reduce(
                out=smatq[:, :, 1, :], in_=ident[:].rearrange("p (l j k) -> p l j k", l=2, j=M), axis=AXIS_X, op=ADD
            )
        for n in range(LEAD):
            if n not in QSET:
                a2r(n)

        def slot(n):
            if n < NBATCH:
                if n in HALF or n in QSET:
                    g_tree(n)
                for c in CIL_STEP.get(n, ()):
                    cil(c)
                t1(n)
            if 1 <= n <= NBATCH:
                sums(n - 1)
            if n < NBATCH:
                evac1(n, 0)
                evac1(n, 1)
            if 1 <= n <= NBATCH:
                aevac(n - 1)
            if n < NBATCH - GN:
                il(n)
            elif n < NBATCH:
                il(n, 0, M // 2)
            elif n == NBATCH:
                il(NBATCH - GN, M // 2, M)
            if n > GN and n % GN == 1:
                for m in range(n - GN - 1, n - 1):
                    if m in HALF:
                        cast(m)
                        v1(m)
            if n == NBATCH + 1:
                for m in range(NBATCH - GN + 1, NBATCH):
                    il(m, M // 2, M)
            if 0 <= n - 2 < NBATCH:
                vsums(n - 2)
            if n + LEAD < NBATCH and n + LEAD not in QSET:
                a2r(n + LEAD)
            if n + XBUFS < NBATCH:
                load(n + XBUFS)

        def phase(g, k):
            last = g == NG - 1
            if k == 0 and last:
                quant_x(g, (0,))
            elif k == 0:
                quant_x(g)
            elif k == 1:
                if g == 0:
                    quant_c()
                quant_av(g)
            elif k == 2 and last:
                pe_small(g)
                pe_bank(g, 0)
                pe_bank(g, 1)
                qs_evac(g)
            elif k == 3 and last:
                quant_x(g, (1,))
                pe_bank(g, 2)
                pe_bank(g, 3)
                small(g)
                for h in range(2):
                    cbuild(g, h)
                    tadd_c(g, 2 * h)
                    tadd_c(g, 2 * h + 1)
            elif last or k == 2:
                return
            elif k == 3:
                pe_small(g)
                pe_bank(g, 0)
                qs_evac(g)
            elif k == 4:
                small(g)
                tadd(g, 0)
                pe_bank(g, 1)
            elif k == 5:
                tadd(g, 1)
                pe_bank(g, 2)
            elif k == 6:
                tadd(g, 2)
                pe_bank(g, 3)
                finish(g, 0)
            else:
                tadd(g, 3)
                finish(g, 1)

        for s in range(GN * NG + 11):
            if s <= NBATCH + 1:
                slot(s)
            for g in range(NG) if s != NBATCH + 1 else range(NG - 1, -1, -1):
                k = s - (GN * g + GN)
                if 0 <= k <= 7:
                    phase(g, k)
